import numpy as np
import ml_dtypes


def mxq(x, axis, fmt="e4m3"):
    dtype, down = {"e4m3": (ml_dtypes.float8_e4m3fn, 7), "e5m2": (ml_dtypes.float8_e5m2, 14)}[fmt]
    v = np.moveaxis(np.asarray(x, np.float32).astype(ml_dtypes.bfloat16).astype(np.float64), axis, -1)
    blocks = v.reshape(v.shape[:-1] + (-1, 32))
    amax = np.abs(blocks).max(-1, keepdims=True)
    byte = np.maximum(np.where(amax > 0, np.frexp(amax)[1] - 1 + 127, 0) - down, 1)
    scale = np.exp2(byte - 127.0)
    codes = (blocks / scale).astype(np.float32).astype(dtype).astype(np.float64)
    return np.moveaxis((codes * scale).reshape(v.shape), -1, axis)


WIDE = False


def mx_kscale(k):
    if not WIDE:
        return np.ones(k)
    levels = np.array([10, -10, 5, -5, 0])
    a = np.random.permutation(np.resize(levels, k // 512 * 4)).reshape(k // 512, 4)
    idx = np.arange(k)
    return np.exp2(a[idx // 512, idx % 128 // 32])


BF16 = ml_dtypes.bfloat16


def bf(x):
    return np.asarray(x, np.float32).astype(BF16)


def f64(x):
    return np.asarray(x).astype(np.float64)


B, P, C, HS, NG = 2, 512, 768, 512, 8
GMIN, GMAX = -1.0, 1.0
SKIP = 1.0


def silu(v):
    return v / (1.0 + np.exp(-v))


def rbf(v):
    grid = np.linspace(GMIN, GMAX, NG)
    denom = (GMAX - GMIN) / (NG - 1)
    return np.exp(-np.square((v[..., None] - grid) / denom))


def setup_inputs():
    s = mx_kscale(HS * NG)[::NG]
    u = s / s.max()
    r = np.sqrt(np.log(1.0 / u))
    d = (GMAX - GMIN) / (NG - 1)
    m = (GMAX + d * r) * (r > 0)
    return {"h_mix": bf(np.random.standard_normal((B, C, HS)) * 0.9 * (d / (d + 2.0 * r)) + m),
            "x": bf(np.random.standard_normal((B, P, C))),
            "fc2_spline_w": bf(np.random.standard_normal((P, HS * NG)) * 0.7 / np.sqrt(HS) / np.repeat(u, NG)),
            "fc2_base_w": bf(np.random.standard_normal((P, HS)) / np.sqrt(HS) / (1.0 + m)),
            "fc2_base_b": bf(np.random.standard_normal(P) * 0.1)}


def reference(h_mix, x, fc2_spline_w, fc2_base_w, fc2_base_b):
    h = f64(h_mix)
    basis = rbf(h).reshape(B, C, HS * NG)
    out = mxq(basis, 2, "e4m3") @ mxq(f64(fc2_spline_w).T, 0, "e4m3")
    out = out + (mxq(silu(h), 2, "e4m3") @ mxq(f64(fc2_base_w).T, 0, "e4m3")) + f64(fc2_base_b)
    return np.swapaxes(out, 1, 2) + SKIP * f64(x)

@@ -1,0 +1,239 @@
+from contextlib import ExitStack
+
+import concourse.mybir as mybir
+from concourse.masks import make_identity
+
+F32 = mybir.dt.float32
+BF16 = mybir.dt.bfloat16
+U32 = mybir.dt.uint32
+U8 = mybir.dt.uint8
+FP8X4 = mybir.dt.float8_e4m3fn_x4
+ACT = mybir.ActivationFunctionType
+ALU = mybir.AluOpType
+
+P = 128
+BATCH, CHANNELS, HIDDEN, ROWS, CENTRES = 2, 768, 512, 512, 8
+COLS = BATCH * CHANNELS
+CHUNK = 512
+CHUNKS = COLS // CHUNK
+HALF = CHUNK // 2
+ROW_TILES = ROWS // P
+SPACING = 2.0 / (CENTRES - 1)
+PAIRS = CENTRES // 2
+HALVES = 2
+SPLINE_PASSES = HALVES * PAIRS
+BASE_PASS = SPLINE_PASSES
+PASSES = SPLINE_PASSES + 1
+SCALAR_SQUARES_EVERY = 3
+
+FLOPS = 2 * COLS * ROWS * (HIDDEN * CENTRES + HIDDEN)
+
+
+def class_order(words, groups):
+    return words.rearrange("r (g a c x) -> r g c a x", g=groups, a=16, c=4, x=2)
+
+
+def partition_order(words, groups):
+    return words.rearrange("r (g c a x) -> r g c a x", g=groups, c=4, a=16, x=2)
+
+
+def tile_kan1_pb_kernel(tc, h_mix, x, fc2_spline_w, fc2_base_w, fc2_base_b, out):
+    nc = tc.nc
+    with ExitStack() as stack:
+        keep = stack.enter_context(tc.tile_pool(name="keep", bufs=1))
+        stage = stack.enter_context(tc.tile_pool(name="stage", bufs=2))
+        ring = stack.enter_context(tc.tile_pool(name="ring", bufs=3))
+        turned = stack.enter_context(tc.psum_pool(name="turned", bufs=4))
+        sums = stack.enter_context(tc.psum_pool(name="sums", bufs=1))
+
+        h_rows = h_mix.flatten_outer_dims()
+        h_nat = []
+        for ch in range(CHUNKS):
+            h_tile = keep.tile([P, 4 * HIDDEN], BF16, name="h_nat%d" % ch)
+            nc.sync.dma_start(
+                out=h_tile[:].rearrange("r (t j) -> r t j", t=4),
+                in_=h_rows[ch * CHUNK : (ch + 1) * CHUNK, :].rearrange("(t r) j -> r t j", r=P),
+            )
+            h_nat.append(h_tile)
+        bw_nat = keep.tile([P, ROW_TILES * HIDDEN], BF16)
+        nc.sync.dma_start(
+            out=bw_nat[:].rearrange("q (m j) -> q m j", m=ROW_TILES),
+            in_=fc2_base_w.rearrange("(m q) j -> q m j", q=P),
+        )
+        w_nat = []
+        for m in range(ROW_TILES):
+            w_tile = ring.tile([P, HIDDEN * CENTRES], BF16, name="w_nat", bufs=ROW_TILES)
+            nc.sync.dma_start(out=w_tile[:], in_=fc2_spline_w[m * P : (m + 1) * P, :])
+            w_nat.append(w_tile)
+        bias_rows = keep.tile([P, P], BF16)
+        nc.vector.memset(bias_rows[:], 0.0)
+        nc.sync.dma_start(out=bias_rows[0:ROW_TILES, :], in_=fc2_base_b.rearrange("(m q) -> m q", q=P))
+        x_sb = keep.tile([P, ROW_TILES * COLS], BF16)
+        for m in range(ROW_TILES):
+            nc.sync.dma_start(
+                out=x_sb[:, m * COLS : (m + 1) * COLS].rearrange("q (b c) -> q b c", b=BATCH),
+                in_=x[:, m * P : (m + 1) * P, :].rearrange("b q c -> q b c"),
+            )
+
+        ident_f32 = keep.tile([P, P], F32)
+        make_identity(nc, ident_f32[:])
+        ident_bf16 = keep.tile([P, P], BF16)
+        make_identity(nc, ident_bf16[:])
+
+        silu_codes = keep.tile([P, COLS], U32, align_bytes=64)
+        silu_scales = keep.tile([P, COLS], U8, align_bytes=64)
+        shifted = []
+        for ch in range(CHUNKS):
+            h_perm = stage.tile([P, 8 * P], F32, tag="perm")
+            nc.vector.tensor_copy(out=partition_order(h_perm[:], 8), in_=class_order(h_nat[ch][:].bitcast(F32), 8))
+            shifted_tile = keep.tile([P, 2 * HALVES * 2 * CHUNK], F32, name="shifted%d" % ch)
+            shifted_view = shifted_tile[:].rearrange("p (e h x) -> p e h x", e=2, h=HALVES)
+            silu_grouped = stage.tile([P, 4 * CHUNK], BF16, align_bytes=64, tag="grouped")
+            for hf in range(2):
+                h_turned = turned.tile([P, CHUNK], F32, tag="turned")
+                for half in range(HALVES):
+                    for t2 in range(2):
+                        g = 2 * (2 * hf + t2) + half
+                        nc.tensor.transpose(
+                            h_turned[:, (2 * half + t2) * P : (2 * half + t2 + 1) * P],
+                            h_perm[:, g * P : (g + 1) * P],
+                            ident_f32[:],
+                        )
+                h_values = h_turned[:].bitcast(BF16)
+                nc.scalar.activation(
+                    out=silu_grouped[:, 4 * HALF * hf : 4 * HALF * (hf + 1)].rearrange(
+                        "p (n h u) -> p n h u", h=HALVES, u=2
+                    ),
+                    in_=h_values.rearrange("p (h n u) -> p n h u", h=HALVES, u=2),
+                    func=ACT.Silu,
+                )
+                by_half = h_values.rearrange("p (h x) -> p h x", h=HALVES)
+                x_cols = slice(2 * HALF * hf, 2 * HALF * (hf + 1))
+                nc.vector.tensor_copy(out=shifted_view[:, 0, :, x_cols], in_=by_half)
+                nc.vector.tensor_scalar_add(out=shifted_view[:, 1, :, x_cols], in0=by_half, scalar1=-SPACING)
+            shifted.append(shifted_view)
+            n_cols = slice(ch * CHUNK, (ch + 1) * CHUNK)
+            nc.vector.quantize_mx(
+                out=silu_codes[:, n_cols].bitcast(FP8X4), scales=silu_scales[:, n_cols], in_=silu_grouped[:]
+            )
+
+        bias_turned = turned.tile([P, P], BF16, tag="turned")
+        nc.tensor.transpose(bias_turned[:], bias_rows[:], ident_bf16[:])
+        bias_sb = keep.tile([P, ROW_TILES], F32)
+        nc.vector.tensor_copy(out=bias_sb[:], in_=bias_turned[:, 0:ROW_TILES])
+
+        w_codes = keep.tile([P, ROW_TILES * PASSES * P], U32, align_bytes=64)
+        w_scales = keep.tile([P, ROW_TILES * PASSES * P], U8, align_bytes=64)
+
+        bw_perm = keep.tile([P, 8 * P], F32)
+        nc.vector.tensor_copy(out=partition_order(bw_perm[:], 8), in_=class_order(bw_nat[:].bitcast(F32), 8))
+        bw_grouped = keep.tile([P, ROW_TILES * 4 * P], BF16, align_bytes=64)
+        for mp in range(ROW_TILES // 2):
+            bw_turned = turned.tile([P, CHUNK], F32, tag="turned")
+            for g in range(4):
+                nc.tensor.transpose(
+                    bw_turned[:, g * P : (g + 1) * P], bw_perm[:, (4 * mp + g) * P : (4 * mp + g + 1) * P], ident_f32[:]
+                )
+            nc.scalar.copy(
+                out=bw_grouped[:].bitcast(F32)[:, mp * CHUNK : (mp + 1) * CHUNK].rearrange(
+                    "p (m q h) -> p m q h", m=2, h=HALVES
+                ),
+                in_=bw_turned[:].rearrange("p (m h q) -> p m q h", m=2, h=HALVES),
+            )
+        for m in range(ROW_TILES):
+            w_cols = slice((m * PASSES + BASE_PASS) * P, (m * PASSES + BASE_PASS + 1) * P)
+            nc.vector.quantize_mx(
+                out=w_codes[:, w_cols].bitcast(FP8X4),
+                scales=w_scales[:, w_cols],
+                in_=bw_grouped[:, m * 4 * P : (m + 1) * 4 * P],
+            )
+
+        for m in range(ROW_TILES):
+            for half in range(HALVES):
+                w_perm = stage.tile([P, 8 * P], F32, tag="perm")
+                nc.vector.tensor_copy(
+                    out=w_perm[:].rearrange("q (s c a x) -> q s c a x", s=8, c=4, a=16, x=2),
+                    in_=w_nat[m][:]
+                    .bitcast(F32)[:, half * 8 * P : (half + 1) * 8 * P]
+                    .rearrange("q (a c x s) -> q s c a x", a=16, c=4, x=2, s=8),
+                )
+                w_grouped = stage.tile([P, PAIRS * 4 * P], BF16, align_bytes=64, tag="grouped")
+                for pi0 in range(0, PAIRS, 2):
+                    w_turned = turned.tile([P, CHUNK], F32, tag="turned")
+                    for a2 in range(2):
+                        for u in range(2):
+                            s = 4 * u + pi0 + a2
+                            nc.tensor.transpose(
+                                w_turned[:, (2 * a2 + u) * P : (2 * a2 + u + 1) * P],
+                                w_perm[:, s * P : (s + 1) * P],
+                                ident_f32[:],
+                            )
+                    nc.scalar.copy(
+                        out=w_grouped[:].bitcast(F32)[:, pi0 * 2 * P : (pi0 + 2) * 2 * P].rearrange(
+                            "p (a q u) -> p a q u", a=2, u=2
+                        ),
+                        in_=w_turned[:].rearrange("p (a u q) -> p a q u", a=2, u=2),
+                    )
+                w_cols = slice((m * PASSES + half * PAIRS) * P, (m * PASSES + (half + 1) * PAIRS) * P)
+                nc.vector.quantize_mx(
+                    out=w_codes[:, w_cols].bitcast(FP8X4), scales=w_scales[:, w_cols], in_=w_grouped[:]
+                )
+
+        def multiply(acc, k_pass, codes, scales, start, stop):
+            for m in range(ROW_TILES):
+                w_cols = slice((m * PASSES + k_pass) * P, (m * PASSES + k_pass + 1) * P)
+                nc.tensor.matmul_mx(
+                    out=acc[m][:],
+                    lhsT=w_codes[:, w_cols].bitcast(FP8X4),
+                    lhsT_scale=w_scales[:, w_cols],
+                    rhs=codes.bitcast(FP8X4),
+                    rhs_scale=scales,
+                    start=start,
+                    stop=stop,
+                )
+
+        for ch in range(CHUNKS):
+            acc = [sums.tile([P, CHUNK], F32, name="acc%d" % m) for m in range(ROW_TILES)]
+            n_cols = slice(ch * CHUNK, (ch + 1) * CHUNK)
+            multiply(acc, BASE_PASS, silu_codes[:, n_cols], silu_scales[:, n_cols], True, False)
+            for k_pass in range(SPLINE_PASSES):
+                half, pi = divmod(k_pass, PAIRS)
+                centre = -1.0 + 2 * pi * SPACING
+                source = shifted[ch][:, :, half, :]
+                square = ring.tile([P, 4 * CHUNK], F32)
+                square_view = square[:].rearrange("p (e x) -> p e x", e=2)
+                if (ch * SPLINE_PASSES + k_pass) % SCALAR_SQUARES_EVERY == SCALAR_SQUARES_EVERY - 1:
+                    nc.scalar.activation(out=square_view, in_=source, func=ACT.Square, bias=-centre, scale=1.0)
+                    rest = 0.0
+                else:
+                    nc.vector.scalar_tensor_tensor(
+                        out=square_view, in0=source, scalar=2.0 * centre, in1=source, op0=ALU.subtract, op1=ALU.mult
+                    )
+                    rest = centre * centre
+                basis = ring.tile([P, 4 * CHUNK], BF16, align_bytes=64)
+                nc.scalar.activation(
+                    out=basis[:].rearrange("p (x e) -> p x e", e=2),
+                    in_=square[:].rearrange("p (e x) -> p x e", e=2),
+                    func=ACT.Exp,
+                    bias=-rest / (SPACING * SPACING),
+                    scale=-1.0 / (SPACING * SPACING),
+                )
+                codes = ring.tile([P, CHUNK], U32, align_bytes=64, bufs=4)
+                scales = ring.tile([P, CHUNK], U8, align_bytes=64, bufs=4)
+                nc.vector.quantize_mx(out=codes[:].bitcast(FP8X4), scales=scales[:], in_=basis[:])
+                multiply(acc, k_pass, codes[:], scales[:], False, k_pass == SPLINE_PASSES - 1)
+            for m in range(ROW_TILES):
+                result = ring.tile([P, CHUNK], F32)
+                nc.vector.scalar_tensor_tensor(
+                    out=result[:],
+                    in0=acc[m][:],
+                    scalar=bias_sb[:, m : m + 1],
+                    in1=x_sb[:, m * COLS + ch * CHUNK : m * COLS + (ch + 1) * CHUNK],
+                    op0=ALU.add,
+                    op1=ALU.add,
+                )
+                for hf in range(2):
+                    b, c0 = divmod(ch * CHUNK + hf * HALF, CHANNELS)
+                    nc.sync.dma_start(
+                        out=out[b, m * P : (m + 1) * P, c0 : c0 + HALF], in_=result[:, hf * HALF : (hf + 1) * HALF]
+                    )

@@ -16,7 +16,7 @@ BATCH, CHANNELS, HIDDEN, ROWS, CENTRES = 2, 768, 512, 512, 8
 COLS = BATCH * CHANNELS
 CHUNK = 512
 CHUNKS = COLS // CHUNK
-HALF = CHUNK // 2
+STORE_COLS = 256
 ROW_TILES = ROWS // P
 SPACING = 2.0 / (CENTRES - 1)
 PAIRS = CENTRES // 2
@@ -24,28 +24,39 @@ HALVES = 2
 SPLINE_PASSES = HALVES * PAIRS
 BASE_PASS = SPLINE_PASSES
 PASSES = SPLINE_PASSES + 1
-SCALAR_SQUARES_EVERY = 3
+STEPS = CHUNKS * SPLINE_PASSES
+WORD_GROUPS = 8
+AHEAD = 2
+SCALAR_SQUARES_EVERY = 4
+JOBS = HALVES * ROW_TILES
+CODE_BUFS = 10
+MID_CHUNK = 3
+
+assert JOBS == SPLINE_PASSES
 
 FLOPS = 2 * COLS * ROWS * (HIDDEN * CENTRES + HIDDEN)
 
 
-def class_order(words, groups):
-    return words.rearrange("r (g a c x) -> r g c a x", g=groups, a=16, c=4, x=2)
+def unit_order(words):
+    return words.rearrange("r (g a c x) -> r g c a x", g=WORD_GROUPS, a=16, c=4, x=2)
 
 
-def partition_order(words, groups):
-    return words.rearrange("r (g c a x) -> r g c a x", g=groups, c=4, a=16, x=2)
+def partition_order(words):
+    return words.rearrange("r (g c a x) -> r g c a x", g=WORD_GROUPS, c=4, a=16, x=2)
 
 
 def tile_kan1_pb_kernel(tc, h_mix, x, fc2_spline_w, fc2_base_w, fc2_base_b, out):
     nc = tc.nc
     with ExitStack() as stack:
+        stack.enter_context(tc.manual_schedule())
         keep = stack.enter_context(tc.tile_pool(name="keep", bufs=1))
-        stage = stack.enter_context(tc.tile_pool(name="stage", bufs=2))
         ring = stack.enter_context(tc.tile_pool(name="ring", bufs=3))
         turned = stack.enter_context(tc.psum_pool(name="turned", bufs=4))
         sums = stack.enter_context(tc.psum_pool(name="sums", bufs=1))
 
+        bias_rows = keep.tile([P, P], BF16)
+        nc.vector.memset(bias_rows[:], 0.0)
+        nc.sync.dma_start(out=bias_rows[0:ROW_TILES, :], in_=fc2_base_b.rearrange("(m q) -> m q", q=P))
         h_rows = h_mix.flatten_outer_dims()
         h_nat = []
         for ch in range(CHUNKS):
@@ -62,12 +73,9 @@ def tile_kan1_pb_kernel(tc, h_mix, x, fc2_spline_w, fc2_base_w, fc2_base_b, out)
         )
         w_nat = []
         for m in range(ROW_TILES):
-            w_tile = ring.tile([P, HIDDEN * CENTRES], BF16, name="w_nat", bufs=ROW_TILES)
+            w_tile = keep.tile([P, HIDDEN * CENTRES], BF16, name="w_nat%d" % m)
             nc.sync.dma_start(out=w_tile[:], in_=fc2_spline_w[m * P : (m + 1) * P, :])
             w_nat.append(w_tile)
-        bias_rows = keep.tile([P, P], BF16)
-        nc.vector.memset(bias_rows[:], 0.0)
-        nc.sync.dma_start(out=bias_rows[0:ROW_TILES, :], in_=fc2_base_b.rearrange("(m q) -> m q", q=P))
         x_sb = keep.tile([P, ROW_TILES * COLS], BF16)
         for m in range(ROW_TILES):
             nc.sync.dma_start(
@@ -80,42 +88,65 @@ def tile_kan1_pb_kernel(tc, h_mix, x, fc2_spline_w, fc2_base_w, fc2_base_b, out)
         ident_bf16 = keep.tile([P, P], BF16)
         make_identity(nc, ident_bf16[:])
 
-        silu_codes = keep.tile([P, COLS], U32, align_bytes=64)
-        silu_scales = keep.tile([P, COLS], U8, align_bytes=64)
-        shifted = []
-        for ch in range(CHUNKS):
-            h_perm = stage.tile([P, 8 * P], F32, tag="perm")
-            nc.vector.tensor_copy(out=partition_order(h_perm[:], 8), in_=class_order(h_nat[ch][:].bitcast(F32), 8))
-            shifted_tile = keep.tile([P, 2 * HALVES * 2 * CHUNK], F32, name="shifted%d" % ch)
-            shifted_view = shifted_tile[:].rearrange("p (e h x) -> p e h x", e=2, h=HALVES)
-            silu_grouped = stage.tile([P, 4 * CHUNK], BF16, align_bytes=64, tag="grouped")
-            for hf in range(2):
-                h_turned = turned.tile([P, CHUNK], F32, tag="turned")
-                for half in range(HALVES):
-                    for t2 in range(2):
-                        g = 2 * (2 * hf + t2) + half
-                        nc.tensor.transpose(
-                            h_turned[:, (2 * half + t2) * P : (2 * half + t2 + 1) * P],
-                            h_perm[:, g * P : (g + 1) * P],
-                            ident_f32[:],
-                        )
-                h_values = h_turned[:].bitcast(BF16)
-                nc.scalar.activation(
-                    out=silu_grouped[:, 4 * HALF * hf : 4 * HALF * (hf + 1)].rearrange(
-                        "p (n h u) -> p n h u", h=HALVES, u=2
-                    ),
-                    in_=h_values.rearrange("p (h n u) -> p n h u", h=HALVES, u=2),
-                    func=ACT.Silu,
+        warm_in = keep.tile([P, 1], F32)
+        nc.vector.memset(warm_in[:], 0.0)
+        warm_out = keep.tile([P, 1], F32)
+        nc.scalar.activation(out=warm_out[:], in_=warm_in[:], func=ACT.Silu)
+
+        def turn(words, groups):
+            bank = turned.tile([P, CHUNK], F32, tag="turned", name="bank")
+            for place, g in enumerate(groups):
+                nc.tensor.transpose(
+                    bank[:, place * P : (place + 1) * P], words[:, g * P : (g + 1) * P], ident_f32[:]
                 )
-                by_half = h_values.rearrange("p (h x) -> p h x", h=HALVES)
-                x_cols = slice(2 * HALF * hf, 2 * HALF * (hf + 1))
-                nc.vector.tensor_copy(out=shifted_view[:, 0, :, x_cols], in_=by_half)
-                nc.vector.tensor_scalar_add(out=shifted_view[:, 1, :, x_cols], in0=by_half, scalar1=-SPACING)
-            shifted.append(shifted_view)
-            n_cols = slice(ch * CHUNK, (ch + 1) * CHUNK)
-            nc.vector.quantize_mx(
-                out=silu_codes[:, n_cols].bitcast(FP8X4), scales=silu_scales[:, n_cols], in_=silu_grouped[:]
+            return bank
+
+        h_perm = {}
+        hidden = []
+        silu_grouped = []
+
+        def permute_hidden(ch):
+            h_perm[ch] = ring.tile([P, WORD_GROUPS * P], F32, tag="perm", name="h_perm", bufs=2)
+            for half in range(HALVES):
+                nc.vector.tensor_copy(
+                    out=h_perm[ch][:, half * CHUNK : (half + 1) * CHUNK].rearrange(
+                        "r (t c a x) -> r t c a x", t=4, c=4, a=16, x=2
+                    ),
+                    in_=h_nat[ch][:]
+                    .bitcast(F32)
+                    .rearrange("r (t h w) -> r t h w", t=4, h=HALVES)[:, :, half, :]
+                    .rearrange("r t (a c x) -> r t c a x", a=16, c=4, x=2),
+                )
+
+        def turn_hidden(ch):
+            hidden_tile = keep.tile([P, 4 * CHUNK], BF16, name="hidden%d" % ch)
+            for half in range(HALVES):
+                bank = turn(h_perm[ch], range(4 * half, 4 * half + 4))
+                nc.vector.tensor_copy(
+                    out=hidden_tile[:].bitcast(F32)[:, half * CHUNK : (half + 1) * CHUNK], in_=bank[:]
+                )
+            hidden.append(hidden_tile)
+            grouped = ring.tile([P, 4 * CHUNK], BF16, align_bytes=64, tag="grouped", name="silu_grouped")
+            nc.scalar.activation(
+                out=grouped[:].rearrange("p (n h u) -> p n h u", h=HALVES, u=2),
+                in_=hidden_tile[:].rearrange("p (h n u) -> p n h u", h=HALVES, u=2),
+                func=ACT.Silu,
             )
+            silu_grouped.append(grouped)
+
+        shifted = {}
+
+        def shift(ch):
+            shifted[ch] = ring.tile([P, 2 * 4 * CHUNK], F32, name="shifted", bufs=2)
+            nc.vector.tensor_copy(out=shifted[ch][:, 0 : 4 * CHUNK], in_=hidden[ch][:])
+            nc.vector.tensor_scalar_add(out=shifted[ch][:, 4 * CHUNK : 8 * CHUNK], in0=hidden[ch][:], scalar1=-SPACING)
+
+        permute_hidden(0)
+        for ch in range(CHUNKS):
+            if ch + 1 < CHUNKS:
+                permute_hidden(ch + 1)
+            turn_hidden(ch)
+        shift(0)
 
         bias_turned = turned.tile([P, P], BF16, tag="turned")
         nc.tensor.transpose(bias_turned[:], bias_rows[:], ident_bf16[:])
@@ -125,21 +156,28 @@ def tile_kan1_pb_kernel(tc, h_mix, x, fc2_spline_w, fc2_base_w, fc2_base_b, out)
         w_codes = keep.tile([P, ROW_TILES * PASSES * P], U32, align_bytes=64)
         w_scales = keep.tile([P, ROW_TILES * PASSES * P], U8, align_bytes=64)
 
-        bw_perm = keep.tile([P, 8 * P], F32)
-        nc.vector.tensor_copy(out=partition_order(bw_perm[:], 8), in_=class_order(bw_nat[:].bitcast(F32), 8))
-        bw_grouped = keep.tile([P, ROW_TILES * 4 * P], BF16, align_bytes=64)
-        for mp in range(ROW_TILES // 2):
-            bw_turned = turned.tile([P, CHUNK], F32, tag="turned")
-            for g in range(4):
-                nc.tensor.transpose(
-                    bw_turned[:, g * P : (g + 1) * P], bw_perm[:, (4 * mp + g) * P : (4 * mp + g + 1) * P], ident_f32[:]
-                )
-            nc.scalar.copy(
-                out=bw_grouped[:].bitcast(F32)[:, mp * CHUNK : (mp + 1) * CHUNK].rearrange(
-                    "p (m q h) -> p m q h", m=2, h=HALVES
-                ),
-                in_=bw_turned[:].rearrange("p (m h q) -> p m q h", m=2, h=HALVES),
+        def regroup(grouped, first_word, bank):
+            nc.vector.tensor_copy(
+                out=grouped[:]
+                .bitcast(F32)[:, first_word : first_word + CHUNK]
+                .rearrange("p (a q s) -> p a q s", a=2, s=2),
+                in_=bank[:].rearrange("p (a s q) -> p a q s", a=2, s=2),
             )
+
+        bw_perm = ring.tile([P, WORD_GROUPS * P], F32, tag="perm", bufs=2)
+        nc.vector.tensor_copy(out=partition_order(bw_perm[:]), in_=unit_order(bw_nat[:].bitcast(F32)))
+        bw_banks = [turn(bw_perm, range(4 * m_pair, 4 * m_pair + 4)) for m_pair in range(2)]
+        silu_codes = keep.tile([P, COLS], U32, align_bytes=64)
+        silu_scales = keep.tile([P, COLS], U8, align_bytes=64)
+        for ch in range(CHUNKS):
+            n_cols = slice(ch * CHUNK, (ch + 1) * CHUNK)
+            nc.vector.quantize_mx(
+                out=silu_codes[:, n_cols].bitcast(FP8X4), scales=silu_scales[:, n_cols], in_=silu_grouped[ch][:]
+            )
+        bw_grouped = ring.tile([P, ROW_TILES * 4 * P], BF16, align_bytes=64, tag="grouped")
+        for m_pair in range(2):
+            regroup(bw_grouped, m_pair * CHUNK, bw_banks[m_pair])
+
         for m in range(ROW_TILES):
             w_cols = slice((m * PASSES + BASE_PASS) * P, (m * PASSES + BASE_PASS + 1) * P)
             nc.vector.quantize_mx(
@@ -148,92 +186,128 @@ def tile_kan1_pb_kernel(tc, h_mix, x, fc2_spline_w, fc2_base_w, fc2_base_b, out)
                 in_=bw_grouped[:, m * 4 * P : (m + 1) * 4 * P],
             )
 
-        for m in range(ROW_TILES):
-            for half in range(HALVES):
-                w_perm = stage.tile([P, 8 * P], F32, tag="perm")
-                nc.vector.tensor_copy(
-                    out=w_perm[:].rearrange("q (s c a x) -> q s c a x", s=8, c=4, a=16, x=2),
-                    in_=w_nat[m][:]
-                    .bitcast(F32)[:, half * 8 * P : (half + 1) * 8 * P]
-                    .rearrange("q (a c x s) -> q s c a x", a=16, c=4, x=2, s=8),
-                )
-                w_grouped = stage.tile([P, PAIRS * 4 * P], BF16, align_bytes=64, tag="grouped")
-                for pi0 in range(0, PAIRS, 2):
-                    w_turned = turned.tile([P, CHUNK], F32, tag="turned")
-                    for a2 in range(2):
-                        for u in range(2):
-                            s = 4 * u + pi0 + a2
-                            nc.tensor.transpose(
-                                w_turned[:, (2 * a2 + u) * P : (2 * a2 + u + 1) * P],
-                                w_perm[:, s * P : (s + 1) * P],
-                                ident_f32[:],
-                            )
-                    nc.scalar.copy(
-                        out=w_grouped[:].bitcast(F32)[:, pi0 * 2 * P : (pi0 + 2) * 2 * P].rearrange(
-                            "p (a q u) -> p a q u", a=2, u=2
-                        ),
-                        in_=w_turned[:].rearrange("p (a u q) -> p a q u", a=2, u=2),
-                    )
-                w_cols = slice((m * PASSES + half * PAIRS) * P, (m * PASSES + (half + 1) * PAIRS) * P)
-                nc.vector.quantize_mx(
-                    out=w_codes[:, w_cols].bitcast(FP8X4), scales=w_scales[:, w_cols], in_=w_grouped[:]
-                )
+        w_banks = {}
 
-        def multiply(acc, k_pass, codes, scales, start, stop):
+        def turn_weights(job):
+            half, m = divmod(job, ROW_TILES)
+            w_perm = ring.tile([P, WORD_GROUPS * P], F32, tag="perm", bufs=2)
+            nc.vector.tensor_copy(
+                out=partition_order(w_perm[:]),
+                in_=w_nat[m][:]
+                .bitcast(F32)[:, half * WORD_GROUPS * P : (half + 1) * WORD_GROUPS * P]
+                .rearrange("q (a c x g) -> q g c a x", a=16, c=4, x=2, g=WORD_GROUPS),
+            )
+            w_banks[job] = [
+                turn(w_perm, [4 * u + pi0 + a for a in range(2) for u in range(2)]) for pi0 in range(0, PAIRS, 2)
+            ]
+
+        def pack_weights(job):
+            half, m = divmod(job, ROW_TILES)
+            w_grouped = ring.tile([P, PAIRS * 4 * P], BF16, align_bytes=64, tag="grouped")
+            for place, bank in enumerate(w_banks[job]):
+                regroup(w_grouped, place * CHUNK, bank)
+            if job + 1 < JOBS:
+                turn_weights(job + 1)
+            w_cols = slice((m * PASSES + half * PAIRS) * P, (m * PASSES + (half + 1) * PAIRS) * P)
+            nc.vector.quantize_mx(out=w_codes[:, w_cols].bitcast(FP8X4), scales=w_scales[:, w_cols], in_=w_grouped[:])
+
+        square = {}
+        basis = {}
+        rest = {}
+        codes = {}
+        scales = {}
+        acc = {}
+
+        def squares(step):
+            ch, k_pass = divmod(step, SPLINE_PASSES)
+            half, pi = divmod(k_pass, PAIRS)
+            centre = -1.0 + 2 * pi * SPACING
+            source = shifted[ch][:].rearrange("p (e h x) -> p e h x", e=2, h=HALVES)[:, :, half, :]
+            square[step] = ring.tile([P, 4 * CHUNK], F32, name="square")
+            target = square[step][:].rearrange("p (e x) -> p e x", e=2)
+            if ch == 0 or k_pass % SCALAR_SQUARES_EVERY == SCALAR_SQUARES_EVERY - 1:
+                nc.scalar.activation(out=target, in_=source, func=ACT.Square, bias=-centre, scale=1.0)
+                rest[step] = 0.0
+            else:
+                nc.vector.scalar_tensor_tensor(
+                    out=target, in0=source, scalar=2.0 * centre, in1=source, op0=ALU.subtract, op1=ALU.mult
+                )
+                rest[step] = centre * centre
+
+        def exponentials(step):
+            basis[step] = ring.tile([P, 4 * CHUNK], BF16, align_bytes=64, name="basis")
+            nc.scalar.activation(
+                out=basis[step][:].rearrange("p (x e) -> p x e", e=2),
+                in_=square[step][:].rearrange("p (e x) -> p x e", e=2),
+                func=ACT.Exp,
+                bias=-rest[step] / (SPACING * SPACING),
+                scale=-1.0 / (SPACING * SPACING),
+            )
+
+        def quantise(step):
+            codes[step] = ring.tile([P, CHUNK], U32, align_bytes=64, name="codes", bufs=CODE_BUFS)
+            scales[step] = ring.tile([P, CHUNK], U8, align_bytes=64, name="scales", bufs=CODE_BUFS)
+            nc.vector.quantize_mx(out=codes[step][:].bitcast(FP8X4), scales=scales[step][:], in_=basis[step][:])
+
+        def one_pass(ch, k_pass, rhs, rhs_scale):
             for m in range(ROW_TILES):
                 w_cols = slice((m * PASSES + k_pass) * P, (m * PASSES + k_pass + 1) * P)
                 nc.tensor.matmul_mx(
-                    out=acc[m][:],
+                    out=acc[ch][m][:],
                     lhsT=w_codes[:, w_cols].bitcast(FP8X4),
                     lhsT_scale=w_scales[:, w_cols],
-                    rhs=codes.bitcast(FP8X4),
-                    rhs_scale=scales,
-                    start=start,
-                    stop=stop,
+                    rhs=rhs.bitcast(FP8X4),
+                    rhs_scale=rhs_scale,
+                    start=(k_pass == BASE_PASS),
+                    stop=(k_pass == SPLINE_PASSES - 1),
                 )
 
-        for ch in range(CHUNKS):
-            acc = [sums.tile([P, CHUNK], F32, name="acc%d" % m) for m in range(ROW_TILES)]
-            n_cols = slice(ch * CHUNK, (ch + 1) * CHUNK)
-            multiply(acc, BASE_PASS, silu_codes[:, n_cols], silu_scales[:, n_cols], True, False)
-            for k_pass in range(SPLINE_PASSES):
-                half, pi = divmod(k_pass, PAIRS)
-                centre = -1.0 + 2 * pi * SPACING
-                source = shifted[ch][:, :, half, :]
-                square = ring.tile([P, 4 * CHUNK], F32)
-                square_view = square[:].rearrange("p (e x) -> p e x", e=2)
-                if (ch * SPLINE_PASSES + k_pass) % SCALAR_SQUARES_EVERY == SCALAR_SQUARES_EVERY - 1:
-                    nc.scalar.activation(out=square_view, in_=source, func=ACT.Square, bias=-centre, scale=1.0)
-                    rest = 0.0
-                else:
-                    nc.vector.scalar_tensor_tensor(
-                        out=square_view, in0=source, scalar=2.0 * centre, in1=source, op0=ALU.subtract, op1=ALU.mult
-                    )
-                    rest = centre * centre
-                basis = ring.tile([P, 4 * CHUNK], BF16, align_bytes=64)
-                nc.scalar.activation(
-                    out=basis[:].rearrange("p (x e) -> p x e", e=2),
-                    in_=square[:].rearrange("p (e x) -> p x e", e=2),
-                    func=ACT.Exp,
-                    bias=-rest / (SPACING * SPACING),
-                    scale=-1.0 / (SPACING * SPACING),
-                )
-                codes = ring.tile([P, CHUNK], U32, align_bytes=64, bufs=4)
-                scales = ring.tile([P, CHUNK], U8, align_bytes=64, bufs=4)
-                nc.vector.quantize_mx(out=codes[:].bitcast(FP8X4), scales=scales[:], in_=basis[:])
-                multiply(acc, k_pass, codes[:], scales[:], False, k_pass == SPLINE_PASSES - 1)
+        def multiply(step):
+            ch, k_pass = divmod(step, SPLINE_PASSES)
+            if k_pass == 0:
+                acc[ch] = [sums.tile([P, CHUNK], F32, name="acc%d" % m) for m in range(ROW_TILES)]
+                n_cols = slice(ch * CHUNK, (ch + 1) * CHUNK)
+                one_pass(ch, BASE_PASS, silu_codes[:, n_cols], silu_scales[:, n_cols])
+            one_pass(ch, k_pass, codes[step][:], scales[step][:])
+
+        def finish(ch):
             for m in range(ROW_TILES):
                 result = ring.tile([P, CHUNK], F32)
                 nc.vector.scalar_tensor_tensor(
                     out=result[:],
-                    in0=acc[m][:],
+                    in0=acc[ch][m][:],
                     scalar=bias_sb[:, m : m + 1],
                     in1=x_sb[:, m * COLS + ch * CHUNK : m * COLS + (ch + 1) * CHUNK],
                     op0=ALU.add,
                     op1=ALU.add,
                 )
-                for hf in range(2):
-                    b, c0 = divmod(ch * CHUNK + hf * HALF, CHANNELS)
+                for first in range(0, CHUNK, STORE_COLS):
+                    b, c0 = divmod(ch * CHUNK + first, CHANNELS)
                     nc.sync.dma_start(
-                        out=out[b, m * P : (m + 1) * P, c0 : c0 + HALF], in_=result[:, hf * HALF : (hf + 1) * HALF]
+                        out=out[b, m * P : (m + 1) * P, c0 : c0 + STORE_COLS], in_=result[:, first : first + STORE_COLS]
                     )
+
+        turn_weights(0)
+        for step in range(AHEAD):
+            squares(step)
+        for step in range(STEPS):
+            ch, k_pass = divmod(step, SPLINE_PASSES)
+            exponentials(step)
+            if ch == 0:
+                pack_weights(k_pass)
+            if k_pass == MID_CHUNK and ch + 1 < CHUNKS:
+                shift(ch + 1)
+            if step + AHEAD < STEPS:
+                squares(step + AHEAD)
+            quantise(step)
+            if ch == 0:
+                if k_pass >= ROW_TILES:
+                    multiply(step - ROW_TILES)
+            else:
+                if step == SPLINE_PASSES:
+                    for late in range(SPLINE_PASSES - ROW_TILES, SPLINE_PASSES):
+                        multiply(late)
+                multiply(step)
+            if k_pass == MID_CHUNK and ch > 0:
+                finish(ch - 1)
+        finish(CHUNKS - 1)

@@ -27,7 +27,10 @@ PASSES = SPLINE_PASSES + 1
 STEPS = CHUNKS * SPLINE_PASSES
 WORD_GROUPS = 8
 AHEAD = 2
-SCALAR_SQUARES_EVERY = 4
+SHARE = 4
+UNIT_COLS = 256
+UNITS = COLS // UNIT_COLS
+UNITS_PER_CHUNK = CHUNK // UNIT_COLS
 JOBS = HALVES * ROW_TILES
 CODE_BUFS = 10
 MID_CHUNK = 3
@@ -38,11 +41,11 @@ FLOPS = 2 * COLS * ROWS * (HIDDEN * CENTRES + HIDDEN)
 
 
 def unit_order(words):
-    return words.rearrange("r (g a c x) -> r g c a x", g=WORD_GROUPS, a=16, c=4, x=2)
+    return words.rearrange("r (g a c x) -> r g c a x", a=16, c=4, x=2)
 
 
 def partition_order(words):
-    return words.rearrange("r (g c a x) -> r g c a x", g=WORD_GROUPS, c=4, a=16, x=2)
+    return words.rearrange("r (g c a x) -> r g c a x", c=4, a=16, x=2)
 
 
 def tile_kan1_pb_kernel(tc, h_mix, x, fc2_spline_w, fc2_base_w, fc2_base_b, out):
@@ -59,11 +62,11 @@ def tile_kan1_pb_kernel(tc, h_mix, x, fc2_spline_w, fc2_base_w, fc2_base_b, out)
         nc.sync.dma_start(out=bias_rows[0:ROW_TILES, :], in_=fc2_base_b.rearrange("(m q) -> m q", q=P))
         h_rows = h_mix.flatten_outer_dims()
         h_nat = []
-        for ch in range(CHUNKS):
-            h_tile = keep.tile([P, 4 * HIDDEN], BF16, name="h_nat%d" % ch)
+        for unit in range(UNITS):
+            h_tile = keep.tile([P, 2 * HIDDEN], BF16, name="h_nat%d" % unit)
             nc.sync.dma_start(
-                out=h_tile[:].rearrange("r (t j) -> r t j", t=4),
-                in_=h_rows[ch * CHUNK : (ch + 1) * CHUNK, :].rearrange("(t r) j -> r t j", r=P),
+                out=h_tile[:].rearrange("r (t j) -> r t j", t=2),
+                in_=h_rows[unit * UNIT_COLS : (unit + 1) * UNIT_COLS, :].rearrange("(t r) j -> r t j", r=P),
             )
             h_nat.append(h_tile)
         bw_nat = keep.tile([P, ROW_TILES * HIDDEN], BF16)
@@ -105,47 +108,40 @@ def tile_kan1_pb_kernel(tc, h_mix, x, fc2_spline_w, fc2_base_w, fc2_base_b, out)
         hidden = []
         silu_grouped = []
 
-        def permute_hidden(ch):
-            h_perm[ch] = ring.tile([P, WORD_GROUPS * P], F32, tag="perm", name="h_perm", bufs=2)
-            for half in range(HALVES):
-                nc.vector.tensor_copy(
-                    out=h_perm[ch][:, half * CHUNK : (half + 1) * CHUNK].rearrange(
-                        "r (t c a x) -> r t c a x", t=4, c=4, a=16, x=2
-                    ),
-                    in_=h_nat[ch][:]
-                    .bitcast(F32)
-                    .rearrange("r (t h w) -> r t h w", t=4, h=HALVES)[:, :, half, :]
-                    .rearrange("r t (a c x) -> r t c a x", a=16, c=4, x=2),
-                )
+        def permute_hidden(unit):
+            h_perm[unit] = ring.tile([P, 4 * P], F32, name="h_perm", bufs=2)
+            nc.vector.tensor_copy(out=partition_order(h_perm[unit][:]), in_=unit_order(h_nat[unit][:].bitcast(F32)))
 
-        def turn_hidden(ch):
-            hidden_tile = keep.tile([P, 4 * CHUNK], BF16, name="hidden%d" % ch)
-            for half in range(HALVES):
-                bank = turn(h_perm[ch], range(4 * half, 4 * half + 4))
-                nc.vector.tensor_copy(
-                    out=hidden_tile[:].bitcast(F32)[:, half * CHUNK : (half + 1) * CHUNK], in_=bank[:]
+        def turn_hidden(unit):
+            ch, part = divmod(unit, UNITS_PER_CHUNK)
+            if part == 0:
+                hidden.append(keep.tile([P, 4 * CHUNK], BF16, name="hidden%d" % ch))
+                silu_grouped.append(
+                    ring.tile([P, 4 * CHUNK], BF16, align_bytes=64, tag="grouped", name="silu_grouped")
                 )
-            hidden.append(hidden_tile)
-            grouped = ring.tile([P, 4 * CHUNK], BF16, align_bytes=64, tag="grouped", name="silu_grouped")
+            n_cols = slice(part * UNIT_COLS, (part + 1) * UNIT_COLS)
+            bank = turn(h_perm[unit], [2 * t + half for half in range(HALVES) for t in range(2)])
+            nc.vector.tensor_copy(
+                out=hidden[ch][:].bitcast(F32).rearrange("p (h n) -> p h n", h=HALVES)[:, :, n_cols],
+                in_=bank[:].rearrange("p (h n) -> p h n", h=HALVES),
+            )
             nc.scalar.activation(
-                out=grouped[:].rearrange("p (n h u) -> p n h u", h=HALVES, u=2),
-                in_=hidden_tile[:].rearrange("p (h n u) -> p n h u", h=HALVES, u=2),
+                out=silu_grouped[ch][:].rearrange("p (n h u) -> p n h u", h=HALVES, u=2)[:, n_cols, :, :],
+                in_=hidden[ch][:].rearrange("p (h n u) -> p n h u", h=HALVES, u=2)[:, n_cols, :, :],
                 func=ACT.Silu,
             )
-            silu_grouped.append(grouped)
 
         shifted = {}
 
         def shift(ch):
-            shifted[ch] = ring.tile([P, 2 * 4 * CHUNK], F32, name="shifted", bufs=2)
-            nc.vector.tensor_copy(out=shifted[ch][:, 0 : 4 * CHUNK], in_=hidden[ch][:])
-            nc.vector.tensor_scalar_add(out=shifted[ch][:, 4 * CHUNK : 8 * CHUNK], in0=hidden[ch][:], scalar1=-SPACING)
+            shifted[ch] = ring.tile([P, 4 * CHUNK], F32, name="shifted", bufs=2)
+            nc.vector.tensor_scalar_add(out=shifted[ch][:], in0=hidden[ch][:], scalar1=-SPACING)
 
         permute_hidden(0)
-        for ch in range(CHUNKS):
-            if ch + 1 < CHUNKS:
-                permute_hidden(ch + 1)
-            turn_hidden(ch)
+        for unit in range(UNITS):
+            if unit + 1 < UNITS:
+                permute_hidden(unit + 1)
+            turn_hidden(unit)
         shift(0)
 
         bias_turned = turned.tile([P, P], BF16, tag="turned")
@@ -222,16 +218,28 @@ def tile_kan1_pb_kernel(tc, h_mix, x, fc2_spline_w, fc2_base_w, fc2_base_b, out)
             ch, k_pass = divmod(step, SPLINE_PASSES)
             half, pi = divmod(k_pass, PAIRS)
             centre = -1.0 + 2 * pi * SPACING
-            source = shifted[ch][:].rearrange("p (e h x) -> p e h x", e=2, h=HALVES)[:, :, half, :]
+            x_cols = slice(half * 2 * CHUNK, (half + 1) * 2 * CHUNK)
             square[step] = ring.tile([P, 4 * CHUNK], F32, name="square")
-            target = square[step][:].rearrange("p (e x) -> p e x", e=2)
-            if ch == 0 or k_pass % SCALAR_SQUARES_EVERY == SCALAR_SQUARES_EVERY - 1:
-                nc.scalar.activation(out=target, in_=source, func=ACT.Square, bias=-centre, scale=1.0)
+            if (k_pass % SHARE == SHARE - 1) != (ch == 0):
+                for e in range(2):
+                    nc.scalar.activation(
+                        out=square[step][:, e * 2 * CHUNK : (e + 1) * 2 * CHUNK],
+                        in_=hidden[ch][:, x_cols],
+                        func=ACT.Square,
+                        bias=-(centre + e * SPACING),
+                        scale=1.0,
+                    )
                 rest[step] = 0.0
             else:
-                nc.vector.scalar_tensor_tensor(
-                    out=target, in0=source, scalar=2.0 * centre, in1=source, op0=ALU.subtract, op1=ALU.mult
-                )
+                for e, source in enumerate((hidden[ch], shifted[ch])):
+                    nc.vector.scalar_tensor_tensor(
+                        out=square[step][:, e * 2 * CHUNK : (e + 1) * 2 * CHUNK],
+                        in0=source[:, x_cols],
+                        scalar=2.0 * centre,
+                        in1=source[:, x_cols],
+                        op0=ALU.subtract,
+                        op1=ALU.mult,
+                    )
                 rest[step] = centre * centre
 
         def exponentials(step):

@@ -26,8 +26,9 @@ BASE_PASS = SPLINE_PASSES
 PASSES = SPLINE_PASSES + 1
 STEPS = CHUNKS * SPLINE_PASSES
 WORD_GROUPS = 8
-AHEAD = 2
+AHEAD = 3
 SHARE = 4
+TURN = 1
 UNIT_COLS = 256
 UNITS = COLS // UNIT_COLS
 UNITS_PER_CHUNK = CHUNK // UNIT_COLS
@@ -219,8 +220,8 @@ def tile_kan1_pb_kernel(tc, h_mix, x, fc2_spline_w, fc2_base_w, fc2_base_b, out)
             half, pi = divmod(k_pass, PAIRS)
             centre = -1.0 + 2 * pi * SPACING
             x_cols = slice(half * 2 * CHUNK, (half + 1) * 2 * CHUNK)
-            square[step] = ring.tile([P, 4 * CHUNK], F32, name="square")
-            if (k_pass % SHARE == SHARE - 1) != (ch == 0):
+            square[step] = ring.tile([P, 4 * CHUNK], F32, name="square", bufs=AHEAD + 1)
+            if (k_pass % SHARE == TURN) != (ch == 0):
                 for e in range(2):
                     nc.scalar.activation(
                         out=square[step][:, e * 2 * CHUNK : (e + 1) * 2 * CHUNK],
@@ -243,7 +244,7 @@ def tile_kan1_pb_kernel(tc, h_mix, x, fc2_spline_w, fc2_base_w, fc2_base_b, out)
                 rest[step] = centre * centre
 
         def exponentials(step):
-            basis[step] = ring.tile([P, 4 * CHUNK], BF16, align_bytes=64, name="basis")
+            basis[step] = ring.tile([P, 4 * CHUNK], BF16, align_bytes=64, name="basis", bufs=4)
             nc.scalar.activation(
                 out=basis[step][:].rearrange("p (x e) -> p x e", e=2),
                 in_=square[step][:].rearrange("p (e x) -> p x e", e=2),
@@ -280,7 +281,7 @@ def tile_kan1_pb_kernel(tc, h_mix, x, fc2_spline_w, fc2_base_w, fc2_base_b, out)
 
         def finish(ch):
             for m in range(ROW_TILES):
-                result = ring.tile([P, CHUNK], F32)
+                result = ring.tile([P, CHUNK], F32, bufs=ROW_TILES)
                 nc.vector.scalar_tensor_tensor(
                     out=result[:],
                     in0=acc[ch][m][:],

@@ -34,7 +34,8 @@ UNITS = COLS // UNIT_COLS
 UNITS_PER_CHUNK = CHUNK // UNIT_COLS
 JOBS = HALVES * ROW_TILES
 CODE_BUFS = 10
-MID_CHUNK = 3
+SHIFT_AFTER = 3
+FINISH_AFTER = 2
 
 assert JOBS == SPLINE_PASSES
 
@@ -55,268 +56,273 @@ def tile_kan1_pb_kernel(tc, h_mix, x, fc2_spline_w, fc2_base_w, fc2_base_b, out)
         stack.enter_context(tc.manual_schedule())
         keep = stack.enter_context(tc.tile_pool(name="keep", bufs=1))
         ring = stack.enter_context(tc.tile_pool(name="ring", bufs=3))
-        turned = stack.enter_context(tc.psum_pool(name="turned", bufs=4))
-        sums = stack.enter_context(tc.psum_pool(name="sums", bufs=1))
+        sum_pools = [stack.enter_context(tc.psum_pool(name="sums_even", bufs=1))]
 
-        bias_rows = keep.tile([P, P], BF16)
-        nc.vector.memset(bias_rows[:], 0.0)
-        nc.sync.dma_start(out=bias_rows[0:ROW_TILES, :], in_=fc2_base_b.rearrange("(m q) -> m q", q=P))
-        h_rows = h_mix.flatten_outer_dims()
-        h_nat = []
-        for unit in range(UNITS):
-            h_tile = keep.tile([P, 2 * HIDDEN], BF16, name="h_nat%d" % unit)
-            nc.sync.dma_start(
-                out=h_tile[:].rearrange("r (t j) -> r t j", t=2),
-                in_=h_rows[unit * UNIT_COLS : (unit + 1) * UNIT_COLS, :].rearrange("(t r) j -> r t j", r=P),
-            )
-            h_nat.append(h_tile)
-        bw_nat = keep.tile([P, ROW_TILES * HIDDEN], BF16)
-        nc.sync.dma_start(
-            out=bw_nat[:].rearrange("q (m j) -> q m j", m=ROW_TILES),
-            in_=fc2_base_w.rearrange("(m q) j -> q m j", q=P),
-        )
-        w_nat = []
-        for m in range(ROW_TILES):
-            w_tile = keep.tile([P, HIDDEN * CENTRES], BF16, name="w_nat%d" % m)
-            nc.sync.dma_start(out=w_tile[:], in_=fc2_spline_w[m * P : (m + 1) * P, :])
-            w_nat.append(w_tile)
-        x_sb = keep.tile([P, ROW_TILES * COLS], BF16)
-        for m in range(ROW_TILES):
-            nc.sync.dma_start(
-                out=x_sb[:, m * COLS : (m + 1) * COLS].rearrange("q (b c) -> q b c", b=BATCH),
-                in_=x[:, m * P : (m + 1) * P, :].rearrange("b q c -> q b c"),
-            )
-
-        ident_f32 = keep.tile([P, P], F32)
-        make_identity(nc, ident_f32[:])
-        ident_bf16 = keep.tile([P, P], BF16)
-        make_identity(nc, ident_bf16[:])
-
-        warm_in = keep.tile([P, 1], F32)
-        nc.vector.memset(warm_in[:], 0.0)
-        warm_out = keep.tile([P, 1], F32)
-        nc.scalar.activation(out=warm_out[:], in_=warm_in[:], func=ACT.Silu)
-
-        def turn(words, groups):
-            bank = turned.tile([P, CHUNK], F32, tag="turned", name="bank")
-            for place, g in enumerate(groups):
-                nc.tensor.transpose(
-                    bank[:, place * P : (place + 1) * P], words[:, g * P : (g + 1) * P], ident_f32[:]
+        with tc.psum_pool(name="turned", bufs=4) as turned:
+            bias_rows = keep.tile([P, P], BF16)
+            nc.vector.memset(bias_rows[:], 0.0)
+            h_rows = h_mix.flatten_outer_dims()
+            h_nat = []
+            for unit in range(UNITS):
+                h_tile = keep.tile([P, 2 * HIDDEN], BF16, name="h_nat%d" % unit)
+                nc.sync.dma_start(
+                    out=h_tile[:].rearrange("r (t j) -> r t j", t=2),
+                    in_=h_rows[unit * UNIT_COLS : (unit + 1) * UNIT_COLS, :].rearrange("(t r) j -> r t j", r=P),
                 )
-            return bank
-
-        h_perm = {}
-        hidden = []
-        silu_grouped = []
-
-        def permute_hidden(unit):
-            h_perm[unit] = ring.tile([P, 4 * P], F32, name="h_perm", bufs=2)
-            nc.vector.tensor_copy(out=partition_order(h_perm[unit][:]), in_=unit_order(h_nat[unit][:].bitcast(F32)))
-
-        def turn_hidden(unit):
-            ch, part = divmod(unit, UNITS_PER_CHUNK)
-            if part == 0:
-                hidden.append(keep.tile([P, 4 * CHUNK], BF16, name="hidden%d" % ch))
-                silu_grouped.append(
-                    ring.tile([P, 4 * CHUNK], BF16, align_bytes=64, tag="grouped", name="silu_grouped")
-                )
-            n_cols = slice(part * UNIT_COLS, (part + 1) * UNIT_COLS)
-            bank = turn(h_perm[unit], [2 * t + half for half in range(HALVES) for t in range(2)])
-            nc.vector.tensor_copy(
-                out=hidden[ch][:].bitcast(F32).rearrange("p (h n) -> p h n", h=HALVES)[:, :, n_cols],
-                in_=bank[:].rearrange("p (h n) -> p h n", h=HALVES),
+                h_nat.append(h_tile)
+            nc.sync.dma_start(out=bias_rows[0:ROW_TILES, :], in_=fc2_base_b.rearrange("(m q) -> m q", q=P))
+            bw_nat = keep.tile([P, ROW_TILES * HIDDEN], BF16)
+            nc.sync.dma_start(
+                out=bw_nat[:].rearrange("q (m j) -> q m j", m=ROW_TILES),
+                in_=fc2_base_w.rearrange("(m q) j -> q m j", q=P),
             )
-            nc.scalar.activation(
-                out=silu_grouped[ch][:].rearrange("p (n h u) -> p n h u", h=HALVES, u=2)[:, n_cols, :, :],
-                in_=hidden[ch][:].rearrange("p (h n u) -> p n h u", h=HALVES, u=2)[:, n_cols, :, :],
-                func=ACT.Silu,
-            )
-
-        shifted = {}
-
-        def shift(ch):
-            shifted[ch] = ring.tile([P, 4 * CHUNK], F32, name="shifted", bufs=2)
-            nc.vector.tensor_scalar_add(out=shifted[ch][:], in0=hidden[ch][:], scalar1=-SPACING)
-
-        permute_hidden(0)
-        for unit in range(UNITS):
-            if unit + 1 < UNITS:
-                permute_hidden(unit + 1)
-            turn_hidden(unit)
-        shift(0)
-
-        bias_turned = turned.tile([P, P], BF16, tag="turned")
-        nc.tensor.transpose(bias_turned[:], bias_rows[:], ident_bf16[:])
-        bias_sb = keep.tile([P, ROW_TILES], F32)
-        nc.vector.tensor_copy(out=bias_sb[:], in_=bias_turned[:, 0:ROW_TILES])
-
-        w_codes = keep.tile([P, ROW_TILES * PASSES * P], U32, align_bytes=64)
-        w_scales = keep.tile([P, ROW_TILES * PASSES * P], U8, align_bytes=64)
-
-        def regroup(grouped, first_word, bank):
-            nc.vector.tensor_copy(
-                out=grouped[:]
-                .bitcast(F32)[:, first_word : first_word + CHUNK]
-                .rearrange("p (a q s) -> p a q s", a=2, s=2),
-                in_=bank[:].rearrange("p (a s q) -> p a q s", a=2, s=2),
-            )
-
-        bw_perm = ring.tile([P, WORD_GROUPS * P], F32, tag="perm", bufs=2)
-        nc.vector.tensor_copy(out=partition_order(bw_perm[:]), in_=unit_order(bw_nat[:].bitcast(F32)))
-        bw_banks = [turn(bw_perm, range(4 * m_pair, 4 * m_pair + 4)) for m_pair in range(2)]
-        silu_codes = keep.tile([P, COLS], U32, align_bytes=64)
-        silu_scales = keep.tile([P, COLS], U8, align_bytes=64)
-        for ch in range(CHUNKS):
-            n_cols = slice(ch * CHUNK, (ch + 1) * CHUNK)
-            nc.vector.quantize_mx(
-                out=silu_codes[:, n_cols].bitcast(FP8X4), scales=silu_scales[:, n_cols], in_=silu_grouped[ch][:]
-            )
-        bw_grouped = ring.tile([P, ROW_TILES * 4 * P], BF16, align_bytes=64, tag="grouped")
-        for m_pair in range(2):
-            regroup(bw_grouped, m_pair * CHUNK, bw_banks[m_pair])
-
-        for m in range(ROW_TILES):
-            w_cols = slice((m * PASSES + BASE_PASS) * P, (m * PASSES + BASE_PASS + 1) * P)
-            nc.vector.quantize_mx(
-                out=w_codes[:, w_cols].bitcast(FP8X4),
-                scales=w_scales[:, w_cols],
-                in_=bw_grouped[:, m * 4 * P : (m + 1) * 4 * P],
-            )
-
-        w_banks = {}
-
-        def turn_weights(job):
-            half, m = divmod(job, ROW_TILES)
-            w_perm = ring.tile([P, WORD_GROUPS * P], F32, tag="perm", bufs=2)
-            nc.vector.tensor_copy(
-                out=partition_order(w_perm[:]),
-                in_=w_nat[m][:]
-                .bitcast(F32)[:, half * WORD_GROUPS * P : (half + 1) * WORD_GROUPS * P]
-                .rearrange("q (a c x g) -> q g c a x", a=16, c=4, x=2, g=WORD_GROUPS),
-            )
-            w_banks[job] = [
-                turn(w_perm, [4 * u + pi0 + a for a in range(2) for u in range(2)]) for pi0 in range(0, PAIRS, 2)
-            ]
-
-        def pack_weights(job):
-            half, m = divmod(job, ROW_TILES)
-            w_grouped = ring.tile([P, PAIRS * 4 * P], BF16, align_bytes=64, tag="grouped")
-            for place, bank in enumerate(w_banks[job]):
-                regroup(w_grouped, place * CHUNK, bank)
-            if job + 1 < JOBS:
-                turn_weights(job + 1)
-            w_cols = slice((m * PASSES + half * PAIRS) * P, (m * PASSES + (half + 1) * PAIRS) * P)
-            nc.vector.quantize_mx(out=w_codes[:, w_cols].bitcast(FP8X4), scales=w_scales[:, w_cols], in_=w_grouped[:])
-
-        square = {}
-        basis = {}
-        rest = {}
-        codes = {}
-        scales = {}
-        acc = {}
-
-        def squares(step):
-            ch, k_pass = divmod(step, SPLINE_PASSES)
-            half, pi = divmod(k_pass, PAIRS)
-            centre = -1.0 + 2 * pi * SPACING
-            x_cols = slice(half * 2 * CHUNK, (half + 1) * 2 * CHUNK)
-            square[step] = ring.tile([P, 4 * CHUNK], F32, name="square", bufs=AHEAD + 1)
-            if (k_pass % SHARE == TURN) != (ch == 0):
-                for e in range(2):
-                    nc.scalar.activation(
-                        out=square[step][:, e * 2 * CHUNK : (e + 1) * 2 * CHUNK],
-                        in_=hidden[ch][:, x_cols],
-                        func=ACT.Square,
-                        bias=-(centre + e * SPACING),
-                        scale=1.0,
-                    )
-                rest[step] = 0.0
-            else:
-                for e, source in enumerate((hidden[ch], shifted[ch])):
-                    nc.vector.scalar_tensor_tensor(
-                        out=square[step][:, e * 2 * CHUNK : (e + 1) * 2 * CHUNK],
-                        in0=source[:, x_cols],
-                        scalar=2.0 * centre,
-                        in1=source[:, x_cols],
-                        op0=ALU.subtract,
-                        op1=ALU.mult,
-                    )
-                rest[step] = centre * centre
-
-        def exponentials(step):
-            basis[step] = ring.tile([P, 4 * CHUNK], BF16, align_bytes=64, name="basis", bufs=4)
-            nc.scalar.activation(
-                out=basis[step][:].rearrange("p (x e) -> p x e", e=2),
-                in_=square[step][:].rearrange("p (e x) -> p x e", e=2),
-                func=ACT.Exp,
-                bias=-rest[step] / (SPACING * SPACING),
-                scale=-1.0 / (SPACING * SPACING),
-            )
-
-        def quantise(step):
-            codes[step] = ring.tile([P, CHUNK], U32, align_bytes=64, name="codes", bufs=CODE_BUFS)
-            scales[step] = ring.tile([P, CHUNK], U8, align_bytes=64, name="scales", bufs=CODE_BUFS)
-            nc.vector.quantize_mx(out=codes[step][:].bitcast(FP8X4), scales=scales[step][:], in_=basis[step][:])
-
-        def one_pass(ch, k_pass, rhs, rhs_scale):
+            w_nat = []
             for m in range(ROW_TILES):
-                w_cols = slice((m * PASSES + k_pass) * P, (m * PASSES + k_pass + 1) * P)
-                nc.tensor.matmul_mx(
-                    out=acc[ch][m][:],
-                    lhsT=w_codes[:, w_cols].bitcast(FP8X4),
-                    lhsT_scale=w_scales[:, w_cols],
-                    rhs=rhs.bitcast(FP8X4),
-                    rhs_scale=rhs_scale,
-                    start=(k_pass == BASE_PASS),
-                    stop=(k_pass == SPLINE_PASSES - 1),
+                w_tile = keep.tile([P, HIDDEN * CENTRES], BF16, name="w_nat%d" % m)
+                nc.sync.dma_start(out=w_tile[:], in_=fc2_spline_w[m * P : (m + 1) * P, :])
+                w_nat.append(w_tile)
+            x_sb = keep.tile([P, ROW_TILES * COLS], BF16)
+            for m in range(ROW_TILES):
+                nc.sync.dma_start(
+                    out=x_sb[:, m * COLS : (m + 1) * COLS].rearrange("q (b c) -> q b c", b=BATCH),
+                    in_=x[:, m * P : (m + 1) * P, :].rearrange("b q c -> q b c"),
                 )
 
-        def multiply(step):
-            ch, k_pass = divmod(step, SPLINE_PASSES)
-            if k_pass == 0:
-                acc[ch] = [sums.tile([P, CHUNK], F32, name="acc%d" % m) for m in range(ROW_TILES)]
+            ident_f32 = keep.tile([P, P], F32)
+            make_identity(nc, ident_f32[:])
+            ident_bf16 = keep.tile([P, P], BF16)
+            make_identity(nc, ident_bf16[:])
+
+            warm_in = keep.tile([P, 1], F32)
+            nc.vector.memset(warm_in[:], 0.0)
+            warm_out = keep.tile([P, 1], F32)
+            nc.scalar.activation(out=warm_out[:], in_=warm_in[:], func=ACT.Silu)
+
+            def turn(words, groups):
+                bank = turned.tile([P, CHUNK], F32, tag="turned", name="bank")
+                for place, g in enumerate(groups):
+                    nc.tensor.transpose(
+                        bank[:, place * P : (place + 1) * P], words[:, g * P : (g + 1) * P], ident_f32[:]
+                    )
+                return bank
+
+            h_perm = {}
+            hidden = []
+            silu_grouped = []
+
+            def permute_hidden(unit):
+                h_perm[unit] = ring.tile([P, 4 * P], F32, name="h_perm", bufs=2)
+                nc.vector.tensor_copy(out=partition_order(h_perm[unit][:]), in_=unit_order(h_nat[unit][:].bitcast(F32)))
+
+            def turn_hidden(unit):
+                ch, part = divmod(unit, UNITS_PER_CHUNK)
+                if part == 0:
+                    hidden.append(keep.tile([P, 4 * CHUNK], BF16, name="hidden%d" % ch))
+                    silu_grouped.append(
+                        ring.tile([P, 4 * CHUNK], BF16, align_bytes=64, tag="grouped", name="silu_grouped")
+                    )
+                n_cols = slice(part * UNIT_COLS, (part + 1) * UNIT_COLS)
+                bank = turn(h_perm[unit], [2 * t + half for half in range(HALVES) for t in range(2)])
+                nc.vector.tensor_copy(
+                    out=hidden[ch][:].bitcast(F32).rearrange("p (h n) -> p h n", h=HALVES)[:, :, n_cols],
+                    in_=bank[:].rearrange("p (h n) -> p h n", h=HALVES),
+                )
+                nc.scalar.activation(
+                    out=silu_grouped[ch][:].rearrange("p (n h u) -> p n h u", h=HALVES, u=2)[:, n_cols, :, :],
+                    in_=hidden[ch][:].rearrange("p (h n u) -> p n h u", h=HALVES, u=2)[:, n_cols, :, :],
+                    func=ACT.Silu,
+                )
+
+            shifted = {}
+
+            def shift(ch):
+                shifted[ch] = ring.tile([P, 4 * CHUNK], F32, name="shifted", bufs=2)
+                nc.vector.tensor_scalar_add(out=shifted[ch][:], in0=hidden[ch][:], scalar1=-SPACING)
+
+            permute_hidden(0)
+            for unit in range(UNITS):
+                if unit + 1 < UNITS:
+                    permute_hidden(unit + 1)
+                turn_hidden(unit)
+            shift(0)
+
+            bias_turned = turned.tile([P, P], BF16, tag="turned")
+            nc.tensor.transpose(bias_turned[:], bias_rows[:], ident_bf16[:])
+            bias_sb = keep.tile([P, ROW_TILES], F32)
+            nc.vector.tensor_copy(out=bias_sb[:], in_=bias_turned[:, 0:ROW_TILES])
+
+            w_codes = keep.tile([P, ROW_TILES * PASSES * P], U32, align_bytes=64)
+            w_scales = keep.tile([P, ROW_TILES * PASSES * P], U8, align_bytes=64)
+
+            def regroup(grouped, first_word, bank):
+                nc.vector.tensor_copy(
+                    out=grouped[:]
+                    .bitcast(F32)[:, first_word : first_word + CHUNK]
+                    .rearrange("p (a q s) -> p a q s", a=2, s=2),
+                    in_=bank[:].rearrange("p (a s q) -> p a q s", a=2, s=2),
+                )
+
+            bw_perm = ring.tile([P, WORD_GROUPS * P], F32, tag="perm", bufs=2)
+            nc.vector.tensor_copy(out=partition_order(bw_perm[:]), in_=unit_order(bw_nat[:].bitcast(F32)))
+            bw_banks = [turn(bw_perm, range(4 * m_pair, 4 * m_pair + 4)) for m_pair in range(2)]
+            silu_codes = keep.tile([P, COLS], U32, align_bytes=64)
+            silu_scales = keep.tile([P, COLS], U8, align_bytes=64)
+            for ch in range(CHUNKS):
                 n_cols = slice(ch * CHUNK, (ch + 1) * CHUNK)
-                one_pass(ch, BASE_PASS, silu_codes[:, n_cols], silu_scales[:, n_cols])
-            one_pass(ch, k_pass, codes[step][:], scales[step][:])
-
-        def finish(ch):
-            for m in range(ROW_TILES):
-                result = ring.tile([P, CHUNK], F32, bufs=ROW_TILES)
-                nc.vector.scalar_tensor_tensor(
-                    out=result[:],
-                    in0=acc[ch][m][:],
-                    scalar=bias_sb[:, m : m + 1],
-                    in1=x_sb[:, m * COLS + ch * CHUNK : m * COLS + (ch + 1) * CHUNK],
-                    op0=ALU.add,
-                    op1=ALU.add,
+                nc.vector.quantize_mx(
+                    out=silu_codes[:, n_cols].bitcast(FP8X4), scales=silu_scales[:, n_cols], in_=silu_grouped[ch][:]
                 )
-                for first in range(0, CHUNK, STORE_COLS):
-                    b, c0 = divmod(ch * CHUNK + first, CHANNELS)
-                    nc.sync.dma_start(
-                        out=out[b, m * P : (m + 1) * P, c0 : c0 + STORE_COLS], in_=result[:, first : first + STORE_COLS]
+            bw_grouped = ring.tile([P, ROW_TILES * 4 * P], BF16, align_bytes=64, tag="grouped")
+            for m_pair in range(2):
+                regroup(bw_grouped, m_pair * CHUNK, bw_banks[m_pair])
+
+            for m in range(ROW_TILES):
+                w_cols = slice((m * PASSES + BASE_PASS) * P, (m * PASSES + BASE_PASS + 1) * P)
+                nc.vector.quantize_mx(
+                    out=w_codes[:, w_cols].bitcast(FP8X4),
+                    scales=w_scales[:, w_cols],
+                    in_=bw_grouped[:, m * 4 * P : (m + 1) * 4 * P],
+                )
+
+            w_banks = {}
+
+            def turn_weights(job):
+                half, m = divmod(job, ROW_TILES)
+                w_perm = ring.tile([P, WORD_GROUPS * P], F32, tag="perm", bufs=2)
+                nc.vector.tensor_copy(
+                    out=partition_order(w_perm[:]),
+                    in_=w_nat[m][:]
+                    .bitcast(F32)[:, half * WORD_GROUPS * P : (half + 1) * WORD_GROUPS * P]
+                    .rearrange("q (a c x g) -> q g c a x", a=16, c=4, x=2, g=WORD_GROUPS),
+                )
+                w_banks[job] = [
+                    turn(w_perm, [4 * u + pi0 + a for a in range(2) for u in range(2)]) for pi0 in range(0, PAIRS, 2)
+                ]
+
+            def pack_weights(job):
+                half, m = divmod(job, ROW_TILES)
+                w_grouped = ring.tile([P, PAIRS * 4 * P], BF16, align_bytes=64, tag="grouped")
+                for place, bank in enumerate(w_banks[job]):
+                    regroup(w_grouped, place * CHUNK, bank)
+                if job + 1 < JOBS:
+                    turn_weights(job + 1)
+                w_cols = slice((m * PASSES + half * PAIRS) * P, (m * PASSES + (half + 1) * PAIRS) * P)
+                nc.vector.quantize_mx(out=w_codes[:, w_cols].bitcast(FP8X4), scales=w_scales[:, w_cols], in_=w_grouped[:])
+
+            square = {}
+            basis = {}
+            rest = {}
+            codes = {}
+            scales = {}
+            acc = {}
+
+            def squares(step):
+                ch, k_pass = divmod(step, SPLINE_PASSES)
+                half, pi = divmod(k_pass, PAIRS)
+                centre = -1.0 + 2 * pi * SPACING
+                x_cols = slice(half * 2 * CHUNK, (half + 1) * 2 * CHUNK)
+                square[step] = ring.tile([P, 4 * CHUNK], F32, name="square", bufs=AHEAD + 1)
+                if (k_pass % SHARE == TURN) != (ch == 0):
+                    for e in range(2):
+                        nc.scalar.activation(
+                            out=square[step][:, e * 2 * CHUNK : (e + 1) * 2 * CHUNK],
+                            in_=hidden[ch][:, x_cols],
+                            func=ACT.Square,
+                            bias=-(centre + e * SPACING),
+                            scale=1.0,
+                        )
+                    rest[step] = 0.0
+                else:
+                    for e, source in enumerate((hidden[ch], shifted[ch])):
+                        nc.vector.scalar_tensor_tensor(
+                            out=square[step][:, e * 2 * CHUNK : (e + 1) * 2 * CHUNK],
+                            in0=source[:, x_cols],
+                            scalar=2.0 * centre,
+                            in1=source[:, x_cols],
+                            op0=ALU.subtract,
+                            op1=ALU.mult,
+                        )
+                    rest[step] = centre * centre
+
+            def exponentials(step):
+                basis[step] = ring.tile([P, 4 * CHUNK], BF16, align_bytes=64, name="basis", bufs=4)
+                nc.scalar.activation(
+                    out=basis[step][:].rearrange("p (x e) -> p x e", e=2),
+                    in_=square[step][:].rearrange("p (e x) -> p x e", e=2),
+                    func=ACT.Exp,
+                    bias=-rest[step] / (SPACING * SPACING),
+                    scale=-1.0 / (SPACING * SPACING),
+                )
+
+            def quantise(step):
+                codes[step] = ring.tile([P, CHUNK], U32, align_bytes=64, name="codes", bufs=CODE_BUFS)
+                scales[step] = ring.tile([P, CHUNK], U8, align_bytes=64, name="scales", bufs=CODE_BUFS)
+                nc.vector.quantize_mx(out=codes[step][:].bitcast(FP8X4), scales=scales[step][:], in_=basis[step][:])
+
+            def one_pass(ch, k_pass, rhs, rhs_scale):
+                for m in range(ROW_TILES):
+                    w_cols = slice((m * PASSES + k_pass) * P, (m * PASSES + k_pass + 1) * P)
+                    nc.tensor.matmul_mx(
+                        out=acc[ch][m][:],
+                        lhsT=w_codes[:, w_cols].bitcast(FP8X4),
+                        lhsT_scale=w_scales[:, w_cols],
+                        rhs=rhs.bitcast(FP8X4),
+                        rhs_scale=rhs_scale,
+                        start=(k_pass == BASE_PASS),
+                        stop=(k_pass == SPLINE_PASSES - 1),
                     )
 
-        turn_weights(0)
-        for step in range(AHEAD):
-            squares(step)
-        for step in range(STEPS):
+            def multiply(step):
+                ch, k_pass = divmod(step, SPLINE_PASSES)
+                if k_pass == 0:
+                    acc[ch] = [sum_pools[ch % 2].tile([P, CHUNK], F32, name="acc%d" % m) for m in range(ROW_TILES)]
+                    n_cols = slice(ch * CHUNK, (ch + 1) * CHUNK)
+                    one_pass(ch, BASE_PASS, silu_codes[:, n_cols], silu_scales[:, n_cols])
+                one_pass(ch, k_pass, codes[step][:], scales[step][:])
+
+            def finish(ch):
+                for m in range(ROW_TILES):
+                    result = ring.tile([P, CHUNK], F32, bufs=ROW_TILES)
+                    nc.vector.scalar_tensor_tensor(
+                        out=result[:],
+                        in0=acc[ch][m][:],
+                        scalar=bias_sb[:, m : m + 1],
+                        in1=x_sb[:, m * COLS + ch * CHUNK : m * COLS + (ch + 1) * CHUNK],
+                        op0=ALU.add,
+                        op1=ALU.add,
+                    )
+                    for first in range(0, CHUNK, STORE_COLS):
+                        b, c0 = divmod(ch * CHUNK + first, CHANNELS)
+                        nc.sync.dma_start(
+                            out=out[b, m * P : (m + 1) * P, c0 : c0 + STORE_COLS], in_=result[:, first : first + STORE_COLS]
+                        )
+
+            turn_weights(0)
+            for step in range(AHEAD):
+                squares(step)
+            for step in range(SPLINE_PASSES):
+                exponentials(step)
+                pack_weights(step)
+                if step == SHIFT_AFTER:
+                    shift(1)
+                squares(step + AHEAD)
+                quantise(step)
+                if step >= ROW_TILES:
+                    multiply(step - ROW_TILES)
+
+        sum_pools.append(stack.enter_context(tc.psum_pool(name="sums_odd", bufs=1)))
+        for step in range(SPLINE_PASSES - ROW_TILES, SPLINE_PASSES):
+            multiply(step)
+
+        for step in range(SPLINE_PASSES, STEPS):
             ch, k_pass = divmod(step, SPLINE_PASSES)
             exponentials(step)
-            if ch == 0:
-                pack_weights(k_pass)
-            if k_pass == MID_CHUNK and ch + 1 < CHUNKS:
+            if k_pass == SHIFT_AFTER and ch + 1 < CHUNKS:
                 shift(ch + 1)
             if step + AHEAD < STEPS:
                 squares(step + AHEAD)
             quantise(step)
-            if ch == 0:
-                if k_pass >= ROW_TILES:
-                    multiply(step - ROW_TILES)
-            else:
-                if step == SPLINE_PASSES:
-                    for late in range(SPLINE_PASSES - ROW_TILES, SPLINE_PASSES):
-                        multiply(late)
-                multiply(step)
-            if k_pass == MID_CHUNK and ch > 0:
+            multiply(step)
+            if k_pass == FINISH_AFTER:
                 finish(ch - 1)
         finish(CHUNKS - 1)

@@ -12,6 +12,7 @@ ACT = mybir.ActivationFunctionType
 ALU = mybir.AluOpType
 
 P = 128
+PACK = 4
 BATCH, CHANNELS, HIDDEN, ROWS, CENTRES = 2, 768, 512, 512, 8
 COLS = BATCH * CHANNELS
 CHUNK = 512
@@ -25,29 +26,34 @@ SPLINE_PASSES = HALVES * PAIRS
 BASE_PASS = SPLINE_PASSES
 PASSES = SPLINE_PASSES + 1
 STEPS = CHUNKS * SPLINE_PASSES
+PER_CENTRE = CHUNK * PACK // 2
 WORD_GROUPS = 8
+SLAB_COLS = 256
+SLABS = COLS // SLAB_COLS
+SLABS_PER_CHUNK = CHUNK // SLAB_COLS
+JOBS = HALVES * ROW_TILES
 AHEAD = 3
+FIRST_SHARE = 8
 SHARE = 4
 TURN = 1
-UNIT_COLS = 256
-UNITS = COLS // UNIT_COLS
-UNITS_PER_CHUNK = CHUNK // UNIT_COLS
-JOBS = HALVES * ROW_TILES
+BASIS_BUFS = 4
 CODE_BUFS = 10
 SHIFT_AFTER = 3
 FINISH_AFTER = 2
 
 assert JOBS == SPLINE_PASSES
+assert SHIFT_AFTER < SPLINE_PASSES - AHEAD
+assert (FINISH_AFTER + AHEAD) % SHARE == TURN
 
 FLOPS = 2 * COLS * ROWS * (HIDDEN * CENTRES + HIDDEN)
 
 
 def unit_order(words):
-    return words.rearrange("r (g a c x) -> r g c a x", a=16, c=4, x=2)
+    return words.rearrange("row (g a c r) -> row g c a r", a=16, c=4, r=2)
 
 
 def partition_order(words):
-    return words.rearrange("r (g c a x) -> r g c a x", c=4, a=16, x=2)
+    return words.rearrange("row (g c a r) -> row g c a r", c=4, a=16, r=2)
 
 
 def tile_kan1_pb_kernel(tc, h_mix, x, fc2_spline_w, fc2_base_w, fc2_base_b, out):
@@ -63,11 +69,11 @@ def tile_kan1_pb_kernel(tc, h_mix, x, fc2_spline_w, fc2_base_w, fc2_base_b, out)
             nc.vector.memset(bias_rows[:], 0.0)
             h_rows = h_mix.flatten_outer_dims()
             h_nat = []
-            for unit in range(UNITS):
-                h_tile = keep.tile([P, 2 * HIDDEN], BF16, name="h_nat%d" % unit)
+            for slab in range(SLABS):
+                h_tile = keep.tile([P, 2 * HIDDEN], BF16, name="h_nat%d" % slab)
                 nc.sync.dma_start(
-                    out=h_tile[:].rearrange("r (t j) -> r t j", t=2),
-                    in_=h_rows[unit * UNIT_COLS : (unit + 1) * UNIT_COLS, :].rearrange("(t r) j -> r t j", r=P),
+                    out=h_tile[:].rearrange("row (t j) -> row t j", t=2),
+                    in_=h_rows[slab * SLAB_COLS : (slab + 1) * SLAB_COLS, :].rearrange("(t row) j -> row t j", row=P),
                 )
                 h_nat.append(h_tile)
             nc.sync.dma_start(out=bias_rows[0:ROW_TILES, :], in_=fc2_base_b.rearrange("(m q) -> m q", q=P))
@@ -110,19 +116,19 @@ def tile_kan1_pb_kernel(tc, h_mix, x, fc2_spline_w, fc2_base_w, fc2_base_b, out)
             hidden = []
             silu_grouped = []
 
-            def permute_hidden(unit):
-                h_perm[unit] = ring.tile([P, 4 * P], F32, name="h_perm", bufs=2)
-                nc.vector.tensor_copy(out=partition_order(h_perm[unit][:]), in_=unit_order(h_nat[unit][:].bitcast(F32)))
+            def permute_hidden(slab):
+                h_perm[slab] = ring.tile([P, 4 * P], F32, name="h_perm", bufs=2)
+                nc.vector.tensor_copy(out=partition_order(h_perm[slab][:]), in_=unit_order(h_nat[slab][:].bitcast(F32)))
 
-            def turn_hidden(unit):
-                ch, part = divmod(unit, UNITS_PER_CHUNK)
+            def turn_hidden(slab):
+                ch, part = divmod(slab, SLABS_PER_CHUNK)
                 if part == 0:
-                    hidden.append(keep.tile([P, 4 * CHUNK], BF16, name="hidden%d" % ch))
+                    hidden.append(keep.tile([P, PACK * CHUNK], BF16, name="hidden%d" % ch))
                     silu_grouped.append(
-                        ring.tile([P, 4 * CHUNK], BF16, align_bytes=64, tag="grouped", name="silu_grouped")
+                        ring.tile([P, PACK * CHUNK], BF16, align_bytes=64, tag="grouped", name="silu_grouped")
                     )
-                n_cols = slice(part * UNIT_COLS, (part + 1) * UNIT_COLS)
-                bank = turn(h_perm[unit], [2 * t + half for half in range(HALVES) for t in range(2)])
+                n_cols = slice(part * SLAB_COLS, (part + 1) * SLAB_COLS)
+                bank = turn(h_perm[slab], [2 * t + half for half in range(HALVES) for t in range(2)])
                 nc.vector.tensor_copy(
                     out=hidden[ch][:].bitcast(F32).rearrange("p (h n) -> p h n", h=HALVES)[:, :, n_cols],
                     in_=bank[:].rearrange("p (h n) -> p h n", h=HALVES),
@@ -136,14 +142,14 @@ def tile_kan1_pb_kernel(tc, h_mix, x, fc2_spline_w, fc2_base_w, fc2_base_b, out)
             shifted = {}
 
             def shift(ch):
-                shifted[ch] = ring.tile([P, 4 * CHUNK], F32, name="shifted", bufs=2)
+                shifted[ch] = ring.tile([P, PACK * CHUNK], F32, name="shifted", bufs=2)
                 nc.vector.tensor_scalar_add(out=shifted[ch][:], in0=hidden[ch][:], scalar1=-SPACING)
 
             permute_hidden(0)
-            for unit in range(UNITS):
-                if unit + 1 < UNITS:
-                    permute_hidden(unit + 1)
-                turn_hidden(unit)
+            for slab in range(SLABS):
+                if slab + 1 < SLABS:
+                    permute_hidden(slab + 1)
+                turn_hidden(slab)
             shift(0)
 
             bias_turned = turned.tile([P, P], BF16, tag="turned")
@@ -172,7 +178,7 @@ def tile_kan1_pb_kernel(tc, h_mix, x, fc2_spline_w, fc2_base_w, fc2_base_b, out)
                 nc.vector.quantize_mx(
                     out=silu_codes[:, n_cols].bitcast(FP8X4), scales=silu_scales[:, n_cols], in_=silu_grouped[ch][:]
                 )
-            bw_grouped = ring.tile([P, ROW_TILES * 4 * P], BF16, align_bytes=64, tag="grouped")
+            bw_grouped = ring.tile([P, ROW_TILES * PACK * P], BF16, align_bytes=64, tag="grouped")
             for m_pair in range(2):
                 regroup(bw_grouped, m_pair * CHUNK, bw_banks[m_pair])
 
@@ -181,7 +187,7 @@ def tile_kan1_pb_kernel(tc, h_mix, x, fc2_spline_w, fc2_base_w, fc2_base_b, out)
                 nc.vector.quantize_mx(
                     out=w_codes[:, w_cols].bitcast(FP8X4),
                     scales=w_scales[:, w_cols],
-                    in_=bw_grouped[:, m * 4 * P : (m + 1) * 4 * P],
+                    in_=bw_grouped[:, m * PACK * P : (m + 1) * PACK * P],
                 )
 
             w_banks = {}
@@ -193,7 +199,7 @@ def tile_kan1_pb_kernel(tc, h_mix, x, fc2_spline_w, fc2_base_w, fc2_base_b, out)
                     out=partition_order(w_perm[:]),
                     in_=w_nat[m][:]
                     .bitcast(F32)[:, half * WORD_GROUPS * P : (half + 1) * WORD_GROUPS * P]
-                    .rearrange("q (a c x g) -> q g c a x", a=16, c=4, x=2, g=WORD_GROUPS),
+                    .rearrange("q (a c r g) -> q g c a r", a=16, c=4, r=2, g=WORD_GROUPS),
                 )
                 w_banks[job] = [
                     turn(w_perm, [4 * u + pi0 + a for a in range(2) for u in range(2)]) for pi0 in range(0, PAIRS, 2)
@@ -201,13 +207,15 @@ def tile_kan1_pb_kernel(tc, h_mix, x, fc2_spline_w, fc2_base_w, fc2_base_b, out)
 
             def pack_weights(job):
                 half, m = divmod(job, ROW_TILES)
-                w_grouped = ring.tile([P, PAIRS * 4 * P], BF16, align_bytes=64, tag="grouped")
+                w_grouped = ring.tile([P, PAIRS * PACK * P], BF16, align_bytes=64, tag="grouped")
                 for place, bank in enumerate(w_banks[job]):
                     regroup(w_grouped, place * CHUNK, bank)
                 if job + 1 < JOBS:
                     turn_weights(job + 1)
                 w_cols = slice((m * PASSES + half * PAIRS) * P, (m * PASSES + (half + 1) * PAIRS) * P)
-                nc.vector.quantize_mx(out=w_codes[:, w_cols].bitcast(FP8X4), scales=w_scales[:, w_cols], in_=w_grouped[:])
+                nc.vector.quantize_mx(
+                    out=w_codes[:, w_cols].bitcast(FP8X4), scales=w_scales[:, w_cols], in_=w_grouped[:]
+                )
 
             square = {}
             basis = {}
@@ -220,13 +228,13 @@ def tile_kan1_pb_kernel(tc, h_mix, x, fc2_spline_w, fc2_base_w, fc2_base_b, out)
                 ch, k_pass = divmod(step, SPLINE_PASSES)
                 half, pi = divmod(k_pass, PAIRS)
                 centre = -1.0 + 2 * pi * SPACING
-                x_cols = slice(half * 2 * CHUNK, (half + 1) * 2 * CHUNK)
-                square[step] = ring.tile([P, 4 * CHUNK], F32, name="square", bufs=AHEAD + 1)
-                if (k_pass % SHARE == TURN) != (ch == 0):
+                v_cols = slice(half * PER_CENTRE, (half + 1) * PER_CENTRE)
+                square[step] = ring.tile([P, PACK * CHUNK], F32, name="square", bufs=AHEAD + 1)
+                if (k_pass % FIRST_SHARE != TURN) if ch == 0 else (k_pass % SHARE == TURN):
                     for e in range(2):
                         nc.scalar.activation(
-                            out=square[step][:, e * 2 * CHUNK : (e + 1) * 2 * CHUNK],
-                            in_=hidden[ch][:, x_cols],
+                            out=square[step][:, e * PER_CENTRE : (e + 1) * PER_CENTRE],
+                            in_=hidden[ch][:, v_cols],
                             func=ACT.Square,
                             bias=-(centre + e * SPACING),
                             scale=1.0,
@@ -235,20 +243,20 @@ def tile_kan1_pb_kernel(tc, h_mix, x, fc2_spline_w, fc2_base_w, fc2_base_b, out)
                 else:
                     for e, source in enumerate((hidden[ch], shifted[ch])):
                         nc.vector.scalar_tensor_tensor(
-                            out=square[step][:, e * 2 * CHUNK : (e + 1) * 2 * CHUNK],
-                            in0=source[:, x_cols],
+                            out=square[step][:, e * PER_CENTRE : (e + 1) * PER_CENTRE],
+                            in0=source[:, v_cols],
                             scalar=2.0 * centre,
-                            in1=source[:, x_cols],
+                            in1=source[:, v_cols],
                             op0=ALU.subtract,
                             op1=ALU.mult,
                         )
                     rest[step] = centre * centre
 
             def exponentials(step):
-                basis[step] = ring.tile([P, 4 * CHUNK], BF16, align_bytes=64, name="basis", bufs=4)
+                basis[step] = ring.tile([P, PACK * CHUNK], BF16, align_bytes=64, name="basis", bufs=BASIS_BUFS)
                 nc.scalar.activation(
-                    out=basis[step][:].rearrange("p (x e) -> p x e", e=2),
-                    in_=square[step][:].rearrange("p (e x) -> p x e", e=2),
+                    out=basis[step][:].rearrange("p (v e) -> p v e", e=2),
+                    in_=square[step][:].rearrange("p (e v) -> p v e", e=2),
                     func=ACT.Exp,
                     bias=-rest[step] / (SPACING * SPACING),
                     scale=-1.0 / (SPACING * SPACING),
@@ -294,7 +302,8 @@ def tile_kan1_pb_kernel(tc, h_mix, x, fc2_spline_w, fc2_base_w, fc2_base_b, out)
                     for first in range(0, CHUNK, STORE_COLS):
                         b, c0 = divmod(ch * CHUNK + first, CHANNELS)
                         nc.sync.dma_start(
-                            out=out[b, m * P : (m + 1) * P, c0 : c0 + STORE_COLS], in_=result[:, first : first + STORE_COLS]
+                            out=out[b, m * P : (m + 1) * P, c0 : c0 + STORE_COLS],
+                            in_=result[:, first : first + STORE_COLS],
                         )
 
             turn_weights(0)

@@ -33,7 +33,7 @@ SLABS = COLS // SLAB_COLS
 SLABS_PER_CHUNK = CHUNK // SLAB_COLS
 JOBS = HALVES * ROW_TILES
 AHEAD = 3
-FIRST_SHARE = 8
+FIRST_SHARE = 4
 SHARE = 4
 TURN = 1
 BASIS_BUFS = 4
@@ -49,11 +49,11 @@ FLOPS = 2 * COLS * ROWS * (HIDDEN * CENTRES + HIDDEN)
 
 
 def unit_order(words):
-    return words.rearrange("row (g a c r) -> row g c a r", a=16, c=4, r=2)
+    return words.rearrange("row (g a c r) -> row g c a r", a=32, c=4, r=2)
 
 
 def partition_order(words):
-    return words.rearrange("row (g c a r) -> row g c a r", c=4, a=16, r=2)
+    return words.rearrange("row (g c a r) -> row g c a r", c=4, a=32, r=2)
 
 
 def tile_kan1_pb_kernel(tc, h_mix, x, fc2_spline_w, fc2_base_w, fc2_base_b, out):
@@ -83,9 +83,16 @@ def tile_kan1_pb_kernel(tc, h_mix, x, fc2_spline_w, fc2_base_w, fc2_base_b, out)
                 in_=fc2_base_w.rearrange("(m q) j -> q m j", q=P),
             )
             w_nat = []
-            for m in range(ROW_TILES):
-                w_tile = keep.tile([P, HIDDEN * CENTRES], BF16, name="w_nat%d" % m)
-                nc.sync.dma_start(out=w_tile[:], in_=fc2_spline_w[m * P : (m + 1) * P, :])
+            for job in range(JOBS):
+                half, m = divmod(job, ROW_TILES)
+                w_tile = keep.tile([P, HIDDEN * CENTRES // 2], BF16, name="w_nat%d" % job)
+                w_rows = fc2_spline_w[m * P : (m + 1) * P, :].rearrange("q (a c s) -> q c a s", c=4, s=32)
+                w_run = HIDDEN * CENTRES // 4
+                for c in range(2):
+                    nc.sync.dma_start(
+                        out=w_tile[:, c * w_run : (c + 1) * w_run].rearrange("q (a s) -> q a s", s=32),
+                        in_=w_rows[:, 2 * half + c, :, :],
+                    )
                 w_nat.append(w_tile)
             x_sb = keep.tile([P, ROW_TILES * COLS], BF16)
             for m in range(ROW_TILES):
@@ -104,13 +111,14 @@ def tile_kan1_pb_kernel(tc, h_mix, x, fc2_spline_w, fc2_base_w, fc2_base_b, out)
             warm_out = keep.tile([P, 1], F32)
             nc.scalar.activation(out=warm_out[:], in_=warm_in[:], func=ACT.Silu)
 
-            def turn(words, groups):
+            def turn(groups):
                 bank = turned.tile([P, CHUNK], F32, tag="turned", name="bank")
-                for place, g in enumerate(groups):
-                    nc.tensor.transpose(
-                        bank[:, place * P : (place + 1) * P], words[:, g * P : (g + 1) * P], ident_f32[:]
-                    )
+                for place, group in enumerate(groups):
+                    nc.tensor.transpose(bank[:, place * P : (place + 1) * P], group, ident_f32[:])
                 return bank
+
+            def group(words, g):
+                return words[:, g * P : (g + 1) * P]
 
             h_perm = {}
             hidden = []
@@ -128,7 +136,7 @@ def tile_kan1_pb_kernel(tc, h_mix, x, fc2_spline_w, fc2_base_w, fc2_base_b, out)
                         ring.tile([P, PACK * CHUNK], BF16, align_bytes=64, tag="grouped", name="silu_grouped")
                     )
                 n_cols = slice(part * SLAB_COLS, (part + 1) * SLAB_COLS)
-                bank = turn(h_perm[slab], [2 * t + half for half in range(HALVES) for t in range(2)])
+                bank = turn([group(h_perm[slab], 2 * t + half) for half in range(HALVES) for t in range(2)])
                 nc.vector.tensor_copy(
                     out=hidden[ch][:].bitcast(F32).rearrange("p (h n) -> p h n", h=HALVES)[:, :, n_cols],
                     in_=bank[:].rearrange("p (h n) -> p h n", h=HALVES),
@@ -168,9 +176,9 @@ def tile_kan1_pb_kernel(tc, h_mix, x, fc2_spline_w, fc2_base_w, fc2_base_b, out)
                     in_=bank[:].rearrange("p (a s q) -> p a q s", a=2, s=2),
                 )
 
-            bw_perm = ring.tile([P, WORD_GROUPS * P], F32, tag="perm", bufs=2)
+            bw_perm = keep.tile([P, WORD_GROUPS * P], F32)
             nc.vector.tensor_copy(out=partition_order(bw_perm[:]), in_=unit_order(bw_nat[:].bitcast(F32)))
-            bw_banks = [turn(bw_perm, range(4 * m_pair, 4 * m_pair + 4)) for m_pair in range(2)]
+            bw_banks = [turn([group(bw_perm, g) for g in range(4 * m_pair, 4 * m_pair + 4)]) for m_pair in range(2)]
             silu_codes = keep.tile([P, COLS], U32, align_bytes=64)
             silu_scales = keep.tile([P, COLS], U8, align_bytes=64)
             for ch in range(CHUNKS):
@@ -193,16 +201,10 @@ def tile_kan1_pb_kernel(tc, h_mix, x, fc2_spline_w, fc2_base_w, fc2_base_b, out)
             w_banks = {}
 
             def turn_weights(job):
-                half, m = divmod(job, ROW_TILES)
-                w_perm = ring.tile([P, WORD_GROUPS * P], F32, tag="perm", bufs=2)
-                nc.vector.tensor_copy(
-                    out=partition_order(w_perm[:]),
-                    in_=w_nat[m][:]
-                    .bitcast(F32)[:, half * WORD_GROUPS * P : (half + 1) * WORD_GROUPS * P]
-                    .rearrange("q (a c r g) -> q g c a r", a=16, c=4, r=2, g=WORD_GROUPS),
-                )
+                words = w_nat[job][:].bitcast(F32)
                 w_banks[job] = [
-                    turn(w_perm, [4 * u + pi0 + a for a in range(2) for u in range(2)]) for pi0 in range(0, PAIRS, 2)
+                    turn([words[:, 4 * u + pi0 + a : WORD_GROUPS * P : WORD_GROUPS] for a in range(2) for u in range(2)])
+                    for pi0 in range(0, PAIRS, 2)
                 ]
 
             def pack_weights(job):
@@ -252,26 +254,34 @@ def tile_kan1_pb_kernel(tc, h_mix, x, fc2_spline_w, fc2_base_w, fc2_base_b, out)
                         )
                     rest[step] = centre * centre
 
-            def exponentials(step):
+            def make_basis_tiles(step):
                 basis[step] = ring.tile([P, PACK * CHUNK], BF16, align_bytes=64, name="basis", bufs=BASIS_BUFS)
+                codes[step] = ring.tile([P, CHUNK], U32, align_bytes=64, name="codes", bufs=CODE_BUFS)
+                scales[step] = ring.tile([P, CHUNK], U8, align_bytes=64, name="scales", bufs=CODE_BUFS)
+
+            def exponentials(step, first=0, last=CHUNK):
+                if first == 0:
+                    make_basis_tiles(step)
                 nc.scalar.activation(
-                    out=basis[step][:].rearrange("p (v e) -> p v e", e=2),
-                    in_=square[step][:].rearrange("p (e v) -> p v e", e=2),
+                    out=basis[step][:].rearrange("p (v e) -> p v e", e=2)[:, 2 * first : 2 * last, :],
+                    in_=square[step][:].rearrange("p (e v) -> p v e", e=2)[:, 2 * first : 2 * last, :],
                     func=ACT.Exp,
                     bias=-rest[step] / (SPACING * SPACING),
                     scale=-1.0 / (SPACING * SPACING),
                 )
 
-            def quantise(step):
-                codes[step] = ring.tile([P, CHUNK], U32, align_bytes=64, name="codes", bufs=CODE_BUFS)
-                scales[step] = ring.tile([P, CHUNK], U8, align_bytes=64, name="scales", bufs=CODE_BUFS)
-                nc.vector.quantize_mx(out=codes[step][:].bitcast(FP8X4), scales=scales[step][:], in_=basis[step][:])
+            def quantise(step, first=0, last=CHUNK):
+                nc.vector.quantize_mx(
+                    out=codes[step][:, first:last].bitcast(FP8X4),
+                    scales=scales[step][:, first:last],
+                    in_=basis[step][:, PACK * first : PACK * last],
+                )
 
-            def one_pass(ch, k_pass, rhs, rhs_scale):
+            def one_pass(sums, k_pass, rhs, rhs_scale):
                 for m in range(ROW_TILES):
                     w_cols = slice((m * PASSES + k_pass) * P, (m * PASSES + k_pass + 1) * P)
                     nc.tensor.matmul_mx(
-                        out=acc[ch][m][:],
+                        out=sums[m],
                         lhsT=w_codes[:, w_cols].bitcast(FP8X4),
                         lhsT_scale=w_scales[:, w_cols],
                         rhs=rhs.bitcast(FP8X4),
@@ -280,31 +290,36 @@ def tile_kan1_pb_kernel(tc, h_mix, x, fc2_spline_w, fc2_base_w, fc2_base_b, out)
                         stop=(k_pass == SPLINE_PASSES - 1),
                     )
 
-            def multiply(step):
+            def multiply(step, first=0, last=CHUNK):
                 ch, k_pass = divmod(step, SPLINE_PASSES)
+                banks = (ch + (first > 0)) % 2
                 if k_pass == 0:
-                    acc[ch] = [sum_pools[ch % 2].tile([P, CHUNK], F32, name="acc%d" % m) for m in range(ROW_TILES)]
-                    n_cols = slice(ch * CHUNK, (ch + 1) * CHUNK)
-                    one_pass(ch, BASE_PASS, silu_codes[:, n_cols], silu_scales[:, n_cols])
-                one_pass(ch, k_pass, codes[step][:], scales[step][:])
+                    tiles = [sum_pools[banks].tile([P, CHUNK], F32, name="acc%d" % m) for m in range(ROW_TILES)]
+                    acc[ch, first] = [tile[:, 0 : last - first] for tile in tiles]
+                    n_cols = slice(ch * CHUNK + first, ch * CHUNK + last)
+                    one_pass(acc[ch, first], BASE_PASS, silu_codes[:, n_cols], silu_scales[:, n_cols])
+                one_pass(acc[ch, first], k_pass, codes[step][:, first:last], scales[step][:, first:last])
 
-            def finish(ch):
-                for m in range(ROW_TILES):
-                    result = ring.tile([P, CHUNK], F32, bufs=ROW_TILES)
-                    nc.vector.scalar_tensor_tensor(
-                        out=result[:],
-                        in0=acc[ch][m][:],
-                        scalar=bias_sb[:, m : m + 1],
-                        in1=x_sb[:, m * COLS + ch * CHUNK : m * COLS + (ch + 1) * CHUNK],
-                        op0=ALU.add,
-                        op1=ALU.add,
+            results = {}
+
+            def finish(ch, m, first=0, last=CHUNK):
+                if first == 0:
+                    results[ch, m] = ring.tile([P, CHUNK], F32, name="result", bufs=ROW_TILES)
+                result = results[ch, m]
+                nc.vector.scalar_tensor_tensor(
+                    out=result[:, first:last],
+                    in0=acc[ch, first][m],
+                    scalar=bias_sb[:, m : m + 1],
+                    in1=x_sb[:, m * COLS + ch * CHUNK + first : m * COLS + ch * CHUNK + last],
+                    op0=ALU.add,
+                    op1=ALU.add,
+                )
+                for c in range(first, last, STORE_COLS):
+                    b, c0 = divmod(ch * CHUNK + c, CHANNELS)
+                    nc.sync.dma_start(
+                        out=out[b, m * P : (m + 1) * P, c0 : c0 + STORE_COLS],
+                        in_=result[:, c : c + STORE_COLS],
                     )
-                    for first in range(0, CHUNK, STORE_COLS):
-                        b, c0 = divmod(ch * CHUNK + first, CHANNELS)
-                        nc.sync.dma_start(
-                            out=out[b, m * P : (m + 1) * P, c0 : c0 + STORE_COLS],
-                            in_=result[:, first : first + STORE_COLS],
-                        )
 
             turn_weights(0)
             for step in range(AHEAD):
@@ -323,7 +338,8 @@ def tile_kan1_pb_kernel(tc, h_mix, x, fc2_spline_w, fc2_base_w, fc2_base_b, out)
         for step in range(SPLINE_PASSES - ROW_TILES, SPLINE_PASSES):
             multiply(step)
 
-        for step in range(SPLINE_PASSES, STEPS):
+        HALF = CHUNK // 2
+        for step in range(SPLINE_PASSES, STEPS - 1):
             ch, k_pass = divmod(step, SPLINE_PASSES)
             exponentials(step)
             if k_pass == SHIFT_AFTER and ch + 1 < CHUNKS:
@@ -331,7 +347,28 @@ def tile_kan1_pb_kernel(tc, h_mix, x, fc2_spline_w, fc2_base_w, fc2_base_b, out)
             if step + AHEAD < STEPS:
                 squares(step + AHEAD)
             quantise(step)
-            multiply(step)
+            if ch + 1 < CHUNKS:
+                multiply(step)
+            else:
+                multiply(step, 0, HALF)
+                if k_pass > FINISH_AFTER:
+                    multiply(step, HALF, CHUNK)
             if k_pass == FINISH_AFTER:
-                finish(ch - 1)
-        finish(CHUNKS - 1)
+                for m in range(ROW_TILES):
+                    finish(ch - 1, m)
+                if ch + 1 == CHUNKS:
+                    for late in range(step - FINISH_AFTER, step + 1):
+                        multiply(late, HALF, CHUNK)
+
+        exponentials(STEPS - 1, 0, HALF)
+        exponentials(STEPS - 1, HALF, CHUNK)
+        quantise(STEPS - 1, 0, HALF)
+        multiply(STEPS - 1, 0, HALF)
+        for m in range(2):
+            finish(CHUNKS - 1, m, 0, HALF)
+        quantise(STEPS - 1, HALF, CHUNK)
+        multiply(STEPS - 1, HALF, CHUNK)
+        for m in range(2, ROW_TILES):
+            finish(CHUNKS - 1, m, 0, HALF)
+        for m in range(ROW_TILES):
+            finish(CHUNKS - 1, m, HALF, CHUNK)

@@ -31,6 +31,8 @@ WORD_GROUPS = 8
 SLAB_COLS = 256
 SLABS = COLS // SLAB_COLS
 SLABS_PER_CHUNK = CHUNK // SLAB_COLS
+W_JOB = HIDDEN * CENTRES // HALVES
+SORTED_BY_LOAD = 4
 JOBS = HALVES * ROW_TILES
 AHEAD = 3
 FIRST_SHARE = 4
@@ -49,11 +51,11 @@ FLOPS = 2 * COLS * ROWS * (HIDDEN * CENTRES + HIDDEN)
 
 
 def unit_order(words):
-    return words.rearrange("row (g a c r) -> row g c a r", a=32, c=4, r=2)
+    return words.rearrange("row (g a c r) -> row g c a r", a=16, c=4, r=2)
 
 
 def partition_order(words):
-    return words.rearrange("row (g c a r) -> row g c a r", c=4, a=32, r=2)
+    return words.rearrange("row (g c a r) -> row g c a r", c=4, a=16, r=2)
 
 
 def tile_kan1_pb_kernel(tc, h_mix, x, fc2_spline_w, fc2_base_w, fc2_base_b, out):
@@ -85,14 +87,16 @@ def tile_kan1_pb_kernel(tc, h_mix, x, fc2_spline_w, fc2_base_w, fc2_base_b, out)
             w_nat = []
             for job in range(JOBS):
                 half, m = divmod(job, ROW_TILES)
-                w_tile = keep.tile([P, HIDDEN * CENTRES // 2], BF16, name="w_nat%d" % job)
-                w_rows = fc2_spline_w[m * P : (m + 1) * P, :].rearrange("q (a c s) -> q c a s", c=4, s=32)
-                w_run = HIDDEN * CENTRES // 4
-                for c in range(2):
-                    nc.sync.dma_start(
-                        out=w_tile[:, c * w_run : (c + 1) * w_run].rearrange("q (a s) -> q a s", s=32),
-                        in_=w_rows[:, 2 * half + c, :, :],
-                    )
+                w_tile = keep.tile([P, W_JOB], BF16, name="w_nat%d" % job)
+                w_rows = fc2_spline_w[m * P : (m + 1) * P, half * W_JOB : (half + 1) * W_JOB]
+                if job < SORTED_BY_LOAD:
+                    nc.sync.dma_start(out=w_tile[:], in_=w_rows)
+                else:
+                    for c in range(4):
+                        nc.sync.dma_start(
+                            out=w_tile[:].rearrange("q (c a s) -> q c a s", c=4, s=32)[:, c, :, :],
+                            in_=w_rows.rearrange("q (a c s) -> q c a s", c=4, s=32)[:, c, :, :],
+                        )
                 w_nat.append(w_tile)
             x_sb = keep.tile([P, ROW_TILES * COLS], BF16)
             for m in range(ROW_TILES):
@@ -201,7 +205,15 @@ def tile_kan1_pb_kernel(tc, h_mix, x, fc2_spline_w, fc2_base_w, fc2_base_b, out)
             w_banks = {}
 
             def turn_weights(job):
-                words = w_nat[job][:].bitcast(F32)
+                if job < SORTED_BY_LOAD:
+                    w_sorted = ring.tile([P, W_JOB], BF16, tag="perm", bufs=2)
+                    nc.vector.tensor_copy(
+                        out=w_sorted[:].bitcast(F32).rearrange("q (c a s) -> q c a s", c=4, s=16),
+                        in_=w_nat[job][:].bitcast(F32).rearrange("q (a c s) -> q c a s", c=4, s=16),
+                    )
+                else:
+                    w_sorted = w_nat[job]
+                words = w_sorted[:].bitcast(F32)
                 w_banks[job] = [
                     turn([words[:, 4 * u + pi0 + a : WORD_GROUPS * P : WORD_GROUPS] for a in range(2) for u in range(2)])
                     for pi0 in range(0, PAIRS, 2)

@@ -28,20 +28,30 @@ PASSES = SPLINE_PASSES + 1
 STEPS = CHUNKS * SPLINE_PASSES
 PER_CENTRE = CHUNK * PACK // 2
 WORD_GROUPS = 8
-SLAB_COLS = 256
-SLABS = COLS // SLAB_COLS
-SLABS_PER_CHUNK = CHUNK // SLAB_COLS
+SLAB_TILES = (1, 1, 2, 2, 2, 2, 2)
+SQUARE_BANKS = (6, 7)
+SUM_BANKS = 6
+TENSOR_COLS = CHUNK // 4
+TENSOR_HALVES = ((0, 0), (0, 1), (1, 0), (1, 1), (2, 0))
+CLAMP = 16384.0
+HEAD_BANKS = 4
+WEIGHT_BANKS = 4
+EARLY_SLABS = 2
 W_JOB = HIDDEN * CENTRES // HALVES
 SORTED_BY_LOAD = 4
 JOBS = HALVES * ROW_TILES
 AHEAD = 3
-FIRST_SHARE = 4
+FIRST_SHARE = 3
 SHARE = 4
-TURN = 1
+FIRST_TURN = 1
+PASSES_A_STEP = 4
+TURN = 0
 BASIS_BUFS = 4
-CODE_BUFS = 10
+SQUARE_BUFS = AHEAD + 2
+CODE_BUFS = 9
 SHIFT_AFTER = 3
-FINISH_AFTER = 2
+SQUARES_OVER = 3
+FINISH_AFTER = 1
 
 assert JOBS == SPLINE_PASSES
 assert SHIFT_AFTER < SPLINE_PASSES - AHEAD
@@ -64,313 +74,435 @@ def tile_kan1_pb_kernel(tc, h_mix, x, fc2_spline_w, fc2_base_w, fc2_base_b, out)
         stack.enter_context(tc.manual_schedule())
         keep = stack.enter_context(tc.tile_pool(name="keep", bufs=1))
         ring = stack.enter_context(tc.tile_pool(name="ring", bufs=3))
-        sum_pools = [stack.enter_context(tc.psum_pool(name="sums_even", bufs=1))]
+        psum = stack.enter_context(tc.psum_pool(name="psum", bufs=1))
 
-        with tc.psum_pool(name="turned", bufs=4) as turned:
-            bias_rows = keep.tile([P, P], BF16)
-            nc.vector.memset(bias_rows[:], 0.0)
-            h_rows = h_mix.flatten_outer_dims()
-            h_nat = []
-            for slab in range(SLABS):
-                h_tile = keep.tile([P, 2 * HIDDEN], BF16, name="h_nat%d" % slab)
-                nc.sync.dma_start(
-                    out=h_tile[:].rearrange("row (t j) -> row t j", t=2),
-                    in_=h_rows[slab * SLAB_COLS : (slab + 1) * SLAB_COLS, :].rearrange("(t row) j -> row t j", row=P),
-                )
-                h_nat.append(h_tile)
-            nc.sync.dma_start(out=bias_rows[0:ROW_TILES, :], in_=fc2_base_b.rearrange("(m q) -> m q", q=P))
-            bw_nat = keep.tile([P, ROW_TILES * HIDDEN], BF16)
+        def psum_bank(b, dtype=F32, cols=CHUNK):
+            return psum.tile([P, cols], dtype, tag="bank%d" % b, name="bank")
+
+        bias_rows = keep.tile([P, P], BF16)
+        nc.vector.memset(bias_rows[:], 0.0)
+        h_rows = h_mix.flatten_outer_dims()
+        h_nat = []
+        slab_cols = []
+        for slab, tiles in enumerate(SLAB_TILES):
+            n0 = sum(SLAB_TILES[:slab]) * P
+            slab_cols.append((n0, n0 + tiles * P))
+            h_tile = keep.tile([P, tiles * HIDDEN], BF16, name="h_nat%d" % slab)
             nc.sync.dma_start(
-                out=bw_nat[:].rearrange("q (m j) -> q m j", m=ROW_TILES),
-                in_=fc2_base_w.rearrange("(m q) j -> q m j", q=P),
+                out=h_tile[:].rearrange("row (t j) -> row t j", t=tiles),
+                in_=h_rows[n0 : n0 + tiles * P, :].rearrange("(t row) j -> row t j", row=P),
             )
-            w_nat = []
-            for job in range(JOBS):
-                half, m = divmod(job, ROW_TILES)
-                w_tile = keep.tile([P, W_JOB], BF16, name="w_nat%d" % job)
-                w_rows = fc2_spline_w[m * P : (m + 1) * P, half * W_JOB : (half + 1) * W_JOB]
-                if job < SORTED_BY_LOAD:
-                    nc.sync.dma_start(out=w_tile[:], in_=w_rows)
-                else:
-                    for c in range(4):
-                        nc.sync.dma_start(
-                            out=w_tile[:].rearrange("q (c a s) -> q c a s", c=4, s=32)[:, c, :, :],
-                            in_=w_rows.rearrange("q (a c s) -> q c a s", c=4, s=32)[:, c, :, :],
-                        )
-                w_nat.append(w_tile)
-            x_sb = keep.tile([P, ROW_TILES * COLS], BF16)
-            for m in range(ROW_TILES):
-                nc.sync.dma_start(
-                    out=x_sb[:, m * COLS : (m + 1) * COLS].rearrange("q (b c) -> q b c", b=BATCH),
-                    in_=x[:, m * P : (m + 1) * P, :].rearrange("b q c -> q b c"),
-                )
-
-            ident_f32 = keep.tile([P, P], F32)
-            make_identity(nc, ident_f32[:])
-            ident_bf16 = keep.tile([P, P], BF16)
-            make_identity(nc, ident_bf16[:])
-
-            warm_in = keep.tile([P, 1], F32)
-            nc.vector.memset(warm_in[:], 0.0)
-            warm_out = keep.tile([P, 1], F32)
-            nc.scalar.activation(out=warm_out[:], in_=warm_in[:], func=ACT.Silu)
-
-            def turn(groups):
-                bank = turned.tile([P, CHUNK], F32, tag="turned", name="bank")
-                for place, group in enumerate(groups):
-                    nc.tensor.transpose(bank[:, place * P : (place + 1) * P], group, ident_f32[:])
-                return bank
-
-            def group(words, g):
-                return words[:, g * P : (g + 1) * P]
-
-            h_perm = {}
-            hidden = []
-            silu_grouped = []
-
-            def permute_hidden(slab):
-                h_perm[slab] = ring.tile([P, 4 * P], F32, name="h_perm", bufs=2)
-                nc.vector.tensor_copy(out=partition_order(h_perm[slab][:]), in_=unit_order(h_nat[slab][:].bitcast(F32)))
-
-            def turn_hidden(slab):
-                ch, part = divmod(slab, SLABS_PER_CHUNK)
-                if part == 0:
-                    hidden.append(keep.tile([P, PACK * CHUNK], BF16, name="hidden%d" % ch))
-                    silu_grouped.append(
-                        ring.tile([P, PACK * CHUNK], BF16, align_bytes=64, tag="grouped", name="silu_grouped")
-                    )
-                n_cols = slice(part * SLAB_COLS, (part + 1) * SLAB_COLS)
-                bank = turn([group(h_perm[slab], 2 * t + half) for half in range(HALVES) for t in range(2)])
-                nc.vector.tensor_copy(
-                    out=hidden[ch][:].bitcast(F32).rearrange("p (h n) -> p h n", h=HALVES)[:, :, n_cols],
-                    in_=bank[:].rearrange("p (h n) -> p h n", h=HALVES),
-                )
-                nc.scalar.activation(
-                    out=silu_grouped[ch][:].rearrange("p (n h u) -> p n h u", h=HALVES, u=2)[:, n_cols, :, :],
-                    in_=hidden[ch][:].rearrange("p (h n u) -> p n h u", h=HALVES, u=2)[:, n_cols, :, :],
-                    func=ACT.Silu,
-                )
-
-            shifted = {}
-
-            def shift(ch):
-                shifted[ch] = ring.tile([P, PACK * CHUNK], F32, name="shifted", bufs=2)
-                nc.vector.tensor_scalar_add(out=shifted[ch][:], in0=hidden[ch][:], scalar1=-SPACING)
-
-            permute_hidden(0)
-            for slab in range(SLABS):
-                if slab + 1 < SLABS:
-                    permute_hidden(slab + 1)
-                turn_hidden(slab)
-            shift(0)
-
-            bias_turned = turned.tile([P, P], BF16, tag="turned")
-            nc.tensor.transpose(bias_turned[:], bias_rows[:], ident_bf16[:])
-            bias_sb = keep.tile([P, ROW_TILES], F32)
-            nc.vector.tensor_copy(out=bias_sb[:], in_=bias_turned[:, 0:ROW_TILES])
-
-            w_codes = keep.tile([P, ROW_TILES * PASSES * P], U32, align_bytes=64)
-            w_scales = keep.tile([P, ROW_TILES * PASSES * P], U8, align_bytes=64)
-
-            def regroup(grouped, first_word, bank):
-                nc.vector.tensor_copy(
-                    out=grouped[:]
-                    .bitcast(F32)[:, first_word : first_word + CHUNK]
-                    .rearrange("p (a q s) -> p a q s", a=2, s=2),
-                    in_=bank[:].rearrange("p (a s q) -> p a q s", a=2, s=2),
-                )
-
-            bw_perm = keep.tile([P, WORD_GROUPS * P], F32)
-            nc.vector.tensor_copy(out=partition_order(bw_perm[:]), in_=unit_order(bw_nat[:].bitcast(F32)))
-            bw_banks = [turn([group(bw_perm, g) for g in range(4 * m_pair, 4 * m_pair + 4)]) for m_pair in range(2)]
-            silu_codes = keep.tile([P, COLS], U32, align_bytes=64)
-            silu_scales = keep.tile([P, COLS], U8, align_bytes=64)
-            for ch in range(CHUNKS):
-                n_cols = slice(ch * CHUNK, (ch + 1) * CHUNK)
-                nc.vector.quantize_mx(
-                    out=silu_codes[:, n_cols].bitcast(FP8X4), scales=silu_scales[:, n_cols], in_=silu_grouped[ch][:]
-                )
-            bw_grouped = ring.tile([P, ROW_TILES * PACK * P], BF16, align_bytes=64, tag="grouped")
-            for m_pair in range(2):
-                regroup(bw_grouped, m_pair * CHUNK, bw_banks[m_pair])
-
-            for m in range(ROW_TILES):
-                w_cols = slice((m * PASSES + BASE_PASS) * P, (m * PASSES + BASE_PASS + 1) * P)
-                nc.vector.quantize_mx(
-                    out=w_codes[:, w_cols].bitcast(FP8X4),
-                    scales=w_scales[:, w_cols],
-                    in_=bw_grouped[:, m * PACK * P : (m + 1) * PACK * P],
-                )
-
-            w_banks = {}
-
-            def turn_weights(job):
-                if job < SORTED_BY_LOAD:
-                    w_sorted = ring.tile([P, W_JOB], BF16, tag="perm", bufs=2)
-                    nc.vector.tensor_copy(
-                        out=w_sorted[:].bitcast(F32).rearrange("q (c a s) -> q c a s", c=4, s=16),
-                        in_=w_nat[job][:].bitcast(F32).rearrange("q (a c s) -> q c a s", c=4, s=16),
-                    )
-                else:
-                    w_sorted = w_nat[job]
-                words = w_sorted[:].bitcast(F32)
-                w_banks[job] = [
-                    turn([words[:, 4 * u + pi0 + a : WORD_GROUPS * P : WORD_GROUPS] for a in range(2) for u in range(2)])
-                    for pi0 in range(0, PAIRS, 2)
-                ]
-
-            def pack_weights(job):
-                half, m = divmod(job, ROW_TILES)
-                w_grouped = ring.tile([P, PAIRS * PACK * P], BF16, align_bytes=64, tag="grouped")
-                for place, bank in enumerate(w_banks[job]):
-                    regroup(w_grouped, place * CHUNK, bank)
-                if job + 1 < JOBS:
-                    turn_weights(job + 1)
-                w_cols = slice((m * PASSES + half * PAIRS) * P, (m * PASSES + (half + 1) * PAIRS) * P)
-                nc.vector.quantize_mx(
-                    out=w_codes[:, w_cols].bitcast(FP8X4), scales=w_scales[:, w_cols], in_=w_grouped[:]
-                )
-
-            square = {}
-            basis = {}
-            rest = {}
-            codes = {}
-            scales = {}
-            acc = {}
-
-            def squares(step):
-                ch, k_pass = divmod(step, SPLINE_PASSES)
-                half, pi = divmod(k_pass, PAIRS)
-                centre = -1.0 + 2 * pi * SPACING
-                v_cols = slice(half * PER_CENTRE, (half + 1) * PER_CENTRE)
-                square[step] = ring.tile([P, PACK * CHUNK], F32, name="square", bufs=AHEAD + 1)
-                if (k_pass % FIRST_SHARE != TURN) if ch == 0 else (k_pass % SHARE == TURN):
-                    for e in range(2):
-                        nc.scalar.activation(
-                            out=square[step][:, e * PER_CENTRE : (e + 1) * PER_CENTRE],
-                            in_=hidden[ch][:, v_cols],
-                            func=ACT.Square,
-                            bias=-(centre + e * SPACING),
-                            scale=1.0,
-                        )
-                    rest[step] = 0.0
-                else:
-                    for e, source in enumerate((hidden[ch], shifted[ch])):
-                        nc.vector.scalar_tensor_tensor(
-                            out=square[step][:, e * PER_CENTRE : (e + 1) * PER_CENTRE],
-                            in0=source[:, v_cols],
-                            scalar=2.0 * centre,
-                            in1=source[:, v_cols],
-                            op0=ALU.subtract,
-                            op1=ALU.mult,
-                        )
-                    rest[step] = centre * centre
-
-            def make_basis_tiles(step):
-                basis[step] = ring.tile([P, PACK * CHUNK], BF16, align_bytes=64, name="basis", bufs=BASIS_BUFS)
-                codes[step] = ring.tile([P, CHUNK], U32, align_bytes=64, name="codes", bufs=CODE_BUFS)
-                scales[step] = ring.tile([P, CHUNK], U8, align_bytes=64, name="scales", bufs=CODE_BUFS)
-
-            def exponentials(step, first=0, last=CHUNK):
-                if first == 0:
-                    make_basis_tiles(step)
-                nc.scalar.activation(
-                    out=basis[step][:].rearrange("p (v e) -> p v e", e=2)[:, 2 * first : 2 * last, :],
-                    in_=square[step][:].rearrange("p (e v) -> p v e", e=2)[:, 2 * first : 2 * last, :],
-                    func=ACT.Exp,
-                    bias=-rest[step] / (SPACING * SPACING),
-                    scale=-1.0 / (SPACING * SPACING),
-                )
-
-            def quantise(step, first=0, last=CHUNK):
-                nc.vector.quantize_mx(
-                    out=codes[step][:, first:last].bitcast(FP8X4),
-                    scales=scales[step][:, first:last],
-                    in_=basis[step][:, PACK * first : PACK * last],
-                )
-
-            def one_pass(sums, k_pass, rhs, rhs_scale):
-                for m in range(ROW_TILES):
-                    w_cols = slice((m * PASSES + k_pass) * P, (m * PASSES + k_pass + 1) * P)
-                    nc.tensor.matmul_mx(
-                        out=sums[m],
-                        lhsT=w_codes[:, w_cols].bitcast(FP8X4),
-                        lhsT_scale=w_scales[:, w_cols],
-                        rhs=rhs.bitcast(FP8X4),
-                        rhs_scale=rhs_scale,
-                        start=(k_pass == BASE_PASS),
-                        stop=(k_pass == SPLINE_PASSES - 1),
-                    )
-
-            def multiply(step, first=0, last=CHUNK):
-                ch, k_pass = divmod(step, SPLINE_PASSES)
-                banks = (ch + (first > 0)) % 2
-                if k_pass == 0:
-                    tiles = [sum_pools[banks].tile([P, CHUNK], F32, name="acc%d" % m) for m in range(ROW_TILES)]
-                    acc[ch, first] = [tile[:, 0 : last - first] for tile in tiles]
-                    n_cols = slice(ch * CHUNK + first, ch * CHUNK + last)
-                    one_pass(acc[ch, first], BASE_PASS, silu_codes[:, n_cols], silu_scales[:, n_cols])
-                one_pass(acc[ch, first], k_pass, codes[step][:, first:last], scales[step][:, first:last])
-
-            results = {}
-
-            def finish(ch, m, first=0, last=CHUNK):
-                if first == 0:
-                    results[ch, m] = ring.tile([P, CHUNK], F32, name="result", bufs=ROW_TILES)
-                result = results[ch, m]
-                nc.vector.scalar_tensor_tensor(
-                    out=result[:, first:last],
-                    in0=acc[ch, first][m],
-                    scalar=bias_sb[:, m : m + 1],
-                    in1=x_sb[:, m * COLS + ch * CHUNK + first : m * COLS + ch * CHUNK + last],
-                    op0=ALU.add,
-                    op1=ALU.add,
-                )
-                for c in range(first, last, STORE_COLS):
-                    b, c0 = divmod(ch * CHUNK + c, CHANNELS)
+            h_nat.append(h_tile)
+        nc.sync.dma_start(out=bias_rows[0:ROW_TILES, :], in_=fc2_base_b.rearrange("(m q) -> m q", q=P))
+        bw_nat = keep.tile([P, ROW_TILES * HIDDEN], BF16)
+        nc.sync.dma_start(
+            out=bw_nat[:].rearrange("q (m j) -> q m j", m=ROW_TILES),
+            in_=fc2_base_w.rearrange("(m q) j -> q m j", q=P),
+        )
+        w_nat = []
+        for job in range(JOBS):
+            half, m = divmod(job, ROW_TILES)
+            w_tile = keep.tile([P, W_JOB], BF16, name="w_nat%d" % job)
+            w_rows = fc2_spline_w[m * P : (m + 1) * P, half * W_JOB : (half + 1) * W_JOB]
+            if job < SORTED_BY_LOAD:
+                nc.sync.dma_start(out=w_tile[:], in_=w_rows)
+            else:
+                for c in range(4):
                     nc.sync.dma_start(
-                        out=out[b, m * P : (m + 1) * P, c0 : c0 + STORE_COLS],
-                        in_=result[:, c : c + STORE_COLS],
+                        out=w_tile[:].rearrange("q (c a s) -> q c a s", c=4, s=32)[:, c, :, :],
+                        in_=w_rows.rearrange("q (a c s) -> q c a s", c=4, s=32)[:, c, :, :],
                     )
+            w_nat.append(w_tile)
+        x_sb = keep.tile([P, ROW_TILES * COLS], BF16)
+        for m in range(ROW_TILES):
+            nc.sync.dma_start(
+                out=x_sb[:, m * COLS : (m + 1) * COLS].rearrange("q (b c) -> q b c", b=BATCH),
+                in_=x[:, m * P : (m + 1) * P, :].rearrange("b q c -> q b c"),
+            )
 
-            turn_weights(0)
-            for step in range(AHEAD):
-                squares(step)
-            for step in range(SPLINE_PASSES):
-                exponentials(step)
-                pack_weights(step)
-                if step == SHIFT_AFTER:
-                    shift(1)
-                squares(step + AHEAD)
-                quantise(step)
-                if step >= ROW_TILES:
-                    multiply(step - ROW_TILES)
+        ident_f32 = keep.tile([P, P], F32)
+        make_identity(nc, ident_f32[:])
+        ident_bf16 = keep.tile([P, P], BF16)
+        make_identity(nc, ident_bf16[:])
 
-        sum_pools.append(stack.enter_context(tc.psum_pool(name="sums_odd", bufs=1)))
-        for step in range(SPLINE_PASSES - ROW_TILES, SPLINE_PASSES):
-            multiply(step)
+        warm_in = keep.tile([P, 1], F32)
+        nc.vector.memset(warm_in[:], 0.0)
+        warm_out = keep.tile([P, 1], F32)
+        nc.scalar.activation(out=warm_out[:], in_=warm_in[:], func=ACT.Silu)
+
+        curve = keep.tile([P, P], F32)
+        nc.gpsimd.tensor_scalar(
+            out=curve[:], in0=ident_f32[:], scalar1=1.0 / (SPACING * SPACING), scalar2=0.0, op0=ALU.mult, op1=ALU.add
+        )
+        slopes = {}
+        levels = {}
+        for pi in range(1, PAIRS):
+            slopes[pi] = keep.tile([P, P], BF16, name="slope%d" % pi)
+            nc.gpsimd.tensor_scalar(
+                out=slopes[pi][:], in0=ident_bf16[:], scalar1=-4.0 * pi / SPACING, scalar2=0.0, op0=ALU.mult, op1=ALU.add
+            )
+            levels[pi] = keep.tile([P, 2 * TENSOR_COLS], BF16, name="level%d" % pi)
+            nc.gpsimd.memset(levels[pi][:], 4.0 * pi)
+
+        def turn(b, groups):
+            bank = psum_bank(b)
+            for place, group in enumerate(groups):
+                nc.tensor.transpose(bank[:, place * P : (place + 1) * P], group, ident_f32[:])
+            return bank
+
+        def group(words, g):
+            return words[:, g * P : (g + 1) * P]
+
+        h_perm = {}
+        hidden = []
+        silu_grouped = []
+
+        def permute_hidden(slab):
+            words = SLAB_TILES[slab] * HALVES * P
+            h_perm[slab] = ring.tile([P, words], F32, name="h_perm", bufs=3)
+            nc.vector.tensor_copy(out=partition_order(h_perm[slab][:]), in_=unit_order(h_nat[slab][:].bitcast(F32)))
+
+        h_banks = {}
+
+        def turn_hidden(slab):
+            tiles = SLAB_TILES[slab]
+            h_banks[slab] = turn(slab % HEAD_BANKS, [group(h_perm[slab], 2 * t + half) for half in range(HALVES) for t in range(tiles)])
+
+        def place(slab):
+            n0, n1 = slab_cols[slab]
+            ch = n0 // CHUNK
+            if n0 % CHUNK == 0:
+                hidden.append(keep.tile([P, PACK * CHUNK], BF16, name="hidden%d" % ch))
+                silu_grouped.append(
+                    ring.tile([P, PACK * CHUNK], BF16, align_bytes=64, tag="grouped", name="silu_grouped")
+                )
+            return ch, slice(n0 - ch * CHUNK, n1 - ch * CHUNK)
+
+        def copy_hidden(slab, ch, n_cols):
+            words = SLAB_TILES[slab] * HALVES * P
+            nc.vector.tensor_copy(
+                out=hidden[ch][:].bitcast(F32).rearrange("p (h n) -> p h n", h=HALVES)[:, :, n_cols],
+                in_=h_banks[slab][:, :words].rearrange("p (h n) -> p h n", h=HALVES),
+            )
+
+        def n_h_u(values):
+            return values.rearrange("p (h n u) -> p n h u", h=HALVES, u=2)
+
+        def silu(ch, n_cols, source):
+            nc.scalar.activation(
+                out=silu_grouped[ch][:].rearrange("p (n h u) -> p n h u", h=HALVES, u=2)[:, n_cols, :, :],
+                in_=source,
+                func=ACT.Silu,
+            )
+
+        def clamp(ch):
+            some = hidden[ch][:].rearrange("p (h v) -> p h v", h=HALVES)[:, :, 0 : 2 * TENSOR_COLS]
+            nc.vector.tensor_scalar(out=some, in0=some, scalar1=-CLAMP, scalar2=CLAMP, op0=ALU.max, op1=ALU.min)
+
+        shifted = {}
+
+        def shift(ch):
+            shifted[ch] = ring.tile([P, PACK * CHUNK], F32, name="shifted", bufs=2)
+            nc.vector.tensor_scalar_add(out=shifted[ch][:], in0=hidden[ch][:], scalar1=-SPACING)
+
+        for slab in range(EARLY_SLABS + 1):
+            permute_hidden(slab)
+        places = []
+        for slab in range(EARLY_SLABS):
+            turn_hidden(slab)
+            places.append(place(slab))
+            words = SLAB_TILES[slab] * HALVES * P
+            silu(*places[slab], n_h_u(h_banks[slab][:, :words].bitcast(BF16)))
+        for slab in range(EARLY_SLABS, len(SLAB_TILES)):
+            if slab + 1 < len(SLAB_TILES):
+                permute_hidden(slab + 1)
+            turn_hidden(slab)
+            ch, n_cols = place(slab)
+            copy_hidden(slab, ch, n_cols)
+            silu(ch, n_cols, n_h_u(hidden[ch][:])[:, n_cols, :, :])
+            if slab == EARLY_SLABS:
+                for early in range(EARLY_SLABS):
+                    copy_hidden(early, *places[early])
+        clamp(0)
+        shift(0)
+
+        square = {}
+        basis = {}
+        rest = {}
+        codes = {}
+        scales = {}
+        acc = {}
+
+        def on_tensor(step):
+            ch, k_pass = divmod(step, SPLINE_PASSES)
+            half, pi = divmod(k_pass, PAIRS)
+            return pi > 0 and (ch, half) in TENSOR_HALVES
+
+        tensor_square = {}
+
+        def squares_on_tensor(step):
+            ch, k_pass = divmod(step, SPLINE_PASSES)
+            half, pi = divmod(k_pass, PAIRS)
+            cols = 2 * TENSOR_COLS
+            bank = psum_bank(SQUARE_BANKS[step % 2])
+            tensor_square[step] = bank
+            nc.tensor.matmul(
+                bank[:].rearrange("p (e v) -> p e v", e=2),
+                lhsT=curve[:],
+                rhs=square[step - pi][:].rearrange("p (e v) -> p e v", e=2)[:, :, 0:cols],
+                start=True,
+                stop=False,
+            )
+            for e in range(2):
+                nc.tensor.matmul(
+                    bank[:, e * cols : (e + 1) * cols],
+                    lhsT=slopes[pi][:],
+                    rhs=hidden[ch][:, half * PER_CENTRE : half * PER_CENTRE + cols],
+                    start=False,
+                    stop=False,
+                )
+            nc.tensor.matmul(
+                bank[:, cols : 2 * cols], lhsT=ident_bf16[:], rhs=levels[pi][:], start=False, stop=True
+            )
+
+        def squares(step):
+            ch, k_pass = divmod(step, SPLINE_PASSES)
+            half, pi = divmod(k_pass, PAIRS)
+            centre = -1.0 + 2 * pi * SPACING
+            first = 2 * TENSOR_COLS if on_tensor(step) else 0
+            v_cols = slice(half * PER_CENTRE + first, (half + 1) * PER_CENTRE)
+            square[step] = ring.tile([P, PACK * CHUNK], F32, name="square", bufs=SQUARE_BUFS)
+            if (k_pass % FIRST_SHARE != FIRST_TURN) if ch == 0 else (k_pass % SHARE == TURN):
+                for e in range(2):
+                    nc.scalar.activation(
+                        out=square[step][:, e * PER_CENTRE + first : (e + 1) * PER_CENTRE],
+                        in_=hidden[ch][:, v_cols],
+                        func=ACT.Square,
+                        bias=-(centre + e * SPACING),
+                        scale=1.0,
+                    )
+                rest[step] = 0.0
+            else:
+                for e, source in enumerate((hidden[ch], shifted[ch])):
+                    nc.vector.scalar_tensor_tensor(
+                        out=square[step][:, e * PER_CENTRE + first : (e + 1) * PER_CENTRE],
+                        in0=source[:, v_cols],
+                        scalar=2.0 * centre,
+                        in1=source[:, v_cols],
+                        op0=ALU.subtract,
+                        op1=ALU.mult,
+                    )
+                rest[step] = centre * centre
+
+        bias_turned = psum_bank(len(SLAB_TILES) % HEAD_BANKS, BF16, P)
+        nc.tensor.transpose(bias_turned[:], bias_rows[:], ident_bf16[:])
+        bias_sb = keep.tile([P, ROW_TILES], F32)
+        nc.vector.tensor_copy(out=bias_sb[:], in_=bias_turned[:, 0:ROW_TILES])
+
+        w_codes = keep.tile([P, ROW_TILES * PASSES * P], U32, align_bytes=64)
+        w_scales = keep.tile([P, ROW_TILES * PASSES * P], U8, align_bytes=64)
+
+        def w_cols(k_pass, m):
+            half, pi = divmod(k_pass, PAIRS)
+            place = SPLINE_PASSES * ROW_TILES + m if k_pass == BASE_PASS else (half * ROW_TILES + m) * PAIRS + pi
+            return slice(place * P, (place + 1) * P)
+
+        def regroup(grouped, first_word, bank):
+            nc.vector.tensor_copy(
+                out=grouped[:]
+                .bitcast(F32)[:, first_word : first_word + CHUNK]
+                .rearrange("p (a q s) -> p a q s", a=2, s=2),
+                in_=bank[:].rearrange("p (a s q) -> p a q s", a=2, s=2),
+            )
+
+        bw_perm = keep.tile([P, WORD_GROUPS * P], F32)
+        nc.vector.tensor_copy(out=partition_order(bw_perm[:]), in_=unit_order(bw_nat[:].bitcast(F32)))
+        bw_banks = [
+            turn(WEIGHT_BANKS + m_pair, [group(bw_perm, g) for g in range(4 * m_pair, 4 * m_pair + 4)])
+            for m_pair in range(2)
+        ]
+        squares(0)
+        squares_on_tensor(1)
+        silu_codes = keep.tile([P, COLS], U32, align_bytes=64)
+        silu_scales = keep.tile([P, COLS], U8, align_bytes=64)
+        for ch in range(CHUNKS):
+            n_cols = slice(ch * CHUNK, (ch + 1) * CHUNK)
+            nc.vector.quantize_mx(
+                out=silu_codes[:, n_cols].bitcast(FP8X4), scales=silu_scales[:, n_cols], in_=silu_grouped[ch][:]
+            )
+        bw_grouped = ring.tile([P, ROW_TILES * PACK * P], BF16, align_bytes=64, tag="grouped")
+        for m_pair in range(2):
+            regroup(bw_grouped, m_pair * CHUNK, bw_banks[m_pair])
+
+        base_cols = slice(SPLINE_PASSES * ROW_TILES * P, PASSES * ROW_TILES * P)
+        nc.vector.quantize_mx(
+            out=w_codes[:, base_cols].bitcast(FP8X4), scales=w_scales[:, base_cols], in_=bw_grouped[:]
+        )
+
+        w_banks = {}
+
+        def turn_weights(job):
+            if job < SORTED_BY_LOAD:
+                w_sorted = ring.tile([P, W_JOB], BF16, tag="perm", bufs=2)
+                nc.vector.tensor_copy(
+                    out=w_sorted[:].bitcast(F32).rearrange("q (c a s) -> q c a s", c=4, s=16),
+                    in_=w_nat[job][:].bitcast(F32).rearrange("q (a c s) -> q c a s", c=4, s=16),
+                )
+            else:
+                w_sorted = w_nat[job]
+            words = w_sorted[:].bitcast(F32)
+            w_banks[job] = [
+                turn(
+                    WEIGHT_BANKS + pi0 // 2,
+                    [words[:, 4 * u + pi0 + a : WORD_GROUPS * P : WORD_GROUPS] for a in range(2) for u in range(2)],
+                )
+                for pi0 in range(0, PAIRS, 2)
+            ]
+
+        def pack_weights(job):
+            w_grouped = ring.tile([P, PAIRS * PACK * P], BF16, align_bytes=64, tag="grouped")
+            for place, bank in enumerate(w_banks[job]):
+                regroup(w_grouped, place * CHUNK, bank)
+            if job + 1 < JOBS:
+                turn_weights(job + 1)
+            job_cols = slice(job * PAIRS * P, (job + 1) * PAIRS * P)
+            nc.vector.quantize_mx(
+                out=w_codes[:, job_cols].bitcast(FP8X4), scales=w_scales[:, job_cols], in_=w_grouped[:]
+            )
+
+        def make_basis_tiles(step):
+            basis[step] = ring.tile([P, PACK * CHUNK], BF16, align_bytes=64, name="basis", bufs=BASIS_BUFS)
+            codes[step] = ring.tile([P, CHUNK], U32, align_bytes=64, name="codes", bufs=CODE_BUFS)
+            scales[step] = ring.tile([P, CHUNK], U8, align_bytes=64, name="scales", bufs=CODE_BUFS)
+
+        def exponentials(step, first=0, last=CHUNK):
+            if first == 0:
+                make_basis_tiles(step)
+            if on_tensor(step):
+                pi = step % PAIRS
+                first = TENSOR_COLS
+                left = 4.0 * pi * pi - 4.0 * pi / SPACING + rest[step - pi] / (SPACING * SPACING)
+                nc.scalar.activation(
+                    out=basis[step][:].rearrange("p (v e) -> p v e", e=2)[:, 0 : 2 * first, :],
+                    in_=tensor_square[step][:].rearrange("p (e v) -> p v e", e=2),
+                    func=ACT.Exp,
+                    bias=-left,
+                    scale=-1.0,
+                )
+            nc.scalar.activation(
+                out=basis[step][:].rearrange("p (v e) -> p v e", e=2)[:, 2 * first : 2 * last, :],
+                in_=square[step][:].rearrange("p (e v) -> p v e", e=2)[:, 2 * first : 2 * last, :],
+                func=ACT.Exp,
+                bias=-rest[step] / (SPACING * SPACING),
+                scale=-1.0 / (SPACING * SPACING),
+            )
+
+        def quantise(step, first=0, last=CHUNK):
+            nc.vector.quantize_mx(
+                out=codes[step][:, first:last].bitcast(FP8X4),
+                scales=scales[step][:, first:last],
+                in_=basis[step][:, PACK * first : PACK * last],
+            )
+
+        def one_pass(group, m, k_pass, rhs, rhs_scale):
+            nc.tensor.matmul_mx(
+                out=acc[group][m],
+                lhsT=w_codes[:, w_cols(k_pass, m)].bitcast(FP8X4),
+                lhsT_scale=w_scales[:, w_cols(k_pass, m)],
+                rhs=rhs.bitcast(FP8X4),
+                rhs_scale=rhs_scale,
+                start=(k_pass == BASE_PASS),
+                stop=(k_pass == SPLINE_PASSES - 1),
+            )
+
+        def multiply(step, first=0, last=CHUNK, tiles=range(ROW_TILES)):
+            ch, k_pass = divmod(step, SPLINE_PASSES)
+            group = (ch, first)
+            for m in tiles:
+                if k_pass == 0:
+                    turn_of = ROW_TILES * (ch + (first > 0)) + m
+                    b = SQUARE_BANKS[m % 2] if first > 0 and m >= 2 else turn_of % SUM_BANKS
+                    acc.setdefault(group, {})[m] = psum_bank(b, F32, last - first)[:]
+                    n_cols = slice(ch * CHUNK + first, ch * CHUNK + last)
+                    one_pass(group, m, BASE_PASS, silu_codes[:, n_cols], silu_scales[:, n_cols])
+                one_pass(group, m, k_pass, codes[step][:, first:last], scales[step][:, first:last])
+
+        results = {}
+
+        def finish(ch, m, first=0, last=CHUNK):
+            if first == 0:
+                results[ch, m] = ring.tile([P, CHUNK], F32, name="result", bufs=ROW_TILES)
+            result = results[ch, m]
+            nc.vector.scalar_tensor_tensor(
+                out=result[:, first:last],
+                in0=acc[ch, first][m],
+                scalar=bias_sb[:, m : m + 1],
+                in1=x_sb[:, m * COLS + ch * CHUNK + first : m * COLS + ch * CHUNK + last],
+                op0=ALU.add,
+                op1=ALU.add,
+            )
+            for c in range(first, last, STORE_COLS):
+                b, c0 = divmod(ch * CHUNK + c, CHANNELS)
+                nc.sync.dma_start(
+                    out=out[b, m * P : (m + 1) * P, c0 : c0 + STORE_COLS],
+                    in_=result[:, c : c + STORE_COLS],
+                )
+
+        def squares_ahead(step):
+            pi = step % PAIRS
+            for ahead in {PAIRS - 1: (2, 3), 1: (2,)}.get(pi, ()):
+                if step + ahead < STEPS and on_tensor(step + ahead):
+                    squares_on_tensor(step + ahead)
+
+        turn_weights(0)
+        squares(1)
+        squares_on_tensor(2)
+        squares(2)
+        waiting = []
+        for step in range(SPLINE_PASSES):
+            exponentials(step)
+            squares_ahead(step)
+            pack_weights(step)
+            if step == SHIFT_AFTER:
+                clamp(1)
+                shift(1)
+            squares(step + AHEAD)
+            quantise(step)
+            half, done = divmod(step, ROW_TILES)
+            waiting += [(step, m) for m in range(done)] + [(late, done) for late in range(half * PAIRS, step + 1)]
+            for late, m in waiting[:PASSES_A_STEP]:
+                multiply(late, tiles=(m,))
+            waiting = waiting[PASSES_A_STEP:]
+        for late, m in waiting:
+            multiply(late, tiles=(m,))
 
         HALF = CHUNK // 2
         for step in range(SPLINE_PASSES, STEPS - 1):
             ch, k_pass = divmod(step, SPLINE_PASSES)
             exponentials(step)
+            squares_ahead(step)
             if k_pass == SHIFT_AFTER and ch + 1 < CHUNKS:
+                clamp(ch + 1)
                 shift(ch + 1)
             if step + AHEAD < STEPS:
                 squares(step + AHEAD)
             quantise(step)
             if ch + 1 < CHUNKS:
-                multiply(step)
+                spans = [(0, CHUNK, 0, 2, 0), (0, CHUNK, 2, 4, FINISH_AFTER)]
             else:
-                multiply(step, 0, HALF)
-                if k_pass > FINISH_AFTER:
-                    multiply(step, HALF, CHUNK)
+                spans = [
+                    (0, HALF, 0, 2, 0),
+                    (0, HALF, 2, 4, FINISH_AFTER),
+                    (HALF, CHUNK, 0, 2, FINISH_AFTER),
+                    (HALF, CHUNK, 2, 4, SQUARES_OVER),
+                ]
             if k_pass == FINISH_AFTER:
                 for m in range(ROW_TILES):
                     finish(ch - 1, m)
-                if ch + 1 == CHUNKS:
-                    for late in range(step - FINISH_AFTER, step + 1):
-                        multiply(late, HALF, CHUNK)
+            for first, last, m0, m1, opened in spans:
+                if k_pass >= opened:
+                    for late in range(step - k_pass if k_pass == opened else step, step + 1):
+                        multiply(late, first, last, range(m0, m1))
 
         exponentials(STEPS - 1, 0, HALF)
         exponentials(STEPS - 1, HALF, CHUNK)

@@ -41,21 +41,18 @@ W_JOB = HIDDEN * CENTRES // HALVES
 SORTED_BY_LOAD = 4
 JOBS = HALVES * ROW_TILES
 AHEAD = 3
-FIRST_SHARE = 3
-SHARE = 4
+FIRST_SHARE = 4
 FIRST_TURN = 1
 PASSES_A_STEP = 4
-TURN = 0
 BASIS_BUFS = 4
 SQUARE_BUFS = AHEAD + 2
 CODE_BUFS = 9
 SHIFT_AFTER = 3
 SQUARES_OVER = 3
-FINISH_AFTER = 1
+FINISH_AFTER = (1, 0)
 
 assert JOBS == SPLINE_PASSES
 assert SHIFT_AFTER < SPLINE_PASSES - AHEAD
-assert (FINISH_AFTER + AHEAD) % SHARE == TURN
 
 FLOPS = 2 * COLS * ROWS * (HIDDEN * CENTRES + HIDDEN)
 
@@ -272,7 +269,7 @@ def tile_kan1_pb_kernel(tc, h_mix, x, fc2_spline_w, fc2_base_w, fc2_base_b, out)
             first = 2 * TENSOR_COLS if on_tensor(step) else 0
             v_cols = slice(half * PER_CENTRE + first, (half + 1) * PER_CENTRE)
             square[step] = ring.tile([P, PACK * CHUNK], F32, name="square", bufs=SQUARE_BUFS)
-            if (k_pass % FIRST_SHARE != FIRST_TURN) if ch == 0 else (k_pass % SHARE == TURN):
+            if (k_pass % FIRST_SHARE != FIRST_TURN) if ch == 0 else (pi == 0 and (ch, half) in TENSOR_HALVES):
                 for e in range(2):
                     nc.scalar.activation(
                         out=square[step][:, e * PER_CENTRE + first : (e + 1) * PER_CENTRE],
@@ -469,14 +466,31 @@ def tile_kan1_pb_kernel(tc, h_mix, x, fc2_spline_w, fc2_base_w, fc2_base_b, out)
             squares(step + AHEAD)
             quantise(step)
             half, done = divmod(step, ROW_TILES)
-            waiting += [(step, m) for m in range(done)] + [(late, done) for late in range(half * PAIRS, step + 1)]
             for late, m in waiting[:PASSES_A_STEP]:
                 multiply(late, tiles=(m,))
             waiting = waiting[PASSES_A_STEP:]
+            waiting += [(step, m) for m in range(done)] + [(late, done) for late in range(half * PAIRS, step + 1)]
         for late, m in waiting:
             multiply(late, tiles=(m,))
 
         HALF = CHUNK // 2
+
+        def passes(step):
+            ch, k_pass = divmod(step, SPLINE_PASSES)
+            if ch + 1 < CHUNKS:
+                spans = [(0, CHUNK, 0, 2, 0), (0, CHUNK, 2, 4, FINISH_AFTER[0])]
+            else:
+                spans = [
+                    (0, HALF, 0, 2, 0),
+                    (0, HALF, 2, 4, FINISH_AFTER[1]),
+                    (HALF, CHUNK, 0, 2, FINISH_AFTER[1]),
+                    (HALF, CHUNK, 2, 4, SQUARES_OVER),
+                ]
+            for first, last, m0, m1, opened in spans:
+                if k_pass >= opened:
+                    for late in range(step - k_pass if k_pass == opened else step, step + 1):
+                        multiply(late, first, last, range(m0, m1))
+
         for step in range(SPLINE_PASSES, STEPS - 1):
             ch, k_pass = divmod(step, SPLINE_PASSES)
             exponentials(step)
@@ -487,22 +501,12 @@ def tile_kan1_pb_kernel(tc, h_mix, x, fc2_spline_w, fc2_base_w, fc2_base_b, out)
             if step + AHEAD < STEPS:
                 squares(step + AHEAD)
             quantise(step)
-            if ch + 1 < CHUNKS:
-                spans = [(0, CHUNK, 0, 2, 0), (0, CHUNK, 2, 4, FINISH_AFTER)]
-            else:
-                spans = [
-                    (0, HALF, 0, 2, 0),
-                    (0, HALF, 2, 4, FINISH_AFTER),
-                    (HALF, CHUNK, 0, 2, FINISH_AFTER),
-                    (HALF, CHUNK, 2, 4, SQUARES_OVER),
-                ]
-            if k_pass == FINISH_AFTER:
+            if step > SPLINE_PASSES:
+                passes(step - 1)
+            if k_pass == FINISH_AFTER[ch - 1]:
                 for m in range(ROW_TILES):
                     finish(ch - 1, m)
-            for first, last, m0, m1, opened in spans:
-                if k_pass >= opened:
-                    for late in range(step - k_pass if k_pass == opened else step, step + 1):
-                        multiply(late, first, last, range(m0, m1))
+        passes(STEPS - 2)
 
         exponentials(STEPS - 1, 0, HALF)
         exponentials(STEPS - 1, HALF, CHUNK)

@@ -17,6 +17,8 @@ BATCH, CHANNELS, HIDDEN, ROWS, CENTRES = 2, 768, 512, 512, 8
 COLS = BATCH * CHANNELS
 CHUNK = 512
 CHUNKS = COLS // CHUNK
+HALF = CHUNK // 2
+RESULT_BUFS = 6
 STORE_COLS = 256
 ROW_TILES = ROWS // P
 SPACING = 2.0 / (CENTRES - 1)
@@ -32,7 +34,6 @@ SLAB_TILES = (1, 1, 2, 2, 2, 2, 2)
 SQUARE_BANKS = (6, 7)
 SUM_BANKS = 6
 TENSOR_COLS = CHUNK // 4
-TENSOR_HALVES = ((0, 0), (0, 1), (1, 0), (1, 1), (2, 0))
 CLAMP = 16384.0
 HEAD_BANKS = 4
 WEIGHT_BANKS = 4
@@ -40,15 +41,15 @@ EARLY_SLABS = 2
 W_JOB = HIDDEN * CENTRES // HALVES
 SORTED_BY_LOAD = 4
 JOBS = HALVES * ROW_TILES
-AHEAD = 3
-FIRST_SHARE = 4
+AHEAD = 2
+SCALAR_COLS = CHUNK // 2
+FIRST_SHARE = 3
 FIRST_TURN = 1
 PASSES_A_STEP = 4
 BASIS_BUFS = 4
 SQUARE_BUFS = AHEAD + 2
 CODE_BUFS = 9
 SHIFT_AFTER = 3
-SQUARES_OVER = 3
 FINISH_AFTER = (1, 0)
 
 assert JOBS == SPLINE_PASSES
@@ -132,14 +133,13 @@ def tile_kan1_pb_kernel(tc, h_mix, x, fc2_spline_w, fc2_base_w, fc2_base_b, out)
             out=curve[:], in0=ident_f32[:], scalar1=1.0 / (SPACING * SPACING), scalar2=0.0, op0=ALU.mult, op1=ALU.add
         )
         slopes = {}
-        levels = {}
         for pi in range(1, PAIRS):
-            slopes[pi] = keep.tile([P, P], BF16, name="slope%d" % pi)
-            nc.gpsimd.tensor_scalar(
-                out=slopes[pi][:], in0=ident_bf16[:], scalar1=-4.0 * pi / SPACING, scalar2=0.0, op0=ALU.mult, op1=ALU.add
-            )
-            levels[pi] = keep.tile([P, 2 * TENSOR_COLS], BF16, name="level%d" % pi)
-            nc.gpsimd.memset(levels[pi][:], 4.0 * pi)
+            slopes[pi] = []
+            for e, ident in enumerate((ident_bf16, ident_f32)):
+                slopes[pi].append(keep.tile([P, P], (BF16, F32)[e], name="slope%d%d" % (pi, e)))
+                nc.gpsimd.tensor_scalar(
+                    out=slopes[pi][e][:], in0=ident[:], scalar1=-4.0 * pi / SPACING, scalar2=0.0, op0=ALU.mult, op1=ALU.add
+                )
 
         def turn(b, groups):
             bank = psum_bank(b)
@@ -221,19 +221,15 @@ def tile_kan1_pb_kernel(tc, h_mix, x, fc2_spline_w, fc2_base_w, fc2_base_b, out)
                 for early in range(EARLY_SLABS):
                     copy_hidden(early, *places[early])
         clamp(0)
-        shift(0)
 
         square = {}
         basis = {}
-        rest = {}
         codes = {}
         scales = {}
         acc = {}
 
         def on_tensor(step):
-            ch, k_pass = divmod(step, SPLINE_PASSES)
-            half, pi = divmod(k_pass, PAIRS)
-            return pi > 0 and (ch, half) in TENSOR_HALVES
+            return step % PAIRS > 0
 
         tensor_square = {}
 
@@ -250,46 +246,54 @@ def tile_kan1_pb_kernel(tc, h_mix, x, fc2_spline_w, fc2_base_w, fc2_base_b, out)
                 start=True,
                 stop=False,
             )
-            for e in range(2):
+            for e, source in enumerate((hidden[ch], shifted[ch])):
                 nc.tensor.matmul(
                     bank[:, e * cols : (e + 1) * cols],
-                    lhsT=slopes[pi][:],
-                    rhs=hidden[ch][:, half * PER_CENTRE : half * PER_CENTRE + cols],
+                    lhsT=slopes[pi][e][:],
+                    rhs=source[:, half * PER_CENTRE : half * PER_CENTRE + cols],
                     start=False,
-                    stop=False,
+                    stop=(e == 1),
                 )
-            nc.tensor.matmul(
-                bank[:, cols : 2 * cols], lhsT=ident_bf16[:], rhs=levels[pi][:], start=False, stop=True
-            )
+
+        def shares(step):
+            tensor_end = TENSOR_COLS if on_tensor(step) else 0
+            if step < SPLINE_PASSES:
+                scalar_end = tensor_end if step % FIRST_SHARE == FIRST_TURN else CHUNK
+            else:
+                scalar_end = tensor_end if on_tensor(step) else SCALAR_COLS
+            return {"tensor": (0, tensor_end), "scalar": (tensor_end, scalar_end), "vector": (scalar_end, CHUNK)}
+
+        def first_centre(step):
+            return -1.0 + 2 * (step % PAIRS) * SPACING
 
         def squares(step):
             ch, k_pass = divmod(step, SPLINE_PASSES)
-            half, pi = divmod(k_pass, PAIRS)
-            centre = -1.0 + 2 * pi * SPACING
-            first = 2 * TENSOR_COLS if on_tensor(step) else 0
-            v_cols = slice(half * PER_CENTRE + first, (half + 1) * PER_CENTRE)
+            centre = first_centre(step)
             square[step] = ring.tile([P, PACK * CHUNK], F32, name="square", bufs=SQUARE_BUFS)
-            if (k_pass % FIRST_SHARE != FIRST_TURN) if ch == 0 else (pi == 0 and (ch, half) in TENSOR_HALVES):
+            v_of_e = square[step][:].rearrange("p (e v) -> p e v", e=2)
+            v_of_half = k_pass // PAIRS * PER_CENTRE
+            first, last = shares(step)["scalar"]
+            if first < last:
                 for e in range(2):
                     nc.scalar.activation(
-                        out=square[step][:, e * PER_CENTRE + first : (e + 1) * PER_CENTRE],
-                        in_=hidden[ch][:, v_cols],
+                        out=v_of_e[:, e, 2 * first : 2 * last],
+                        in_=hidden[ch][:, v_of_half + 2 * first : v_of_half + 2 * last],
                         func=ACT.Square,
                         bias=-(centre + e * SPACING),
                         scale=1.0,
                     )
-                rest[step] = 0.0
-            else:
+            first, last = shares(step)["vector"]
+            if first < last:
                 for e, source in enumerate((hidden[ch], shifted[ch])):
+                    s = source[:, v_of_half + 2 * first : v_of_half + 2 * last]
                     nc.vector.scalar_tensor_tensor(
-                        out=square[step][:, e * PER_CENTRE + first : (e + 1) * PER_CENTRE],
-                        in0=source[:, v_cols],
+                        out=v_of_e[:, e, 2 * first : 2 * last],
+                        in0=s,
                         scalar=2.0 * centre,
-                        in1=source[:, v_cols],
+                        in1=s,
                         op0=ALU.subtract,
                         op1=ALU.mult,
                     )
-                rest[step] = centre * centre
 
         bias_turned = psum_bank(len(SLAB_TILES) % HEAD_BANKS, BF16, P)
         nc.tensor.transpose(bias_turned[:], bias_rows[:], ident_bf16[:])
@@ -314,6 +318,7 @@ def tile_kan1_pb_kernel(tc, h_mix, x, fc2_spline_w, fc2_base_w, fc2_base_b, out)
 
         bw_perm = keep.tile([P, WORD_GROUPS * P], F32)
         nc.vector.tensor_copy(out=partition_order(bw_perm[:]), in_=unit_order(bw_nat[:].bitcast(F32)))
+        shift(0)
         bw_banks = [
             turn(WEIGHT_BANKS + m_pair, [group(bw_perm, g) for g in range(4 * m_pair, 4 * m_pair + 4)])
             for m_pair in range(2)
@@ -331,12 +336,9 @@ def tile_kan1_pb_kernel(tc, h_mix, x, fc2_spline_w, fc2_base_w, fc2_base_b, out)
         for m_pair in range(2):
             regroup(bw_grouped, m_pair * CHUNK, bw_banks[m_pair])
 
-        base_cols = slice(SPLINE_PASSES * ROW_TILES * P, PASSES * ROW_TILES * P)
-        nc.vector.quantize_mx(
-            out=w_codes[:, base_cols].bitcast(FP8X4), scales=w_scales[:, base_cols], in_=bw_grouped[:]
-        )
 
         w_banks = {}
+        w_grouped = {}
 
         def turn_weights(job):
             if job < SORTED_BY_LOAD:
@@ -357,42 +359,43 @@ def tile_kan1_pb_kernel(tc, h_mix, x, fc2_spline_w, fc2_base_w, fc2_base_b, out)
             ]
 
         def pack_weights(job):
-            w_grouped = ring.tile([P, PAIRS * PACK * P], BF16, align_bytes=64, tag="grouped")
+            w_grouped[job] = ring.tile([P, PAIRS * PACK * P], BF16, align_bytes=64, tag="grouped", name="w_grouped")
             for place, bank in enumerate(w_banks[job]):
-                regroup(w_grouped, place * CHUNK, bank)
+                regroup(w_grouped[job], place * CHUNK, bank)
             if job + 1 < JOBS:
                 turn_weights(job + 1)
+
+        def quantise_weights(job):
             job_cols = slice(job * PAIRS * P, (job + 1) * PAIRS * P)
             nc.vector.quantize_mx(
-                out=w_codes[:, job_cols].bitcast(FP8X4), scales=w_scales[:, job_cols], in_=w_grouped[:]
+                out=w_codes[:, job_cols].bitcast(FP8X4), scales=w_scales[:, job_cols], in_=w_grouped[job][:]
             )
 
-        def make_basis_tiles(step):
-            basis[step] = ring.tile([P, PACK * CHUNK], BF16, align_bytes=64, name="basis", bufs=BASIS_BUFS)
-            codes[step] = ring.tile([P, CHUNK], U32, align_bytes=64, name="codes", bufs=CODE_BUFS)
-            scales[step] = ring.tile([P, CHUNK], U8, align_bytes=64, name="scales", bufs=CODE_BUFS)
+        def rest(step, engine):
+            if engine == "scalar":
+                return 0.0
+            if engine == "vector":
+                return (first_centre(step) / SPACING) ** 2
+            pi = step % PAIRS
+            maker = "scalar" if shares(step - pi)["scalar"][1] > 0 else "vector"
+            return 4.0 * pi * pi - 4.0 * pi / SPACING + rest(step - pi, maker)
 
         def exponentials(step, first=0, last=CHUNK):
             if first == 0:
-                make_basis_tiles(step)
-            if on_tensor(step):
-                pi = step % PAIRS
-                first = TENSOR_COLS
-                left = 4.0 * pi * pi - 4.0 * pi / SPACING + rest[step - pi] / (SPACING * SPACING)
-                nc.scalar.activation(
-                    out=basis[step][:].rearrange("p (v e) -> p v e", e=2)[:, 0 : 2 * first, :],
-                    in_=tensor_square[step][:].rearrange("p (e v) -> p v e", e=2),
-                    func=ACT.Exp,
-                    bias=-left,
-                    scale=-1.0,
-                )
-            nc.scalar.activation(
-                out=basis[step][:].rearrange("p (v e) -> p v e", e=2)[:, 2 * first : 2 * last, :],
-                in_=square[step][:].rearrange("p (e v) -> p v e", e=2)[:, 2 * first : 2 * last, :],
-                func=ACT.Exp,
-                bias=-rest[step] / (SPACING * SPACING),
-                scale=-1.0 / (SPACING * SPACING),
-            )
+                basis[step] = ring.tile([P, PACK * CHUNK], BF16, align_bytes=64, name="basis", bufs=BASIS_BUFS)
+                codes[step] = ring.tile([P, CHUNK], U32, align_bytes=64, name="codes", bufs=CODE_BUFS)
+                scales[step] = ring.tile([P, CHUNK], U8, align_bytes=64, name="scales", bufs=CODE_BUFS)
+            for engine, (begin, end) in shares(step).items():
+                begin, end = max(begin, first), min(end, last)
+                if begin < end:
+                    source = tensor_square[step] if engine == "tensor" else square[step]
+                    nc.scalar.activation(
+                        out=basis[step][:].rearrange("p (v e) -> p v e", e=2)[:, 2 * begin : 2 * end, :],
+                        in_=source[:].rearrange("p (e v) -> p v e", e=2)[:, 2 * begin : 2 * end, :],
+                        func=ACT.Exp,
+                        bias=-rest(step, engine),
+                        scale=-1.0 if engine == "tensor" else -1.0 / (SPACING * SPACING),
+                    )
 
         def quantise(step, first=0, last=CHUNK):
             nc.vector.quantize_mx(
@@ -401,9 +404,14 @@ def tile_kan1_pb_kernel(tc, h_mix, x, fc2_spline_w, fc2_base_w, fc2_base_b, out)
                 in_=basis[step][:, PACK * first : PACK * last],
             )
 
-        def one_pass(group, m, k_pass, rhs, rhs_scale):
+        groups = {ch: [(m, 0, CHUNK) for m in range(ROW_TILES)] for ch in range(CHUNKS - 1)}
+        groups[CHUNKS - 1] = [(m, first, first + HALF) for first in (0, HALF) for m in range(2)]
+        groups[CHUNKS - 1] += [(m, 0, CHUNK) for m in range(2, ROW_TILES)]
+
+        def one_pass(ch, group, k_pass, rhs, rhs_scale):
+            m = group[0]
             nc.tensor.matmul_mx(
-                out=acc[group][m],
+                out=acc[ch, group],
                 lhsT=w_codes[:, w_cols(k_pass, m)].bitcast(FP8X4),
                 lhsT_scale=w_scales[:, w_cols(k_pass, m)],
                 rhs=rhs.bitcast(FP8X4),
@@ -412,27 +420,22 @@ def tile_kan1_pb_kernel(tc, h_mix, x, fc2_spline_w, fc2_base_w, fc2_base_b, out)
                 stop=(k_pass == SPLINE_PASSES - 1),
             )
 
-        def multiply(step, first=0, last=CHUNK, tiles=range(ROW_TILES)):
+        def multiply(step, group):
             ch, k_pass = divmod(step, SPLINE_PASSES)
-            group = (ch, first)
-            for m in tiles:
-                if k_pass == 0:
-                    turn_of = ROW_TILES * (ch + (first > 0)) + m
-                    b = SQUARE_BANKS[m % 2] if first > 0 and m >= 2 else turn_of % SUM_BANKS
-                    acc.setdefault(group, {})[m] = psum_bank(b, F32, last - first)[:]
-                    n_cols = slice(ch * CHUNK + first, ch * CHUNK + last)
-                    one_pass(group, m, BASE_PASS, silu_codes[:, n_cols], silu_scales[:, n_cols])
-                one_pass(group, m, k_pass, codes[step][:, first:last], scales[step][:, first:last])
+            m, first, last = group
+            if k_pass == 0:
+                b = (ROW_TILES * ch + groups[ch].index(group)) % SUM_BANKS
+                acc[ch, group] = psum_bank(b, F32, last - first)[:]
+                n_cols = slice(ch * CHUNK + first, ch * CHUNK + last)
+                one_pass(ch, group, BASE_PASS, silu_codes[:, n_cols], silu_scales[:, n_cols])
+            one_pass(ch, group, k_pass, codes[step][:, first:last], scales[step][:, first:last])
 
-        results = {}
-
-        def finish(ch, m, first=0, last=CHUNK):
-            if first == 0:
-                results[ch, m] = ring.tile([P, CHUNK], F32, name="result", bufs=ROW_TILES)
-            result = results[ch, m]
+        def finish(ch, group):
+            m, first, last = group
+            result = ring.tile([P, CHUNK], F32, name="result", bufs=RESULT_BUFS)
             nc.vector.scalar_tensor_tensor(
                 out=result[:, first:last],
-                in0=acc[ch, first][m],
+                in0=acc[ch, group],
                 scalar=bias_sb[:, m : m + 1],
                 in1=x_sb[:, m * COLS + ch * CHUNK + first : m * COLS + ch * CHUNK + last],
                 op0=ALU.add,
@@ -452,9 +455,13 @@ def tile_kan1_pb_kernel(tc, h_mix, x, fc2_spline_w, fc2_base_w, fc2_base_b, out)
                     squares_on_tensor(step + ahead)
 
         turn_weights(0)
-        squares(1)
+        base_cols = slice(SPLINE_PASSES * ROW_TILES * P, PASSES * ROW_TILES * P)
+        nc.vector.quantize_mx(
+            out=w_codes[:, base_cols].bitcast(FP8X4), scales=w_scales[:, base_cols], in_=bw_grouped[:]
+        )
         squares_on_tensor(2)
-        squares(2)
+        for step in range(1, AHEAD):
+            squares(step)
         waiting = []
         for step in range(SPLINE_PASSES):
             exponentials(step)
@@ -462,61 +469,55 @@ def tile_kan1_pb_kernel(tc, h_mix, x, fc2_spline_w, fc2_base_w, fc2_base_b, out)
             pack_weights(step)
             if step == SHIFT_AFTER:
                 clamp(1)
-                shift(1)
             squares(step + AHEAD)
             quantise(step)
+            quantise_weights(step)
+            if step == SHIFT_AFTER:
+                shift(1)
             half, done = divmod(step, ROW_TILES)
             for late, m in waiting[:PASSES_A_STEP]:
-                multiply(late, tiles=(m,))
+                multiply(late, groups[0][m])
             waiting = waiting[PASSES_A_STEP:]
             waiting += [(step, m) for m in range(done)] + [(late, done) for late in range(half * PAIRS, step + 1)]
         for late, m in waiting:
-            multiply(late, tiles=(m,))
+            multiply(late, groups[0][m])
 
-        HALF = CHUNK // 2
 
         def passes(step):
             ch, k_pass = divmod(step, SPLINE_PASSES)
-            if ch + 1 < CHUNKS:
-                spans = [(0, CHUNK, 0, 2, 0), (0, CHUNK, 2, 4, FINISH_AFTER[0])]
-            else:
-                spans = [
-                    (0, HALF, 0, 2, 0),
-                    (0, HALF, 2, 4, FINISH_AFTER[1]),
-                    (HALF, CHUNK, 0, 2, FINISH_AFTER[1]),
-                    (HALF, CHUNK, 2, 4, SQUARES_OVER),
-                ]
-            for first, last, m0, m1, opened in spans:
-                if k_pass >= opened:
+            opened = FINISH_AFTER[ch - 1]
+            for group in groups[ch][:2]:
+                multiply(step, group)
+            if k_pass >= opened:
+                for group in groups[ch][2:]:
                     for late in range(step - k_pass if k_pass == opened else step, step + 1):
-                        multiply(late, first, last, range(m0, m1))
+                        multiply(late, group)
 
         for step in range(SPLINE_PASSES, STEPS - 1):
             ch, k_pass = divmod(step, SPLINE_PASSES)
             exponentials(step)
             squares_ahead(step)
-            if k_pass == SHIFT_AFTER and ch + 1 < CHUNKS:
+            shift_now = k_pass == SHIFT_AFTER and ch + 1 < CHUNKS
+            if shift_now:
                 clamp(ch + 1)
-                shift(ch + 1)
             if step + AHEAD < STEPS:
                 squares(step + AHEAD)
             quantise(step)
+            if shift_now:
+                shift(ch + 1)
             if step > SPLINE_PASSES:
                 passes(step - 1)
             if k_pass == FINISH_AFTER[ch - 1]:
-                for m in range(ROW_TILES):
-                    finish(ch - 1, m)
+                for group in groups[ch - 1]:
+                    finish(ch - 1, group)
         passes(STEPS - 2)
 
         exponentials(STEPS - 1, 0, HALF)
         exponentials(STEPS - 1, HALF, CHUNK)
-        quantise(STEPS - 1, 0, HALF)
-        multiply(STEPS - 1, 0, HALF)
-        for m in range(2):
-            finish(CHUNKS - 1, m, 0, HALF)
-        quantise(STEPS - 1, HALF, CHUNK)
-        multiply(STEPS - 1, HALF, CHUNK)
-        for m in range(2, ROW_TILES):
-            finish(CHUNKS - 1, m, 0, HALF)
-        for m in range(ROW_TILES):
-            finish(CHUNKS - 1, m, HALF, CHUNK)
+        last_groups = groups[CHUNKS - 1]
+        for first, part in ((0, last_groups[:2]), (HALF, last_groups[2:])):
+            quantise(STEPS - 1, first, first + HALF)
+            for group in part:
+                multiply(STEPS - 1, group)
+            for group in part:
+                finish(CHUNKS - 1, group)

@@ -41,11 +41,12 @@ EARLY_SLABS = 2
 W_JOB = HIDDEN * CENTRES // HALVES
 SORTED_BY_LOAD = 4
 JOBS = HALVES * ROW_TILES
+QUANTISE_FIRST = STEPS - 4
 AHEAD = 2
-SCALAR_COLS = CHUNK // 2
-FIRST_SHARE = 3
+SCALAR_COLS = 3 * CHUNK // 4
+FIRST_SHARE = 4
 FIRST_TURN = 1
-PASSES_A_STEP = 4
+PASSES_A_STEP = 3
 BASIS_BUFS = 4
 SQUARE_BUFS = AHEAD + 2
 CODE_BUFS = 9
@@ -111,12 +112,6 @@ def tile_kan1_pb_kernel(tc, h_mix, x, fc2_spline_w, fc2_base_w, fc2_base_b, out)
                         in_=w_rows.rearrange("q (a c s) -> q c a s", c=4, s=32)[:, c, :, :],
                     )
             w_nat.append(w_tile)
-        x_sb = keep.tile([P, ROW_TILES * COLS], BF16)
-        for m in range(ROW_TILES):
-            nc.sync.dma_start(
-                out=x_sb[:, m * COLS : (m + 1) * COLS].rearrange("q (b c) -> q b c", b=BATCH),
-                in_=x[:, m * P : (m + 1) * P, :].rearrange("b q c -> q b c"),
-            )
 
         ident_f32 = keep.tile([P, P], F32)
         make_identity(nc, ident_f32[:])
@@ -152,7 +147,7 @@ def tile_kan1_pb_kernel(tc, h_mix, x, fc2_spline_w, fc2_base_w, fc2_base_b, out)
 
         h_perm = {}
         hidden = []
-        silu_grouped = []
+        silu_grouped = keep.tile([P, PACK * COLS], BF16, align_bytes=64, tag="silu_then_x", name="silu_grouped")
 
         def permute_hidden(slab):
             words = SLAB_TILES[slab] * HALVES * P
@@ -170,9 +165,6 @@ def tile_kan1_pb_kernel(tc, h_mix, x, fc2_spline_w, fc2_base_w, fc2_base_b, out)
             ch = n0 // CHUNK
             if n0 % CHUNK == 0:
                 hidden.append(keep.tile([P, PACK * CHUNK], BF16, name="hidden%d" % ch))
-                silu_grouped.append(
-                    ring.tile([P, PACK * CHUNK], BF16, align_bytes=64, tag="grouped", name="silu_grouped")
-                )
             return ch, slice(n0 - ch * CHUNK, n1 - ch * CHUNK)
 
         def copy_hidden(slab, ch, n_cols):
@@ -187,7 +179,9 @@ def tile_kan1_pb_kernel(tc, h_mix, x, fc2_spline_w, fc2_base_w, fc2_base_b, out)
 
         def silu(ch, n_cols, source):
             nc.scalar.activation(
-                out=silu_grouped[ch][:].rearrange("p (n h u) -> p n h u", h=HALVES, u=2)[:, n_cols, :, :],
+                out=silu_grouped[:, ch * PACK * CHUNK : (ch + 1) * PACK * CHUNK].rearrange(
+                    "p (n h u) -> p n h u", h=HALVES, u=2
+                )[:, n_cols, :, :],
                 in_=source,
                 func=ACT.Silu,
             )
@@ -327,10 +321,17 @@ def tile_kan1_pb_kernel(tc, h_mix, x, fc2_spline_w, fc2_base_w, fc2_base_b, out)
         squares_on_tensor(1)
         silu_codes = keep.tile([P, COLS], U32, align_bytes=64)
         silu_scales = keep.tile([P, COLS], U8, align_bytes=64)
-        for ch in range(CHUNKS):
-            n_cols = slice(ch * CHUNK, (ch + 1) * CHUNK)
+        for n0, n1 in ((0, 2 * CHUNK), (2 * CHUNK, COLS)):
             nc.vector.quantize_mx(
-                out=silu_codes[:, n_cols].bitcast(FP8X4), scales=silu_scales[:, n_cols], in_=silu_grouped[ch][:]
+                out=silu_codes[:, n0:n1].bitcast(FP8X4),
+                scales=silu_scales[:, n0:n1],
+                in_=silu_grouped[:, PACK * n0 : PACK * n1],
+            )
+        x_sb = keep.tile([P, ROW_TILES * COLS], BF16, align_bytes=64, tag="silu_then_x", name="x_sb")
+        for m in range(ROW_TILES):
+            nc.sync.dma_start(
+                out=x_sb[:, m * COLS : (m + 1) * COLS].rearrange("q (b c) -> q b c", b=BATCH),
+                in_=x[:, m * P : (m + 1) * P, :].rearrange("b q c -> q b c"),
             )
         bw_grouped = ring.tile([P, ROW_TILES * PACK * P], BF16, align_bytes=64, tag="grouped")
         for m_pair in range(2):
@@ -500,9 +501,12 @@ def tile_kan1_pb_kernel(tc, h_mix, x, fc2_spline_w, fc2_base_w, fc2_base_b, out)
             shift_now = k_pass == SHIFT_AFTER and ch + 1 < CHUNKS
             if shift_now:
                 clamp(ch + 1)
+            if step >= QUANTISE_FIRST:
+                quantise(step)
             if step + AHEAD < STEPS:
                 squares(step + AHEAD)
-            quantise(step)
+            if step < QUANTISE_FIRST:
+                quantise(step)
             if shift_now:
                 shift(ch + 1)
             if step > SPLINE_PASSES:
@@ -519,5 +523,5 @@ def tile_kan1_pb_kernel(tc, h_mix, x, fc2_spline_w, fc2_base_w, fc2_base_b, out)
             quantise(STEPS - 1, first, first + HALF)
             for group in part:
                 multiply(STEPS - 1, group)
-            for group in part:
-                finish(CHUNKS - 1, group)
+        for group in last_groups:
+            finish(CHUNKS - 1, group)

@@ -41,12 +41,13 @@ EARLY_SLABS = 2
 W_JOB = HIDDEN * CENTRES // HALVES
 SORTED_BY_LOAD = 4
 JOBS = HALVES * ROW_TILES
-QUANTISE_FIRST = STEPS - 4
+QUANTISE_FIRST = 20
 AHEAD = 2
-SCALAR_COLS = 3 * CHUNK // 4
+TENSOR_FROM = 2
+SCALAR_STEPS = (8, 12, 20)
 FIRST_SHARE = 4
 FIRST_TURN = 1
-PASSES_A_STEP = 3
+PASSES_A_STEP = 2
 BASIS_BUFS = 4
 SQUARE_BUFS = AHEAD + 2
 CODE_BUFS = 9
@@ -223,7 +224,7 @@ def tile_kan1_pb_kernel(tc, h_mix, x, fc2_spline_w, fc2_base_w, fc2_base_b, out)
         acc = {}
 
         def on_tensor(step):
-            return step % PAIRS > 0
+            return step % PAIRS >= TENSOR_FROM
 
         tensor_square = {}
 
@@ -254,7 +255,7 @@ def tile_kan1_pb_kernel(tc, h_mix, x, fc2_spline_w, fc2_base_w, fc2_base_b, out)
             if step < SPLINE_PASSES:
                 scalar_end = tensor_end if step % FIRST_SHARE == FIRST_TURN else CHUNK
             else:
-                scalar_end = tensor_end if on_tensor(step) else SCALAR_COLS
+                scalar_end = CHUNK if step in SCALAR_STEPS else tensor_end
             return {"tensor": (0, tensor_end), "scalar": (tensor_end, scalar_end), "vector": (scalar_end, CHUNK)}
 
         def first_centre(step):
@@ -318,7 +319,6 @@ def tile_kan1_pb_kernel(tc, h_mix, x, fc2_spline_w, fc2_base_w, fc2_base_b, out)
             for m_pair in range(2)
         ]
         squares(0)
-        squares_on_tensor(1)
         silu_codes = keep.tile([P, COLS], U32, align_bytes=64)
         silu_scales = keep.tile([P, COLS], U8, align_bytes=64)
         for n0, n1 in ((0, 2 * CHUNK), (2 * CHUNK, COLS)):
@@ -519,9 +519,12 @@ def tile_kan1_pb_kernel(tc, h_mix, x, fc2_spline_w, fc2_base_w, fc2_base_b, out)
         exponentials(STEPS - 1, 0, HALF)
         exponentials(STEPS - 1, HALF, CHUNK)
         last_groups = groups[CHUNKS - 1]
-        for first, part in ((0, last_groups[:2]), (HALF, last_groups[2:])):
-            quantise(STEPS - 1, first, first + HALF)
-            for group in part:
-                multiply(STEPS - 1, group)
-        for group in last_groups:
+        quantise(STEPS - 1, 0, HALF)
+        for group in last_groups[:2]:
+            multiply(STEPS - 1, group)
+        finish(CHUNKS - 1, last_groups[0])
+        quantise(STEPS - 1, HALF, CHUNK)
+        for group in last_groups[2:]:
+            multiply(STEPS - 1, group)
+        for group in last_groups[1:]:
             finish(CHUNKS - 1, group)

@@ -30,14 +30,15 @@ PASSES = SPLINE_PASSES + 1
 STEPS = CHUNKS * SPLINE_PASSES
 PER_CENTRE = CHUNK * PACK // 2
 WORD_GROUPS = 8
-SLAB_TILES = (1, 1, 2, 2, 2, 2, 2)
+SLAB_TILES = (1, 1, 1, 1, 2, 2, 2, 2)
 SQUARE_BANKS = (6, 7)
 SUM_BANKS = 6
 TENSOR_COLS = CHUNK // 4
 CLAMP = 16384.0
-HEAD_BANKS = 4
+HEAD_BANKS = 6
 WEIGHT_BANKS = 4
-EARLY_SLABS = 2
+EARLY_COPIES_AFTER = 4
+EARLY_SLABS = 1
 W_JOB = HIDDEN * CENTRES // HALVES
 SORTED_BY_LOAD = 4
 JOBS = HALVES * ROW_TILES
@@ -212,7 +213,7 @@ def tile_kan1_pb_kernel(tc, h_mix, x, fc2_spline_w, fc2_base_w, fc2_base_b, out)
             ch, n_cols = place(slab)
             copy_hidden(slab, ch, n_cols)
             silu(ch, n_cols, n_h_u(hidden[ch][:])[:, n_cols, :, :])
-            if slab == EARLY_SLABS:
+            if slab == EARLY_COPIES_AFTER:
                 for early in range(EARLY_SLABS):
                     copy_hidden(early, *places[early])
         clamp(0)

@@ -40,14 +40,13 @@ WEIGHT_BANKS = 4
 EARLY_COPIES_AFTER = 4
 EARLY_SLABS = 1
 W_JOB = HIDDEN * CENTRES // HALVES
-SORTED_BY_LOAD = 4
+SORTED_BY_LOAD = 3
 JOBS = HALVES * ROW_TILES
 QUANTISE_FIRST = 20
+FIRST_VECTOR_STEPS = (1, 3, 7)
 AHEAD = 2
 TENSOR_FROM = 2
 SCALAR_STEPS = (8, 12, 20)
-FIRST_SHARE = 4
-FIRST_TURN = 1
 PASSES_A_STEP = 2
 BASIS_BUFS = 4
 SQUARE_BUFS = AHEAD + 2
@@ -130,13 +129,14 @@ def tile_kan1_pb_kernel(tc, h_mix, x, fc2_spline_w, fc2_base_w, fc2_base_b, out)
             out=curve[:], in0=ident_f32[:], scalar1=1.0 / (SPACING * SPACING), scalar2=0.0, op0=ALU.mult, op1=ALU.add
         )
         slopes = {}
+        levels = {}
         for pi in range(1, PAIRS):
-            slopes[pi] = []
-            for e, ident in enumerate((ident_bf16, ident_f32)):
-                slopes[pi].append(keep.tile([P, P], (BF16, F32)[e], name="slope%d%d" % (pi, e)))
-                nc.gpsimd.tensor_scalar(
-                    out=slopes[pi][e][:], in0=ident[:], scalar1=-4.0 * pi / SPACING, scalar2=0.0, op0=ALU.mult, op1=ALU.add
-                )
+            slopes[pi] = keep.tile([P, P], BF16, name="slope%d" % pi)
+            nc.gpsimd.tensor_scalar(
+                out=slopes[pi][:], in0=ident_bf16[:], scalar1=-4.0 * pi / SPACING, scalar2=0.0, op0=ALU.mult, op1=ALU.add
+            )
+            levels[pi] = keep.tile([P, 2 * TENSOR_COLS], BF16, name="level%d" % pi)
+            nc.gpsimd.memset(levels[pi][:], 4.0 * pi)
 
         def turn(b, groups):
             bank = psum_bank(b)
@@ -242,19 +242,20 @@ def tile_kan1_pb_kernel(tc, h_mix, x, fc2_spline_w, fc2_base_w, fc2_base_b, out)
                 start=True,
                 stop=False,
             )
-            for e, source in enumerate((hidden[ch], shifted[ch])):
+            for e in range(2):
                 nc.tensor.matmul(
                     bank[:, e * cols : (e + 1) * cols],
-                    lhsT=slopes[pi][e][:],
-                    rhs=source[:, half * PER_CENTRE : half * PER_CENTRE + cols],
+                    lhsT=slopes[pi][:],
+                    rhs=hidden[ch][:, half * PER_CENTRE : half * PER_CENTRE + cols],
                     start=False,
-                    stop=(e == 1),
+                    stop=False,
                 )
+            nc.tensor.matmul(bank[:, cols : 2 * cols], lhsT=ident_bf16[:], rhs=levels[pi][:], start=False, stop=True)
 
         def shares(step):
             tensor_end = TENSOR_COLS if on_tensor(step) else 0
             if step < SPLINE_PASSES:
-                scalar_end = tensor_end if step % FIRST_SHARE == FIRST_TURN else CHUNK
+                scalar_end = tensor_end if step in FIRST_VECTOR_STEPS else CHUNK
             else:
                 scalar_end = CHUNK if step in SCALAR_STEPS else tensor_end
             return {"tensor": (0, tensor_end), "scalar": (tensor_end, scalar_end), "vector": (scalar_end, CHUNK)}

@@ -30,7 +30,7 @@ PASSES = SPLINE_PASSES + 1
 STEPS = CHUNKS * SPLINE_PASSES
 PER_CENTRE = CHUNK * PACK // 2
 WORD_GROUPS = 8
-SLAB_TILES = (1, 1, 1, 1, 2, 2, 2, 2)
+SLAB_TILES = (1, 1, 2, 2, 2, 2, 2)
 SQUARE_BANKS = (6, 7)
 SUM_BANKS = 6
 TENSOR_COLS = CHUNK // 4
@@ -46,7 +46,7 @@ QUANTISE_FIRST = 20
 FIRST_VECTOR_STEPS = (1, 3, 7)
 AHEAD = 2
 TENSOR_FROM = 2
-SCALAR_STEPS = (8, 12, 20)
+SCALAR_COLS = (CHUNK, CHUNK // 2)
 PASSES_A_STEP = 2
 BASIS_BUFS = 4
 SQUARE_BUFS = AHEAD + 2
@@ -257,7 +257,7 @@ def tile_kan1_pb_kernel(tc, h_mix, x, fc2_spline_w, fc2_base_w, fc2_base_b, out)
             if step < SPLINE_PASSES:
                 scalar_end = tensor_end if step in FIRST_VECTOR_STEPS else CHUNK
             else:
-                scalar_end = CHUNK if step in SCALAR_STEPS else tensor_end
+                scalar_end = tensor_end if step % PAIRS else SCALAR_COLS[step // SPLINE_PASSES - 1]
             return {"tensor": (0, tensor_end), "scalar": (tensor_end, scalar_end), "vector": (scalar_end, CHUNK)}
 
         def first_centre(step):

@@ -43,13 +43,13 @@ W_JOB = HIDDEN * CENTRES // HALVES
 SORTED_BY_LOAD = 3
 JOBS = HALVES * ROW_TILES
 QUANTISE_FIRST = 20
-FIRST_VECTOR_STEPS = (1, 3, 7)
+FIRST_VECTOR_STEPS = (1, 3, 5, 7)
+TENSOR_PAIRS = ((1, 2, 3), (1, 2, 3), (1, 2, 3))
 AHEAD = 2
-TENSOR_FROM = 2
-SCALAR_COLS = (CHUNK, CHUNK // 2)
+SCALAR_COLS = (384, 256)
 PASSES_A_STEP = 2
 BASIS_BUFS = 4
-SQUARE_BUFS = AHEAD + 2
+SQUARE_BUFS = AHEAD + 1
 CODE_BUFS = 9
 SHIFT_AFTER = 3
 FINISH_AFTER = (1, 0)
@@ -58,6 +58,14 @@ assert JOBS == SPLINE_PASSES
 assert SHIFT_AFTER < SPLINE_PASSES - AHEAD
 
 FLOPS = 2 * COLS * ROWS * (HIDDEN * CENTRES + HIDDEN)
+
+
+def on_tensor(step):
+    return step % PAIRS in TENSOR_PAIRS[step // SPLINE_PASSES]
+
+
+def units(pi, e):
+    return 2.0 * pi + e - (CENTRES - 1) / 2.0
 
 
 def unit_order(words):
@@ -124,19 +132,21 @@ def tile_kan1_pb_kernel(tc, h_mix, x, fc2_spline_w, fc2_base_w, fc2_base_b, out)
         warm_out = keep.tile([P, 1], F32)
         nc.scalar.activation(out=warm_out[:], in_=warm_in[:], func=ACT.Silu)
 
-        curve = keep.tile([P, P], F32)
-        nc.gpsimd.tensor_scalar(
-            out=curve[:], in0=ident_f32[:], scalar1=1.0 / (SPACING * SPACING), scalar2=0.0, op0=ALU.mult, op1=ALU.add
-        )
         slopes = {}
         levels = {}
-        for pi in range(1, PAIRS):
-            slopes[pi] = keep.tile([P, P], BF16, name="slope%d" % pi)
-            nc.gpsimd.tensor_scalar(
-                out=slopes[pi][:], in0=ident_bf16[:], scalar1=-4.0 * pi / SPACING, scalar2=0.0, op0=ALU.mult, op1=ALU.add
-            )
+        for pi in range(PAIRS):
+            for e in range(2):
+                slopes[pi, e] = keep.tile([P, P], BF16, name="slope%d_%d" % (pi, e))
+                nc.gpsimd.tensor_scalar(
+                    out=slopes[pi, e][:],
+                    in0=ident_bf16[:],
+                    scalar1=-2.0 * units(pi, e) / SPACING,
+                    scalar2=0.0,
+                    op0=ALU.mult,
+                    op1=ALU.add,
+                )
             levels[pi] = keep.tile([P, 2 * TENSOR_COLS], BF16, name="level%d" % pi)
-            nc.gpsimd.memset(levels[pi][:], 4.0 * pi)
+            nc.gpsimd.memset(levels[pi][:], units(pi, 1) ** 2 - units(pi, 0) ** 2)
 
         def turn(b, groups):
             bank = psum_bank(b)
@@ -155,6 +165,20 @@ def tile_kan1_pb_kernel(tc, h_mix, x, fc2_spline_w, fc2_base_w, fc2_base_b, out)
             words = SLAB_TILES[slab] * HALVES * P
             h_perm[slab] = ring.tile([P, words], F32, name="h_perm", bufs=3)
             nc.vector.tensor_copy(out=partition_order(h_perm[slab][:]), in_=unit_order(h_nat[slab][:].bitcast(F32)))
+
+        plain_square = {}
+
+        def square_plainly(slab):
+            n0 = slab_cols[slab][0]
+            if n0 % CHUNK == 0:
+                ch = n0 // CHUNK
+                plain_square[ch] = keep.tile([P, HIDDEN], F32, name="plain_square%d" % ch)
+                nc.scalar.activation(
+                    out=plain_square[ch][:].rearrange("n (h u p) -> n h u p", h=HALVES, u=2),
+                    in_=h_perm[slab][:, 0 : HALVES * P].bitcast(BF16).rearrange("n (h p u) -> n h u p", h=HALVES, u=2),
+                    func=ACT.Square,
+                    scale=1.0 / SPACING,
+                )
 
         h_banks = {}
 
@@ -196,13 +220,15 @@ def tile_kan1_pb_kernel(tc, h_mix, x, fc2_spline_w, fc2_base_w, fc2_base_b, out)
 
         def shift(ch):
             shifted[ch] = ring.tile([P, PACK * CHUNK], F32, name="shifted", bufs=2)
-            nc.vector.tensor_scalar_add(out=shifted[ch][:], in0=hidden[ch][:], scalar1=-SPACING)
+            some = [t[:].rearrange("p (h v) -> p h v", h=HALVES)[:, :, 2 * TENSOR_COLS :] for t in (shifted[ch], hidden[ch])]
+            nc.vector.tensor_scalar_add(out=some[0], in0=some[1], scalar1=-SPACING)
 
         for slab in range(EARLY_SLABS + 1):
             permute_hidden(slab)
         places = []
         for slab in range(EARLY_SLABS):
             turn_hidden(slab)
+            square_plainly(slab)
             places.append(place(slab))
             words = SLAB_TILES[slab] * HALVES * P
             silu(*places[slab], n_h_u(h_banks[slab][:, :words].bitcast(BF16)))
@@ -210,6 +236,7 @@ def tile_kan1_pb_kernel(tc, h_mix, x, fc2_spline_w, fc2_base_w, fc2_base_b, out)
             if slab + 1 < len(SLAB_TILES):
                 permute_hidden(slab + 1)
             turn_hidden(slab)
+            square_plainly(slab)
             ch, n_cols = place(slab)
             copy_hidden(slab, ch, n_cols)
             silu(ch, n_cols, n_h_u(hidden[ch][:])[:, n_cols, :, :])
@@ -224,8 +251,11 @@ def tile_kan1_pb_kernel(tc, h_mix, x, fc2_spline_w, fc2_base_w, fc2_base_b, out)
         scales = {}
         acc = {}
 
-        def on_tensor(step):
-            return step % PAIRS >= TENSOR_FROM
+        TENSOR_STEPS = [step for step in range(STEPS) if on_tensor(step)]
+
+        def start_of(step):
+            i = TENSOR_STEPS.index(step)
+            return max(TENSOR_STEPS[i - 2], step - 3) if i >= 2 else -1
 
         tensor_square = {}
 
@@ -233,19 +263,23 @@ def tile_kan1_pb_kernel(tc, h_mix, x, fc2_spline_w, fc2_base_w, fc2_base_b, out)
             ch, k_pass = divmod(step, SPLINE_PASSES)
             half, pi = divmod(k_pass, PAIRS)
             cols = 2 * TENSOR_COLS
-            bank = psum_bank(SQUARE_BANKS[step % 2])
+            bank = psum_bank(SQUARE_BANKS[TENSOR_STEPS.index(step) % 2])
             tensor_square[step] = bank
-            nc.tensor.matmul(
-                bank[:].rearrange("p (e v) -> p e v", e=2),
-                lhsT=curve[:],
-                rhs=square[step - pi][:].rearrange("p (e v) -> p e v", e=2)[:, :, 0:cols],
-                start=True,
-                stop=False,
-            )
+            for e in range(2):
+                for u in range(2):
+                    place = (2 * half + u) * P
+                    nc.tensor.matmul(
+                        bank[:].rearrange("p (e n u) -> p e n u", e=2, u=2)[:, e, :, u],
+                        lhsT=plain_square[ch][:, place : place + P],
+                        rhs=ident_f32[:],
+                        is_transpose=True,
+                        start=(e == 0 and u == 0),
+                        stop=False,
+                    )
             for e in range(2):
                 nc.tensor.matmul(
                     bank[:, e * cols : (e + 1) * cols],
-                    lhsT=slopes[pi][:],
+                    lhsT=slopes[pi, e][:],
                     rhs=hidden[ch][:, half * PER_CENTRE : half * PER_CENTRE + cols],
                     start=False,
                     stop=False,
@@ -255,9 +289,9 @@ def tile_kan1_pb_kernel(tc, h_mix, x, fc2_spline_w, fc2_base_w, fc2_base_b, out)
         def shares(step):
             tensor_end = TENSOR_COLS if on_tensor(step) else 0
             if step < SPLINE_PASSES:
-                scalar_end = tensor_end if step in FIRST_VECTOR_STEPS else CHUNK
+                scalar_end = TENSOR_COLS if step in FIRST_VECTOR_STEPS else CHUNK
             else:
-                scalar_end = tensor_end if step % PAIRS else SCALAR_COLS[step // SPLINE_PASSES - 1]
+                scalar_end = TENSOR_COLS if step % PAIRS else SCALAR_COLS[step // SPLINE_PASSES - 1]
             return {"tensor": (0, tensor_end), "scalar": (tensor_end, scalar_end), "vector": (scalar_end, CHUNK)}
 
         def first_centre(step):
@@ -377,11 +411,7 @@ def tile_kan1_pb_kernel(tc, h_mix, x, fc2_spline_w, fc2_base_w, fc2_base_b, out)
         def rest(step, engine):
             if engine == "scalar":
                 return 0.0
-            if engine == "vector":
-                return (first_centre(step) / SPACING) ** 2
-            pi = step % PAIRS
-            maker = "scalar" if shares(step - pi)["scalar"][1] > 0 else "vector"
-            return 4.0 * pi * pi - 4.0 * pi / SPACING + rest(step - pi, maker)
+            return units(step % PAIRS, 0) ** 2
 
         def exponentials(step, first=0, last=CHUNK):
             if first == 0:
@@ -452,17 +482,17 @@ def tile_kan1_pb_kernel(tc, h_mix, x, fc2_spline_w, fc2_base_w, fc2_base_b, out)
                 )
 
         def squares_ahead(step):
-            pi = step % PAIRS
-            for ahead in {PAIRS - 1: (2, 3), 1: (2,)}.get(pi, ()):
-                if step + ahead < STEPS and on_tensor(step + ahead):
-                    squares_on_tensor(step + ahead)
+            for later in TENSOR_STEPS:
+                if start_of(later) == step:
+                    squares_on_tensor(later)
 
+        for step in TENSOR_STEPS[:2]:
+            squares_on_tensor(step)
         turn_weights(0)
         base_cols = slice(SPLINE_PASSES * ROW_TILES * P, PASSES * ROW_TILES * P)
         nc.vector.quantize_mx(
             out=w_codes[:, base_cols].bitcast(FP8X4), scales=w_scales[:, base_cols], in_=bw_grouped[:]
         )
-        squares_on_tensor(2)
         for step in range(1, AHEAD):
             squares(step)
         waiting = []
@@ -482,8 +512,6 @@ def tile_kan1_pb_kernel(tc, h_mix, x, fc2_spline_w, fc2_base_w, fc2_base_b, out)
                 multiply(late, groups[0][m])
             waiting = waiting[PASSES_A_STEP:]
             waiting += [(step, m) for m in range(done)] + [(late, done) for late in range(half * PAIRS, step + 1)]
-        for late, m in waiting:
-            multiply(late, groups[0][m])
 
 
         def passes(step):
@@ -500,6 +528,9 @@ def tile_kan1_pb_kernel(tc, h_mix, x, fc2_spline_w, fc2_base_w, fc2_base_b, out)
             ch, k_pass = divmod(step, SPLINE_PASSES)
             exponentials(step)
             squares_ahead(step)
+            for late, m in waiting:
+                multiply(late, groups[0][m])
+            waiting = []
             shift_now = k_pass == SHIFT_AFTER and ch + 1 < CHUNKS
             if shift_now:
                 clamp(ch + 1)

@@ -269,7 +269,7 @@ def tile_kan1_pb_kernel(tc, h_mix, x, fc2_spline_w, fc2_base_w, fc2_base_b, out)
                 for u in range(2):
                     place = (2 * half + u) * P
                     nc.tensor.matmul(
-                        bank[:].rearrange("p (e n u) -> p e n u", e=2, u=2)[:, e, :, u],
+                        bank[:, (2 * e + u) * P : (2 * e + u + 1) * P],
                         lhsT=plain_square[ch][:, place : place + P],
                         rhs=ident_f32[:],
                         is_transpose=True,
@@ -278,9 +278,9 @@ def tile_kan1_pb_kernel(tc, h_mix, x, fc2_spline_w, fc2_base_w, fc2_base_b, out)
                     )
             for e in range(2):
                 nc.tensor.matmul(
-                    bank[:, e * cols : (e + 1) * cols],
+                    bank[:, e * cols : (e + 1) * cols].rearrange("p (u n) -> p u n", u=2),
                     lhsT=slopes[pi, e][:],
-                    rhs=hidden[ch][:, half * PER_CENTRE : half * PER_CENTRE + cols],
+                    rhs=hidden[ch][:, half * PER_CENTRE : half * PER_CENTRE + cols].rearrange("p (n u) -> p u n", u=2),
                     start=False,
                     stop=False,
                 )
@@ -421,10 +421,13 @@ def tile_kan1_pb_kernel(tc, h_mix, x, fc2_spline_w, fc2_base_w, fc2_base_b, out)
             for engine, (begin, end) in shares(step).items():
                 begin, end = max(begin, first), min(end, last)
                 if begin < end:
-                    source = tensor_square[step] if engine == "tensor" else square[step]
+                    if engine == "tensor":
+                        source = tensor_square[step][:].rearrange("p (e u n) -> p n u e", e=2, u=2)[:, begin:end, :, :]
+                    else:
+                        source = square[step][:].rearrange("p (e n u) -> p n u e", e=2, u=2)[:, begin:end, :, :]
                     nc.scalar.activation(
-                        out=basis[step][:].rearrange("p (v e) -> p v e", e=2)[:, 2 * begin : 2 * end, :],
-                        in_=source[:].rearrange("p (e v) -> p v e", e=2)[:, 2 * begin : 2 * end, :],
+                        out=basis[step][:].rearrange("p (n u e) -> p n u e", u=2, e=2)[:, begin:end, :, :],
+                        in_=source,
                         func=ACT.Exp,
                         bias=-rest(step, engine),
                         scale=-1.0 if engine == "tensor" else -1.0 / (SPACING * SPACING),

@@ -1,3 +1,4 @@
+import math
 from contextlib import ExitStack
 
 import concourse.mybir as mybir
@@ -34,7 +35,7 @@ SLAB_TILES = (1, 1, 2, 2, 2, 2, 2)
 SQUARE_BANKS = (6, 7)
 SUM_BANKS = 6
 TENSOR_COLS = CHUNK // 4
-CLAMP = 16384.0
+TENSOR_UNIT = 64.0
 HEAD_BANKS = 6
 WEIGHT_BANKS = 4
 EARLY_COPIES_AFTER = 4
@@ -43,8 +44,8 @@ W_JOB = HIDDEN * CENTRES // HALVES
 SORTED_BY_LOAD = 3
 JOBS = HALVES * ROW_TILES
 QUANTISE_FIRST = 20
-FIRST_VECTOR_STEPS = (1, 3, 5, 7)
-TENSOR_PAIRS = ((1, 2, 3), (1, 2, 3), (1, 2, 3))
+FIRST_VECTOR_STEPS = (1, 3, 7)
+TENSOR_PAIRS = ((0,1,2,3),(0,1,2,3),(0,1,2,3))
 AHEAD = 2
 SCALAR_COLS = (384, 256)
 PASSES_A_STEP = 2
@@ -140,13 +141,13 @@ def tile_kan1_pb_kernel(tc, h_mix, x, fc2_spline_w, fc2_base_w, fc2_base_b, out)
                 nc.gpsimd.tensor_scalar(
                     out=slopes[pi, e][:],
                     in0=ident_bf16[:],
-                    scalar1=-2.0 * units(pi, e) / SPACING,
+                    scalar1=-2.0 * units(pi, e) / (SPACING * TENSOR_UNIT),
                     scalar2=0.0,
                     op0=ALU.mult,
                     op1=ALU.add,
                 )
             levels[pi] = keep.tile([P, 2 * TENSOR_COLS], BF16, name="level%d" % pi)
-            nc.gpsimd.memset(levels[pi][:], units(pi, 1) ** 2 - units(pi, 0) ** 2)
+            nc.gpsimd.memset(levels[pi][:], (units(pi, 1) ** 2 - units(pi, 0) ** 2) / TENSOR_UNIT)
 
         def turn(b, groups):
             bank = psum_bank(b)
@@ -177,7 +178,7 @@ def tile_kan1_pb_kernel(tc, h_mix, x, fc2_spline_w, fc2_base_w, fc2_base_b, out)
                     out=plain_square[ch][:].rearrange("n (h u p) -> n h u p", h=HALVES, u=2),
                     in_=h_perm[slab][:, 0 : HALVES * P].bitcast(BF16).rearrange("n (h p u) -> n h u p", h=HALVES, u=2),
                     func=ACT.Square,
-                    scale=1.0 / SPACING,
+                    scale=1.0 / (SPACING * math.sqrt(TENSOR_UNIT)),
                 )
 
         h_banks = {}
@@ -212,10 +213,6 @@ def tile_kan1_pb_kernel(tc, h_mix, x, fc2_spline_w, fc2_base_w, fc2_base_b, out)
                 func=ACT.Silu,
             )
 
-        def clamp(ch):
-            some = hidden[ch][:].rearrange("p (h v) -> p h v", h=HALVES)[:, :, 0 : 2 * TENSOR_COLS]
-            nc.vector.tensor_scalar(out=some, in0=some, scalar1=-CLAMP, scalar2=CLAMP, op0=ALU.max, op1=ALU.min)
-
         shifted = {}
 
         def shift(ch):
@@ -243,7 +240,6 @@ def tile_kan1_pb_kernel(tc, h_mix, x, fc2_spline_w, fc2_base_w, fc2_base_b, out)
             if slab == EARLY_COPIES_AFTER:
                 for early in range(EARLY_SLABS):
                     copy_hidden(early, *places[early])
-        clamp(0)
 
         square = {}
         basis = {}
@@ -430,7 +426,7 @@ def tile_kan1_pb_kernel(tc, h_mix, x, fc2_spline_w, fc2_base_w, fc2_base_b, out)
                         in_=source,
                         func=ACT.Exp,
                         bias=-rest(step, engine),
-                        scale=-1.0 if engine == "tensor" else -1.0 / (SPACING * SPACING),
+                        scale=-TENSOR_UNIT if engine == "tensor" else -1.0 / (SPACING * SPACING),
                     )
 
         def quantise(step, first=0, last=CHUNK):
@@ -503,8 +499,6 @@ def tile_kan1_pb_kernel(tc, h_mix, x, fc2_spline_w, fc2_base_w, fc2_base_b, out)
             exponentials(step)
             squares_ahead(step)
             pack_weights(step)
-            if step == SHIFT_AFTER:
-                clamp(1)
             squares(step + AHEAD)
             quantise(step)
             quantise_weights(step)
@@ -535,8 +529,6 @@ def tile_kan1_pb_kernel(tc, h_mix, x, fc2_spline_w, fc2_base_w, fc2_base_b, out)
                 multiply(late, groups[0][m])
             waiting = []
             shift_now = k_pass == SHIFT_AFTER and ch + 1 < CHUNKS
-            if shift_now:
-                clamp(ch + 1)
             if step >= QUANTISE_FIRST:
                 quantise(step)
             if step + AHEAD < STEPS:

@@ -32,7 +32,7 @@ STEPS = CHUNKS * SPLINE_PASSES
 PER_CENTRE = CHUNK * PACK // 2
 WORD_GROUPS = 8
 SLAB_TILES = (1, 1, 2, 2, 2, 2, 2)
-SQUARE_BANKS = (6, 7)
+SQUARE_BANKS = ((6, 7), (2, 3))
 SUM_BANKS = 6
 TENSOR_COLS = CHUNK // 4
 TENSOR_UNIT = 64.0
@@ -44,11 +44,11 @@ W_JOB = HIDDEN * CENTRES // HALVES
 SORTED_BY_LOAD = 3
 JOBS = HALVES * ROW_TILES
 QUANTISE_FIRST = 20
-FIRST_VECTOR_STEPS = (1, 3, 7)
-TENSOR_PAIRS = ((0,1,2,3),(0,1,2,3),(0,1,2,3))
+FIRST_VECTOR_STEPS = (1, 3, 6)
+EARLY_BLOCKS = 4
 AHEAD = 2
-SCALAR_COLS = (384, 256)
-PASSES_A_STEP = 2
+SCALAR_COLS = (384, 320)
+PASSES_A_STEP = 3
 BASIS_BUFS = 4
 SQUARE_BUFS = AHEAD + 1
 CODE_BUFS = 9
@@ -59,10 +59,6 @@ assert JOBS == SPLINE_PASSES
 assert SHIFT_AFTER < SPLINE_PASSES - AHEAD
 
 FLOPS = 2 * COLS * ROWS * (HIDDEN * CENTRES + HIDDEN)
-
-
-def on_tensor(step):
-    return step % PAIRS in TENSOR_PAIRS[step // SPLINE_PASSES]
 
 
 def units(pi, e):
@@ -158,6 +154,7 @@ def tile_kan1_pb_kernel(tc, h_mix, x, fc2_spline_w, fc2_base_w, fc2_base_b, out)
         def group(words, g):
             return words[:, g * P : (g + 1) * P]
 
+        tensor_blocks = [(step, 0) for step in range(STEPS)] + [(step, 1) for step in range(EARLY_BLOCKS)]
         h_perm = {}
         hidden = []
         silu_grouped = keep.tile([P, PACK * COLS], BF16, align_bytes=64, tag="silu_then_x", name="silu_grouped")
@@ -170,13 +167,13 @@ def tile_kan1_pb_kernel(tc, h_mix, x, fc2_spline_w, fc2_base_w, fc2_base_b, out)
         plain_square = {}
 
         def square_plainly(slab):
-            n0 = slab_cols[slab][0]
-            if n0 % CHUNK == 0:
-                ch = n0 // CHUNK
-                plain_square[ch] = keep.tile([P, HIDDEN], F32, name="plain_square%d" % ch)
+            ch, block = divmod(slab_cols[slab][0] // P, CHUNK // P)
+            halves = sum((ch * SPLINE_PASSES + half * PAIRS, block) in tensor_blocks for half in range(HALVES))
+            if halves:
+                plain_square[ch, block] = keep.tile([P, halves * 2 * P], F32, name="plain_square%d_%d" % (ch, block))
                 nc.scalar.activation(
-                    out=plain_square[ch][:].rearrange("n (h u p) -> n h u p", h=HALVES, u=2),
-                    in_=h_perm[slab][:, 0 : HALVES * P].bitcast(BF16).rearrange("n (h p u) -> n h u p", h=HALVES, u=2),
+                    out=plain_square[ch, block][:].rearrange("n (h u p) -> n h u p", h=halves, u=2),
+                    in_=h_perm[slab][:, 0 : halves * P].bitcast(BF16).rearrange("n (h p u) -> n h u p", h=halves, u=2),
                     func=ACT.Square,
                     scale=1.0 / (SPACING * math.sqrt(TENSOR_UNIT)),
                 )
@@ -247,26 +244,20 @@ def tile_kan1_pb_kernel(tc, h_mix, x, fc2_spline_w, fc2_base_w, fc2_base_b, out)
         scales = {}
         acc = {}
 
-        TENSOR_STEPS = [step for step in range(STEPS) if on_tensor(step)]
-
-        def start_of(step):
-            i = TENSOR_STEPS.index(step)
-            return max(TENSOR_STEPS[i - 2], step - 3) if i >= 2 else -1
-
         tensor_square = {}
 
-        def squares_on_tensor(step):
+        def squares_on_tensor(step, block):
             ch, k_pass = divmod(step, SPLINE_PASSES)
             half, pi = divmod(k_pass, PAIRS)
             cols = 2 * TENSOR_COLS
-            bank = psum_bank(SQUARE_BANKS[TENSOR_STEPS.index(step) % 2])
-            tensor_square[step] = bank
+            bank = psum_bank(SQUARE_BANKS[block][step % 2])
+            tensor_square[step, block] = bank
             for e in range(2):
                 for u in range(2):
                     place = (2 * half + u) * P
                     nc.tensor.matmul(
                         bank[:, (2 * e + u) * P : (2 * e + u + 1) * P],
-                        lhsT=plain_square[ch][:, place : place + P],
+                        lhsT=plain_square[ch, block][:, place : place + P],
                         rhs=ident_f32[:],
                         is_transpose=True,
                         start=(e == 0 and u == 0),
@@ -276,16 +267,16 @@ def tile_kan1_pb_kernel(tc, h_mix, x, fc2_spline_w, fc2_base_w, fc2_base_b, out)
                 nc.tensor.matmul(
                     bank[:, e * cols : (e + 1) * cols].rearrange("p (u n) -> p u n", u=2),
                     lhsT=slopes[pi, e][:],
-                    rhs=hidden[ch][:, half * PER_CENTRE : half * PER_CENTRE + cols].rearrange("p (n u) -> p u n", u=2),
+                    rhs=hidden[ch][:, half * PER_CENTRE + block * cols : half * PER_CENTRE + (block + 1) * cols].rearrange("p (n u) -> p u n", u=2),
                     start=False,
                     stop=False,
                 )
             nc.tensor.matmul(bank[:, cols : 2 * cols], lhsT=ident_bf16[:], rhs=levels[pi][:], start=False, stop=True)
 
         def shares(step):
-            tensor_end = TENSOR_COLS if on_tensor(step) else 0
+            tensor_end = TENSOR_COLS * sum((step, block) in tensor_blocks for block in range(2))
             if step < SPLINE_PASSES:
-                scalar_end = TENSOR_COLS if step in FIRST_VECTOR_STEPS else CHUNK
+                scalar_end = tensor_end if step in FIRST_VECTOR_STEPS else CHUNK
             else:
                 scalar_end = TENSOR_COLS if step % PAIRS else SCALAR_COLS[step // SPLINE_PASSES - 1]
             return {"tensor": (0, tensor_end), "scalar": (tensor_end, scalar_end), "vector": (scalar_end, CHUNK)}
@@ -414,11 +405,15 @@ def tile_kan1_pb_kernel(tc, h_mix, x, fc2_spline_w, fc2_base_w, fc2_base_b, out)
                 basis[step] = ring.tile([P, PACK * CHUNK], BF16, align_bytes=64, name="basis", bufs=BASIS_BUFS)
                 codes[step] = ring.tile([P, CHUNK], U32, align_bytes=64, name="codes", bufs=CODE_BUFS)
                 scales[step] = ring.tile([P, CHUNK], U8, align_bytes=64, name="scales", bufs=CODE_BUFS)
+            pieces = []
             for engine, (begin, end) in shares(step).items():
+                size = TENSOR_COLS if engine == "tensor" else CHUNK
+                pieces += [(engine, c, min(c + size, end)) for c in range(begin, end, size)]
+            for engine, begin, end in pieces:
                 begin, end = max(begin, first), min(end, last)
                 if begin < end:
                     if engine == "tensor":
-                        source = tensor_square[step][:].rearrange("p (e u n) -> p n u e", e=2, u=2)[:, begin:end, :, :]
+                        source = tensor_square[step, begin // TENSOR_COLS][:].rearrange("p (e u n) -> p n u e", e=2, u=2)
                     else:
                         source = square[step][:].rearrange("p (e n u) -> p n u e", e=2, u=2)[:, begin:end, :, :]
                     nc.scalar.activation(
@@ -481,12 +476,14 @@ def tile_kan1_pb_kernel(tc, h_mix, x, fc2_spline_w, fc2_base_w, fc2_base_b, out)
                 )
 
         def squares_ahead(step):
-            for later in TENSOR_STEPS:
-                if start_of(later) == step:
-                    squares_on_tensor(later)
+            for block in range(2):
+                if (step + 2, block) in tensor_blocks:
+                    squares_on_tensor(step + 2, block)
 
-        for step in TENSOR_STEPS[:2]:
-            squares_on_tensor(step)
+        for step in range(2):
+            for block in range(2):
+                if (step, block) in tensor_blocks:
+                    squares_on_tensor(step, block)
         turn_weights(0)
         base_cols = slice(SPLINE_PASSES * ROW_TILES * P, PASSES * ROW_TILES * P)
         nc.vector.quantize_mx(

@@ -47,7 +47,7 @@ QUANTISE_FIRST = 20
 FIRST_VECTOR_STEPS = (1, 3, 6)
 EARLY_BLOCKS = 4
 AHEAD = 2
-SCALAR_COLS = (384, 320)
+SCALAR_COLS = (448, 320)
 PASSES_A_STEP = 3
 BASIS_BUFS = 4
 SQUARE_BUFS = AHEAD + 1
@@ -547,9 +547,8 @@ def tile_kan1_pb_kernel(tc, h_mix, x, fc2_spline_w, fc2_base_w, fc2_base_b, out)
         quantise(STEPS - 1, 0, HALF)
         for group in last_groups[:2]:
             multiply(STEPS - 1, group)
-        finish(CHUNKS - 1, last_groups[0])
         quantise(STEPS - 1, HALF, CHUNK)
         for group in last_groups[2:]:
             multiply(STEPS - 1, group)
-        for group in last_groups[1:]:
+        for group in last_groups:
             finish(CHUNKS - 1, group)

@@ -47,11 +47,13 @@ QUANTISE_FIRST = 20
 FIRST_VECTOR_STEPS = (1, 3, 6)
 EARLY_BLOCKS = 4
 AHEAD = 2
-SCALAR_COLS = (448, 320)
-PASSES_A_STEP = 3
+SCALAR_COLS = (448, 352)
+PASSES_A_STEP = 4
 BASIS_BUFS = 4
 SQUARE_BUFS = AHEAD + 1
-CODE_BUFS = 9
+JOB_PLACES = (0, 1, 2, 3, 4, 5, 6, 8)
+LENT = 0
+CODE_BUFS = 10
 SHIFT_AFTER = 3
 FINISH_AFTER = (1, 0)
 
@@ -119,31 +121,32 @@ def tile_kan1_pb_kernel(tc, h_mix, x, fc2_spline_w, fc2_base_w, fc2_base_b, out)
                     )
             w_nat.append(w_tile)
 
-        ident_f32 = keep.tile([P, P], F32)
-        make_identity(nc, ident_f32[:])
-        ident_bf16 = keep.tile([P, P], BF16)
-        make_identity(nc, ident_bf16[:])
-
         warm_in = keep.tile([P, 1], F32)
         nc.vector.memset(warm_in[:], 0.0)
         warm_out = keep.tile([P, 1], F32)
         nc.scalar.activation(out=warm_out[:], in_=warm_in[:], func=ACT.Silu)
 
-        slopes = {}
         levels = {}
+        for pi in range(PAIRS):
+            levels[pi] = keep.tile([P, 2 * TENSOR_COLS], BF16, name="level%d" % pi)
+            nc.vector.memset(levels[pi][:], (units(pi, 1) ** 2 - units(pi, 0) ** 2) / TENSOR_UNIT)
+        ident_f32 = keep.tile([P, P], F32)
+        make_identity(nc, ident_f32[:])
+        ident_bf16 = keep.tile([P, P], BF16)
+        nc.vector.tensor_copy(out=ident_bf16[:], in_=ident_f32[:])
+
+        slopes = {}
         for pi in range(PAIRS):
             for e in range(2):
                 slopes[pi, e] = keep.tile([P, P], BF16, name="slope%d_%d" % (pi, e))
-                nc.gpsimd.tensor_scalar(
+                nc.vector.tensor_scalar(
                     out=slopes[pi, e][:],
-                    in0=ident_bf16[:],
+                    in0=ident_f32[:],
                     scalar1=-2.0 * units(pi, e) / (SPACING * TENSOR_UNIT),
                     scalar2=0.0,
                     op0=ALU.mult,
                     op1=ALU.add,
                 )
-            levels[pi] = keep.tile([P, 2 * TENSOR_COLS], BF16, name="level%d" % pi)
-            nc.gpsimd.memset(levels[pi][:], (units(pi, 1) ** 2 - units(pi, 0) ** 2) / TENSOR_UNIT)
 
         def turn(b, groups):
             bank = psum_bank(b)
@@ -246,18 +249,18 @@ def tile_kan1_pb_kernel(tc, h_mix, x, fc2_spline_w, fc2_base_w, fc2_base_b, out)
 
         tensor_square = {}
 
-        def squares_on_tensor(step, block):
+        def squares_on_tensor(step, block, place):
             ch, k_pass = divmod(step, SPLINE_PASSES)
             half, pi = divmod(k_pass, PAIRS)
             cols = 2 * TENSOR_COLS
-            bank = psum_bank(SQUARE_BANKS[block][step % 2])
+            bank = psum_bank(SQUARE_BANKS[block][place % 2])
             tensor_square[step, block] = bank
             for e in range(2):
                 for u in range(2):
-                    place = (2 * half + u) * P
+                    col = (2 * half + u) * P
                     nc.tensor.matmul(
                         bank[:, (2 * e + u) * P : (2 * e + u + 1) * P],
-                        lhsT=plain_square[ch, block][:, place : place + P],
+                        lhsT=plain_square[ch, block][:, col : col + P],
                         rhs=ident_f32[:],
                         is_transpose=True,
                         start=(e == 0 and u == 0),
@@ -386,8 +389,6 @@ def tile_kan1_pb_kernel(tc, h_mix, x, fc2_spline_w, fc2_base_w, fc2_base_b, out)
             w_grouped[job] = ring.tile([P, PAIRS * PACK * P], BF16, align_bytes=64, tag="grouped", name="w_grouped")
             for place, bank in enumerate(w_banks[job]):
                 regroup(w_grouped[job], place * CHUNK, bank)
-            if job + 1 < JOBS:
-                turn_weights(job + 1)
 
         def quantise_weights(job):
             job_cols = slice(job * PAIRS * P, (job + 1) * PAIRS * P)
@@ -475,71 +476,86 @@ def tile_kan1_pb_kernel(tc, h_mix, x, fc2_spline_w, fc2_base_w, fc2_base_b, out)
                     in_=result[:, c : c + STORE_COLS],
                 )
 
-        def squares_ahead(step):
-            for block in range(2):
-                if (step + 2, block) in tensor_blocks:
-                    squares_on_tensor(step + 2, block)
+        order = list(range(PAIRS)) + list(range(SPLINE_PASSES, SPLINE_PASSES + LENT)) + list(range(PAIRS, SPLINE_PASSES))
+        order += list(range(SPLINE_PASSES + LENT, STEPS))
+        first_done = max(order.index(SPLINE_PASSES - 1), JOB_PLACES[JOBS - 1]) + 1
 
-        for step in range(2):
+        for place in range(2):
             for block in range(2):
-                if (step, block) in tensor_blocks:
-                    squares_on_tensor(step, block)
+                if (order[place], block) in tensor_blocks:
+                    squares_on_tensor(order[place], block, place)
         turn_weights(0)
         base_cols = slice(SPLINE_PASSES * ROW_TILES * P, PASSES * ROW_TILES * P)
         nc.vector.quantize_mx(
             out=w_codes[:, base_cols].bitcast(FP8X4), scales=w_scales[:, base_cols], in_=bw_grouped[:]
         )
-        for step in range(1, AHEAD):
-            squares(step)
+        for place in range(1, AHEAD):
+            squares(order[place])
         waiting = []
-        for step in range(SPLINE_PASSES):
+        first_steps = []
+        ready = []
+        quantised = {ch: [] for ch in range(CHUNKS)}
+        done = {}
+
+        def passes(ch, some):
+            for group in some:
+                for step in quantised[ch][done.get((ch, group), 0) :]:
+                    multiply(step, group)
+                done[ch, group] = len(quantised[ch])
+
+        for place, step in enumerate(order[:-1]):
+            ch = step // SPLINE_PASSES
             exponentials(step)
-            squares_ahead(step)
-            pack_weights(step)
-            squares(step + AHEAD)
-            quantise(step)
-            quantise_weights(step)
-            if step == SHIFT_AFTER:
-                shift(1)
-            half, done = divmod(step, ROW_TILES)
-            for late, m in waiting[:PASSES_A_STEP]:
-                multiply(late, groups[0][m])
-            waiting = waiting[PASSES_A_STEP:]
-            waiting += [(step, m) for m in range(done)] + [(late, done) for late in range(half * PAIRS, step + 1)]
-
-
-        def passes(step):
-            ch, k_pass = divmod(step, SPLINE_PASSES)
-            opened = FINISH_AFTER[ch - 1]
-            for group in groups[ch][:2]:
-                multiply(step, group)
-            if k_pass >= opened:
-                for group in groups[ch][2:]:
-                    for late in range(step - k_pass if k_pass == opened else step, step + 1):
-                        multiply(late, group)
-
-        for step in range(SPLINE_PASSES, STEPS - 1):
-            ch, k_pass = divmod(step, SPLINE_PASSES)
-            exponentials(step)
-            squares_ahead(step)
-            for late, m in waiting:
-                multiply(late, groups[0][m])
-            waiting = []
-            shift_now = k_pass == SHIFT_AFTER and ch + 1 < CHUNKS
-            if step >= QUANTISE_FIRST:
+            if place + 2 < STEPS:
+                for block in range(2):
+                    if (order[place + 2], block) in tensor_blocks:
+                        squares_on_tensor(order[place + 2], block, place + 2)
+            if place == first_done:
+                for late, m in waiting:
+                    multiply(late, groups[0][m])
+            job = JOB_PLACES.index(place) if place in JOB_PLACES else None
+            if job is not None:
+                pack_weights(job)
+            if place + 1 in JOB_PLACES:
+                turn_weights(JOB_PLACES.index(place + 1))
+            if place >= QUANTISE_FIRST:
                 quantise(step)
-            if step + AHEAD < STEPS:
-                squares(step + AHEAD)
-            if step < QUANTISE_FIRST:
+            if place + AHEAD < STEPS:
+                squares(order[place + AHEAD])
+            if place < QUANTISE_FIRST:
                 quantise(step)
-            if shift_now:
-                shift(ch + 1)
-            if step > SPLINE_PASSES:
-                passes(step - 1)
-            if k_pass == FINISH_AFTER[ch - 1]:
-                for group in groups[ch - 1]:
-                    finish(ch - 1, group)
-        passes(STEPS - 2)
+            if job is not None:
+                quantise_weights(job)
+            if place + AHEAD + 1 < STEPS and order[place + AHEAD + 1] % SPLINE_PASSES == 0:
+                shift(order[place + AHEAD + 1] // SPLINE_PASSES)
+            if place < first_done:
+                for late, m in waiting[:PASSES_A_STEP]:
+                    multiply(late, groups[0][m])
+                waiting = waiting[PASSES_A_STEP:]
+                if ch == 0:
+                    waiting += [(step, m) for m in range(ROW_TILES) if step // PAIRS * ROW_TILES + m in ready]
+                    first_steps.append(step)
+                if job is not None:
+                    half, m = divmod(job, ROW_TILES)
+                    waiting += [(late, m) for late in first_steps if late // PAIRS == half]
+                    ready.append(job)
+            elif place > first_done:
+                for each in range(1, CHUNKS):
+                    if place > SPLINE_PASSES * (each + 1):
+                        continue
+                    opened = first_done + 1 if each == 1 else SPLINE_PASSES * each + 1
+                    if place >= opened:
+                        passes(each, groups[each][:2])
+                    if place >= opened + (1 if each == 1 else 0):
+                        passes(each, groups[each][2:])
+            if place == first_done + 1:
+                for group in groups[0]:
+                    finish(0, group)
+            if place == 2 * SPLINE_PASSES:
+                for group in groups[1]:
+                    finish(1, group)
+            quantised[ch].append(step)
+        passes(CHUNKS - 1, groups[CHUNKS - 1])
 
         exponentials(STEPS - 1, 0, HALF)
         exponentials(STEPS - 1, HALF, CHUNK)

@@ -44,10 +44,10 @@ W_JOB = HIDDEN * CENTRES // HALVES
 SORTED_BY_LOAD = 3
 JOBS = HALVES * ROW_TILES
 QUANTISE_FIRST = 20
-FIRST_VECTOR_STEPS = (1, 3, 6)
+FIRST_VECTOR_STEPS = (1, 4, 6)
 EARLY_BLOCKS = 4
 AHEAD = 2
-SCALAR_COLS = (448, 352)
+SCALAR_COLS = (480, 352)
 PASSES_A_STEP = 4
 BASIS_BUFS = 4
 SQUARE_BUFS = AHEAD + 1
@@ -461,15 +461,24 @@ def tile_kan1_pb_kernel(tc, h_mix, x, fc2_spline_w, fc2_base_w, fc2_base_b, out)
         def finish(ch, group):
             m, first, last = group
             result = ring.tile([P, CHUNK], F32, name="result", bufs=RESULT_BUFS)
-            nc.vector.scalar_tensor_tensor(
-                out=result[:, first:last],
-                in0=acc[ch, group],
-                scalar=bias_sb[:, m : m + 1],
-                in1=x_sb[:, m * COLS + ch * CHUNK + first : m * COLS + ch * CHUNK + last],
-                op0=ALU.add,
-                op1=ALU.add,
-            )
-            for c in range(first, last, STORE_COLS):
+            add_cols = STORE_COLS if ch == CHUNKS - 1 else last - first
+            for c in range(first, last, add_cols):
+                n0 = m * COLS + ch * CHUNK + c
+                nc.vector.scalar_tensor_tensor(
+                    out=result[:, c : c + add_cols],
+                    in0=acc[ch, group][:, c - first : c - first + add_cols],
+                    scalar=bias_sb[:, m : m + 1],
+                    in1=x_sb[:, n0 : n0 + add_cols],
+                    op0=ALU.add,
+                    op1=ALU.add,
+                )
+                if add_cols == STORE_COLS:
+                    b, c0 = divmod(ch * CHUNK + c, CHANNELS)
+                    nc.sync.dma_start(
+                        out=out[b, m * P : (m + 1) * P, c0 : c0 + STORE_COLS],
+                        in_=result[:, c : c + STORE_COLS],
+                    )
+            for c in range(first, last, STORE_COLS) if add_cols != STORE_COLS else ():
                 b, c0 = divmod(ch * CHUNK + c, CHANNELS)
                 nc.sync.dma_start(
                     out=out[b, m * P : (m + 1) * P, c0 : c0 + STORE_COLS],

import math
from contextlib import ExitStack

import concourse.mybir as mybir
from concourse.masks import make_identity

F32 = mybir.dt.float32
BF16 = mybir.dt.bfloat16
U32 = mybir.dt.uint32
U8 = mybir.dt.uint8
FP8X4 = mybir.dt.float8_e4m3fn_x4
ACT = mybir.ActivationFunctionType
ALU = mybir.AluOpType

P = 128
PACK = 4
BATCH, CHANNELS, HIDDEN, ROWS, CENTRES = 2, 768, 512, 512, 8
COLS = BATCH * CHANNELS
CHUNK = 512
CHUNKS = COLS // CHUNK
HALF = CHUNK // 2
RESULT_BUFS = 6
STORE_COLS = 256
ROW_TILES = ROWS // P
SPACING = 2.0 / (CENTRES - 1)
PAIRS = CENTRES // 2
HALVES = 2
SPLINE_PASSES = HALVES * PAIRS
BASE_PASS = SPLINE_PASSES
PASSES = SPLINE_PASSES + 1
STEPS = CHUNKS * SPLINE_PASSES
PER_CENTRE = CHUNK * PACK // 2
WORD_GROUPS = 8
SLAB_TILES = (1, 1, 2, 2, 2, 2, 2)
SQUARE_BANKS = ((6, 7), (2, 3))
SUM_BANKS = 6
TENSOR_COLS = CHUNK // 4
TENSOR_UNIT = 64.0
HEAD_BANKS = 6
WEIGHT_BANKS = 4
EARLY_COPIES_AFTER = 4
EARLY_SLABS = 1
W_JOB = HIDDEN * CENTRES // HALVES
SORTED_BY_LOAD = 3
JOBS = HALVES * ROW_TILES
QUANTISE_FIRST = 20
FIRST_VECTOR_STEPS = (1, 4, 6)
EARLY_BLOCKS = 4
AHEAD = 2
SCALAR_COLS = (480, 352)
PASSES_A_STEP = 4
BASIS_BUFS = 4
SQUARE_BUFS = AHEAD + 1
JOB_PLACES = (0, 1, 2, 3, 4, 5, 6, 8)
LENT = 0
CODE_BUFS = 10
SHIFT_AFTER = 3
FINISH_AFTER = (1, 0)

assert JOBS == SPLINE_PASSES
assert SHIFT_AFTER < SPLINE_PASSES - AHEAD

FLOPS = 2 * COLS * ROWS * (HIDDEN * CENTRES + HIDDEN)


def units(pi, e):
    return 2.0 * pi + e - (CENTRES - 1) / 2.0


def unit_order(words):
    return words.rearrange("row (g a c r) -> row g c a r", a=16, c=4, r=2)


def partition_order(words):
    return words.rearrange("row (g c a r) -> row g c a r", c=4, a=16, r=2)


def tile_kan1_pb_kernel(tc, h_mix, x, fc2_spline_w, fc2_base_w, fc2_base_b, out):
    nc = tc.nc
    with ExitStack() as stack:
        stack.enter_context(tc.manual_schedule())
        keep = stack.enter_context(tc.tile_pool(name="keep", bufs=1))
        ring = stack.enter_context(tc.tile_pool(name="ring", bufs=3))
        psum = stack.enter_context(tc.psum_pool(name="psum", bufs=1))

        def psum_bank(b, dtype=F32, cols=CHUNK):
            return psum.tile([P, cols], dtype, tag="bank%d" % b, name="bank")

        bias_rows = keep.tile([P, P], BF16)
        nc.vector.memset(bias_rows[:], 0.0)
        h_rows = h_mix.flatten_outer_dims()
        h_nat = []
        slab_cols = []
        for slab, tiles in enumerate(SLAB_TILES):
            n0 = sum(SLAB_TILES[:slab]) * P
            slab_cols.append((n0, n0 + tiles * P))
            h_tile = keep.tile([P, tiles * HIDDEN], BF16, name="h_nat%d" % slab)
            nc.sync.dma_start(
                out=h_tile[:].rearrange("row (t j) -> row t j", t=tiles),
                in_=h_rows[n0 : n0 + tiles * P, :].rearrange("(t row) j -> row t j", row=P),
            )
            h_nat.append(h_tile)
        nc.sync.dma_start(out=bias_rows[0:ROW_TILES, :], in_=fc2_base_b.rearrange("(m q) -> m q", q=P))
        bw_nat = keep.tile([P, ROW_TILES * HIDDEN], BF16)
        nc.sync.dma_start(
            out=bw_nat[:].rearrange("q (m j) -> q m j", m=ROW_TILES),
            in_=fc2_base_w.rearrange("(m q) j -> q m j", q=P),
        )
        w_nat = []
        for job in range(JOBS):
            half, m = divmod(job, ROW_TILES)
            w_tile = keep.tile([P, W_JOB], BF16, name="w_nat%d" % job)
            w_rows = fc2_spline_w[m * P : (m + 1) * P, half * W_JOB : (half + 1) * W_JOB]
            if job < SORTED_BY_LOAD:
                nc.sync.dma_start(out=w_tile[:], in_=w_rows)
            else:
                for c in range(4):
                    nc.sync.dma_start(
                        out=w_tile[:].rearrange("q (c a s) -> q c a s", c=4, s=32)[:, c, :, :],
                        in_=w_rows.rearrange("q (a c s) -> q c a s", c=4, s=32)[:, c, :, :],
                    )
            w_nat.append(w_tile)

        warm_in = keep.tile([P, 1], F32)
        nc.vector.memset(warm_in[:], 0.0)
        warm_out = keep.tile([P, 1], F32)
        nc.scalar.activation(out=warm_out[:], in_=warm_in[:], func=ACT.Silu)

        levels = {}
        for pi in range(PAIRS):
            levels[pi] = keep.tile([P, 2 * TENSOR_COLS], BF16, name="level%d" % pi)
            nc.vector.memset(levels[pi][:], (units(pi, 1) ** 2 - units(pi, 0) ** 2) / TENSOR_UNIT)
        ident_f32 = keep.tile([P, P], F32)
        make_identity(nc, ident_f32[:])
        ident_bf16 = keep.tile([P, P], BF16)
        nc.vector.tensor_copy(out=ident_bf16[:], in_=ident_f32[:])

        slopes = {}
        for pi in range(PAIRS):
            for e in range(2):
                slopes[pi, e] = keep.tile([P, P], BF16, name="slope%d_%d" % (pi, e))
                nc.vector.tensor_scalar(
                    out=slopes[pi, e][:],
                    in0=ident_f32[:],
                    scalar1=-2.0 * units(pi, e) / (SPACING * TENSOR_UNIT),
                    scalar2=0.0,
                    op0=ALU.mult,
                    op1=ALU.add,
                )

        def turn(b, groups):
            bank = psum_bank(b)
            for place, group in enumerate(groups):
                nc.tensor.transpose(bank[:, place * P : (place + 1) * P], group, ident_f32[:])
            return bank

        def group(words, g):
            return words[:, g * P : (g + 1) * P]

        tensor_blocks = [(step, 0) for step in range(STEPS)] + [(step, 1) for step in range(EARLY_BLOCKS)]
        h_perm = {}
        hidden = []
        silu_grouped = keep.tile([P, PACK * COLS], BF16, align_bytes=64, tag="silu_then_x", name="silu_grouped")

        def permute_hidden(slab):
            words = SLAB_TILES[slab] * HALVES * P
            h_perm[slab] = ring.tile([P, words], F32, name="h_perm", bufs=3)
            nc.vector.tensor_copy(out=partition_order(h_perm[slab][:]), in_=unit_order(h_nat[slab][:].bitcast(F32)))

        plain_square = {}

        def square_plainly(slab):
            ch, block = divmod(slab_cols[slab][0] // P, CHUNK // P)
            halves = sum((ch * SPLINE_PASSES + half * PAIRS, block) in tensor_blocks for half in range(HALVES))
            if halves:
                plain_square[ch, block] = keep.tile([P, halves * 2 * P], F32, name="plain_square%d_%d" % (ch, block))
                nc.scalar.activation(
                    out=plain_square[ch, block][:].rearrange("n (h u p) -> n h u p", h=halves, u=2),
                    in_=h_perm[slab][:, 0 : halves * P].bitcast(BF16).rearrange("n (h p u) -> n h u p", h=halves, u=2),
                    func=ACT.Square,
                    scale=1.0 / (SPACING * math.sqrt(TENSOR_UNIT)),
                )

        h_banks = {}

        def turn_hidden(slab):
            tiles = SLAB_TILES[slab]
            h_banks[slab] = turn(slab % HEAD_BANKS, [group(h_perm[slab], 2 * t + half) for half in range(HALVES) for t in range(tiles)])

        def place(slab):
            n0, n1 = slab_cols[slab]
            ch = n0 // CHUNK
            if n0 % CHUNK == 0:
                hidden.append(keep.tile([P, PACK * CHUNK], BF16, name="hidden%d" % ch))
            return ch, slice(n0 - ch * CHUNK, n1 - ch * CHUNK)

        def copy_hidden(slab, ch, n_cols):
            words = SLAB_TILES[slab] * HALVES * P
            nc.vector.tensor_copy(
                out=hidden[ch][:].bitcast(F32).rearrange("p (h n) -> p h n", h=HALVES)[:, :, n_cols],
                in_=h_banks[slab][:, :words].rearrange("p (h n) -> p h n", h=HALVES),
            )

        def n_h_u(values):
            return values.rearrange("p (h n u) -> p n h u", h=HALVES, u=2)

        def silu(ch, n_cols, source):
            nc.scalar.activation(
                out=silu_grouped[:, ch * PACK * CHUNK : (ch + 1) * PACK * CHUNK].rearrange(
                    "p (n h u) -> p n h u", h=HALVES, u=2
                )[:, n_cols, :, :],
                in_=source,
                func=ACT.Silu,
            )

        shifted = {}

        def shift(ch):
            shifted[ch] = ring.tile([P, PACK * CHUNK], F32, name="shifted", bufs=2)
            some = [t[:].rearrange("p (h v) -> p h v", h=HALVES)[:, :, 2 * TENSOR_COLS :] for t in (shifted[ch], hidden[ch])]
            nc.vector.tensor_scalar_add(out=some[0], in0=some[1], scalar1=-SPACING)

        for slab in range(EARLY_SLABS + 1):
            permute_hidden(slab)
        places = []
        for slab in range(EARLY_SLABS):
            turn_hidden(slab)
            square_plainly(slab)
            places.append(place(slab))
            words = SLAB_TILES[slab] * HALVES * P
            silu(*places[slab], n_h_u(h_banks[slab][:, :words].bitcast(BF16)))
        for slab in range(EARLY_SLABS, len(SLAB_TILES)):
            if slab + 1 < len(SLAB_TILES):
                permute_hidden(slab + 1)
            turn_hidden(slab)
            square_plainly(slab)
            ch, n_cols = place(slab)
            copy_hidden(slab, ch, n_cols)
            silu(ch, n_cols, n_h_u(hidden[ch][:])[:, n_cols, :, :])
            if slab == EARLY_COPIES_AFTER:
                for early in range(EARLY_SLABS):
                    copy_hidden(early, *places[early])

        square = {}
        basis = {}
        codes = {}
        scales = {}
        acc = {}

        tensor_square = {}

        def squares_on_tensor(step, block, place):
            ch, k_pass = divmod(step, SPLINE_PASSES)
            half, pi = divmod(k_pass, PAIRS)
            cols = 2 * TENSOR_COLS
            bank = psum_bank(SQUARE_BANKS[block][place % 2])
            tensor_square[step, block] = bank
            for e in range(2):
                for u in range(2):
                    col = (2 * half + u) * P
                    nc.tensor.matmul(
                        bank[:, (2 * e + u) * P : (2 * e + u + 1) * P],
                        lhsT=plain_square[ch, block][:, col : col + P],
                        rhs=ident_f32[:],
                        is_transpose=True,
                        start=(e == 0 and u == 0),
                        stop=False,
                    )
            for e in range(2):
                nc.tensor.matmul(
                    bank[:, e * cols : (e + 1) * cols].rearrange("p (u n) -> p u n", u=2),
                    lhsT=slopes[pi, e][:],
                    rhs=hidden[ch][:, half * PER_CENTRE + block * cols : half * PER_CENTRE + (block + 1) * cols].rearrange("p (n u) -> p u n", u=2),
                    start=False,
                    stop=False,
                )
            nc.tensor.matmul(bank[:, cols : 2 * cols], lhsT=ident_bf16[:], rhs=levels[pi][:], start=False, stop=True)

        def shares(step):
            tensor_end = TENSOR_COLS * sum((step, block) in tensor_blocks for block in range(2))
            if step < SPLINE_PASSES:
                scalar_end = tensor_end if step in FIRST_VECTOR_STEPS else CHUNK
            else:
                scalar_end = TENSOR_COLS if step % PAIRS else SCALAR_COLS[step // SPLINE_PASSES - 1]
            return {"tensor": (0, tensor_end), "scalar": (tensor_end, scalar_end), "vector": (scalar_end, CHUNK)}

        def first_centre(step):
            return -1.0 + 2 * (step % PAIRS) * SPACING

        def squares(step):
            ch, k_pass = divmod(step, SPLINE_PASSES)
            centre = first_centre(step)
            square[step] = ring.tile([P, PACK * CHUNK], F32, name="square", bufs=SQUARE_BUFS)
            v_of_e = square[step][:].rearrange("p (e v) -> p e v", e=2)
            v_of_half = k_pass // PAIRS * PER_CENTRE
            first, last = shares(step)["scalar"]
            if first < last:
                for e in range(2):
                    nc.scalar.activation(
                        out=v_of_e[:, e, 2 * first : 2 * last],
                        in_=hidden[ch][:, v_of_half + 2 * first : v_of_half + 2 * last],
                        func=ACT.Square,
                        bias=-(centre + e * SPACING),
                        scale=1.0,
                    )
            first, last = shares(step)["vector"]
            if first < last:
                for e, source in enumerate((hidden[ch], shifted[ch])):
                    s = source[:, v_of_half + 2 * first : v_of_half + 2 * last]
                    nc.vector.scalar_tensor_tensor(
                        out=v_of_e[:, e, 2 * first : 2 * last],
                        in0=s,
                        scalar=2.0 * centre,
                        in1=s,
                        op0=ALU.subtract,
                        op1=ALU.mult,
                    )

        bias_turned = psum_bank(len(SLAB_TILES) % HEAD_BANKS, BF16, P)
        nc.tensor.transpose(bias_turned[:], bias_rows[:], ident_bf16[:])
        bias_sb = keep.tile([P, ROW_TILES], F32)
        nc.vector.tensor_copy(out=bias_sb[:], in_=bias_turned[:, 0:ROW_TILES])

        w_codes = keep.tile([P, ROW_TILES * PASSES * P], U32, align_bytes=64)
        w_scales = keep.tile([P, ROW_TILES * PASSES * P], U8, align_bytes=64)

        def w_cols(k_pass, m):
            half, pi = divmod(k_pass, PAIRS)
            place = SPLINE_PASSES * ROW_TILES + m if k_pass == BASE_PASS else (half * ROW_TILES + m) * PAIRS + pi
            return slice(place * P, (place + 1) * P)

        def regroup(grouped, first_word, bank):
            nc.vector.tensor_copy(
                out=grouped[:]
                .bitcast(F32)[:, first_word : first_word + CHUNK]
                .rearrange("p (a q s) -> p a q s", a=2, s=2),
                in_=bank[:].rearrange("p (a s q) -> p a q s", a=2, s=2),
            )

        bw_perm = keep.tile([P, WORD_GROUPS * P], F32)
        nc.vector.tensor_copy(out=partition_order(bw_perm[:]), in_=unit_order(bw_nat[:].bitcast(F32)))
        shift(0)
        bw_banks = [
            turn(WEIGHT_BANKS + m_pair, [group(bw_perm, g) for g in range(4 * m_pair, 4 * m_pair + 4)])
            for m_pair in range(2)
        ]
        squares(0)
        silu_codes = keep.tile([P, COLS], U32, align_bytes=64)
        silu_scales = keep.tile([P, COLS], U8, align_bytes=64)
        for n0, n1 in ((0, 2 * CHUNK), (2 * CHUNK, COLS)):
            nc.vector.quantize_mx(
                out=silu_codes[:, n0:n1].bitcast(FP8X4),
                scales=silu_scales[:, n0:n1],
                in_=silu_grouped[:, PACK * n0 : PACK * n1],
            )
        x_sb = keep.tile([P, ROW_TILES * COLS], BF16, align_bytes=64, tag="silu_then_x", name="x_sb")
        for m in range(ROW_TILES):
            nc.sync.dma_start(
                out=x_sb[:, m * COLS : (m + 1) * COLS].rearrange("q (b c) -> q b c", b=BATCH),
                in_=x[:, m * P : (m + 1) * P, :].rearrange("b q c -> q b c"),
            )
        bw_grouped = ring.tile([P, ROW_TILES * PACK * P], BF16, align_bytes=64, tag="grouped")
        for m_pair in range(2):
            regroup(bw_grouped, m_pair * CHUNK, bw_banks[m_pair])


        w_banks = {}
        w_grouped = {}

        def turn_weights(job):
            if job < SORTED_BY_LOAD:
                w_sorted = ring.tile([P, W_JOB], BF16, tag="perm", bufs=2)
                nc.vector.tensor_copy(
                    out=w_sorted[:].bitcast(F32).rearrange("q (c a s) -> q c a s", c=4, s=16),
                    in_=w_nat[job][:].bitcast(F32).rearrange("q (a c s) -> q c a s", c=4, s=16),
                )
            else:
                w_sorted = w_nat[job]
            words = w_sorted[:].bitcast(F32)
            w_banks[job] = [
                turn(
                    WEIGHT_BANKS + pi0 // 2,
                    [words[:, 4 * u + pi0 + a : WORD_GROUPS * P : WORD_GROUPS] for a in range(2) for u in range(2)],
                )
                for pi0 in range(0, PAIRS, 2)
            ]

        def pack_weights(job):
            w_grouped[job] = ring.tile([P, PAIRS * PACK * P], BF16, align_bytes=64, tag="grouped", name="w_grouped")
            for place, bank in enumerate(w_banks[job]):
                regroup(w_grouped[job], place * CHUNK, bank)

        def quantise_weights(job):
            job_cols = slice(job * PAIRS * P, (job + 1) * PAIRS * P)
            nc.vector.quantize_mx(
                out=w_codes[:, job_cols].bitcast(FP8X4), scales=w_scales[:, job_cols], in_=w_grouped[job][:]
            )

        def rest(step, engine):
            if engine == "scalar":
                return 0.0
            return units(step % PAIRS, 0) ** 2

        def exponentials(step, first=0, last=CHUNK):
            if first == 0:
                basis[step] = ring.tile([P, PACK * CHUNK], BF16, align_bytes=64, name="basis", bufs=BASIS_BUFS)
                codes[step] = ring.tile([P, CHUNK], U32, align_bytes=64, name="codes", bufs=CODE_BUFS)
                scales[step] = ring.tile([P, CHUNK], U8, align_bytes=64, name="scales", bufs=CODE_BUFS)
            pieces = []
            for engine, (begin, end) in shares(step).items():
                size = TENSOR_COLS if engine == "tensor" else CHUNK
                pieces += [(engine, c, min(c + size, end)) for c in range(begin, end, size)]
            for engine, begin, end in pieces:
                begin, end = max(begin, first), min(end, last)
                if begin < end:
                    if engine == "tensor":
                        source = tensor_square[step, begin // TENSOR_COLS][:].rearrange("p (e u n) -> p n u e", e=2, u=2)
                    else:
                        source = square[step][:].rearrange("p (e n u) -> p n u e", e=2, u=2)[:, begin:end, :, :]
                    nc.scalar.activation(
                        out=basis[step][:].rearrange("p (n u e) -> p n u e", u=2, e=2)[:, begin:end, :, :],
                        in_=source,
                        func=ACT.Exp,
                        bias=-rest(step, engine),
                        scale=-TENSOR_UNIT if engine == "tensor" else -1.0 / (SPACING * SPACING),
                    )

        def quantise(step, first=0, last=CHUNK):
            nc.vector.quantize_mx(
                out=codes[step][:, first:last].bitcast(FP8X4),
                scales=scales[step][:, first:last],
                in_=basis[step][:, PACK * first : PACK * last],
            )

        groups = {ch: [(m, 0, CHUNK) for m in range(ROW_TILES)] for ch in range(CHUNKS - 1)}
        groups[CHUNKS - 1] = [(m, first, first + HALF) for first in (0, HALF) for m in range(2)]
        groups[CHUNKS - 1] += [(m, 0, CHUNK) for m in range(2, ROW_TILES)]

        def one_pass(ch, group, k_pass, rhs, rhs_scale):
            m = group[0]
            nc.tensor.matmul_mx(
                out=acc[ch, group],
                lhsT=w_codes[:, w_cols(k_pass, m)].bitcast(FP8X4),
                lhsT_scale=w_scales[:, w_cols(k_pass, m)],
                rhs=rhs.bitcast(FP8X4),
                rhs_scale=rhs_scale,
                start=(k_pass == BASE_PASS),
                stop=(k_pass == SPLINE_PASSES - 1),
            )

        def multiply(step, group):
            ch, k_pass = divmod(step, SPLINE_PASSES)
            m, first, last = group
            if k_pass == 0:
                b = (ROW_TILES * ch + groups[ch].index(group)) % SUM_BANKS
                acc[ch, group] = psum_bank(b, F32, last - first)[:]
                n_cols = slice(ch * CHUNK + first, ch * CHUNK + last)
                one_pass(ch, group, BASE_PASS, silu_codes[:, n_cols], silu_scales[:, n_cols])
            one_pass(ch, group, k_pass, codes[step][:, first:last], scales[step][:, first:last])

        def finish(ch, group):
            m, first, last = group
            result = ring.tile([P, CHUNK], F32, name="result", bufs=RESULT_BUFS)
            add_cols = STORE_COLS if ch == CHUNKS - 1 else last - first
            for c in range(first, last, add_cols):
                n0 = m * COLS + ch * CHUNK + c
                nc.vector.scalar_tensor_tensor(
                    out=result[:, c : c + add_cols],
                    in0=acc[ch, group][:, c - first : c - first + add_cols],
                    scalar=bias_sb[:, m : m + 1],
                    in1=x_sb[:, n0 : n0 + add_cols],
                    op0=ALU.add,
                    op1=ALU.add,
                )
                if add_cols == STORE_COLS:
                    b, c0 = divmod(ch * CHUNK + c, CHANNELS)
                    nc.sync.dma_start(
                        out=out[b, m * P : (m + 1) * P, c0 : c0 + STORE_COLS],
                        in_=result[:, c : c + STORE_COLS],
                    )
            for c in range(first, last, STORE_COLS) if add_cols != STORE_COLS else ():
                b, c0 = divmod(ch * CHUNK + c, CHANNELS)
                nc.sync.dma_start(
                    out=out[b, m * P : (m + 1) * P, c0 : c0 + STORE_COLS],
                    in_=result[:, c : c + STORE_COLS],
                )

        order = list(range(PAIRS)) + list(range(SPLINE_PASSES, SPLINE_PASSES + LENT)) + list(range(PAIRS, SPLINE_PASSES))
        order += list(range(SPLINE_PASSES + LENT, STEPS))
        first_done = max(order.index(SPLINE_PASSES - 1), JOB_PLACES[JOBS - 1]) + 1

        for place in range(2):
            for block in range(2):
                if (order[place], block) in tensor_blocks:
                    squares_on_tensor(order[place], block, place)
        turn_weights(0)
        base_cols = slice(SPLINE_PASSES * ROW_TILES * P, PASSES * ROW_TILES * P)
        nc.vector.quantize_mx(
            out=w_codes[:, base_cols].bitcast(FP8X4), scales=w_scales[:, base_cols], in_=bw_grouped[:]
        )
        for place in range(1, AHEAD):
            squares(order[place])
        waiting = []
        first_steps = []
        ready = []
        quantised = {ch: [] for ch in range(CHUNKS)}
        done = {}

        def passes(ch, some):
            for group in some:
                for step in quantised[ch][done.get((ch, group), 0) :]:
                    multiply(step, group)
                done[ch, group] = len(quantised[ch])

        for place, step in enumerate(order[:-1]):
            ch = step // SPLINE_PASSES
            exponentials(step)
            if place + 2 < STEPS:
                for block in range(2):
                    if (order[place + 2], block) in tensor_blocks:
                        squares_on_tensor(order[place + 2], block, place + 2)
            if place == first_done:
                for late, m in waiting:
                    multiply(late, groups[0][m])
            job = JOB_PLACES.index(place) if place in JOB_PLACES else None
            if job is not None:
                pack_weights(job)
            if place + 1 in JOB_PLACES:
                turn_weights(JOB_PLACES.index(place + 1))
            if place >= QUANTISE_FIRST:
                quantise(step)
            if place + AHEAD < STEPS:
                squares(order[place + AHEAD])
            if place < QUANTISE_FIRST:
                quantise(step)
            if job is not None:
                quantise_weights(job)
            if place + AHEAD + 1 < STEPS and order[place + AHEAD + 1] % SPLINE_PASSES == 0:
                shift(order[place + AHEAD + 1] // SPLINE_PASSES)
            if place < first_done:
                for late, m in waiting[:PASSES_A_STEP]:
                    multiply(late, groups[0][m])
                waiting = waiting[PASSES_A_STEP:]
                if ch == 0:
                    waiting += [(step, m) for m in range(ROW_TILES) if step // PAIRS * ROW_TILES + m in ready]
                    first_steps.append(step)
                if job is not None:
                    half, m = divmod(job, ROW_TILES)
                    waiting += [(late, m) for late in first_steps if late // PAIRS == half]
                    ready.append(job)
            elif place > first_done:
                for each in range(1, CHUNKS):
                    if place > SPLINE_PASSES * (each + 1):
                        continue
                    opened = first_done + 1 if each == 1 else SPLINE_PASSES * each + 1
                    if place >= opened:
                        passes(each, groups[each][:2])
                    if place >= opened + (1 if each == 1 else 0):
                        passes(each, groups[each][2:])
            if place == first_done + 1:
                for group in groups[0]:
                    finish(0, group)
            if place == 2 * SPLINE_PASSES:
                for group in groups[1]:
                    finish(1, group)
            quantised[ch].append(step)
        passes(CHUNKS - 1, groups[CHUNKS - 1])

        exponentials(STEPS - 1, 0, HALF)
        exponentials(STEPS - 1, HALF, CHUNK)
        last_groups = groups[CHUNKS - 1]
        quantise(STEPS - 1, 0, HALF)
        for group in last_groups[:2]:
            multiply(STEPS - 1, group)
        quantise(STEPS - 1, HALF, CHUNK)
        for group in last_groups[2:]:
            multiply(STEPS - 1, group)
        for group in last_groups:
            finish(CHUNKS - 1, group)
